import numpy as np
import ml_dtypes


def mxq(x, axis, fmt="e4m3"):
    dtype, down = {"e4m3": (ml_dtypes.float8_e4m3fn, 7), "e5m2": (ml_dtypes.float8_e5m2, 14)}[fmt]
    v = np.moveaxis(np.asarray(x, np.float32).astype(ml_dtypes.bfloat16).astype(np.float64), axis, -1)
    blocks = v.reshape(v.shape[:-1] + (-1, 32))
    amax = np.abs(blocks).max(-1, keepdims=True)
    byte = np.maximum(np.where(amax > 0, np.frexp(amax)[1] - 1 + 127, 0) - down, 1)
    scale = np.exp2(byte - 127.0)
    codes = (blocks / scale).astype(np.float32).astype(dtype).astype(np.float64)
    return np.moveaxis((codes * scale).reshape(v.shape), -1, axis)


WIDE = False


def mx_kscale(k):
    if not WIDE:
        return np.ones(k)
    levels = np.array([10, -10, 5, -5, 0])
    a = np.random.permutation(np.resize(levels, k // 512 * 4)).reshape(k // 512, 4)
    idx = np.arange(k)
    return np.exp2(a[idx // 512, idx % 128 // 32])


BF16 = ml_dtypes.bfloat16


def bf(x):
    return np.asarray(x, np.float32).astype(BF16)


def f64(x):
    return np.asarray(x).astype(np.float64)


N, C, H, W, K, S = 4, 512, 32, 32, 128, 4
P = H * W
M = K * (S + 1)
ALPHA = 100.0
EPS = 1e-12
SX = 0.25
LOGIT = 3.5


def softmax(v, axis):
    e = np.exp(v - v.max(axis=axis, keepdims=True))
    return e / e.sum(axis=axis, keepdims=True)


def setup_inputs():
    s = mx_kscale(C)
    s = s / s.min()
    gain = 1.0 + 0.1 * np.random.standard_normal((K, S + 1, 1))
    x = np.random.standard_normal((N, C, H, W)) * SX * s[None, :, None, None]
    centroids = np.random.standard_normal((K, S + 1, C)) * gain * LOGIT / (2.0 * ALPHA * SX * np.sqrt(C)) / s
    return {"x": bf(x), "centroids": bf(centroids)}


def reference(x, centroids):
    cen = f64(centroids)
    xf = f64(x).reshape(N, C, P)
    c_flat = cen.reshape(M, C)
    w = 2.0 * ALPHA * c_flat
    b = -ALPHA * np.sqrt((c_flat ** 2).sum(axis=1))
    z = mxq(xf, 1, "e4m3").transpose(0, 2, 1) @ mxq(w, 1, "e4m3").T
    conv_out = z.transpose(0, 2, 1) + b[None, :, None]
    conv_out = conv_out.reshape(N, K, S + 1, P)
    soft_assign = softmax(conv_out, 1) * softmax(conv_out, 2)
    mult = np.prod(1.0 + soft_assign, axis=2)
    rep = cen[:, 0, :]
    out = (mxq(mult, 2, "e4m3") @ mxq(xf, 2, "e4m3").transpose(0, 2, 1)) - rep[None, :, :] * mult.sum(axis=-1)[:, :, None]
    out = out / np.maximum(np.sqrt((out ** 2).sum(axis=2, keepdims=True)), EPS)
    out = out.reshape(N, K * C)
    out = out / np.maximum(np.sqrt((out ** 2).sum(axis=1, keepdims=True)), EPS)
    return out

@@ -1,0 +1,466 @@
+from contextlib import ExitStack
+
+import concourse.mybir as mybir
+from concourse.masks import make_identity
+
+F32 = mybir.dt.float32
+BF16 = mybir.dt.bfloat16
+U32 = mybir.dt.uint32
+U8 = mybir.dt.uint8
+FP8X4 = mybir.dt.float8_e4m3fn_x4
+ALU = mybir.AluOpType
+ACTF = mybir.ActivationFunctionType
+AX = mybir.AxisListType
+
+P = 128
+IMAGES = 4
+CH = 512
+PIX = 1024
+K = 128
+S5 = 5
+M = K * S5
+GROUPS = 8
+EPS2 = 1e-24
+
+FLOPS = 2 * IMAGES * PIX * M * CH + 2 * IMAGES * K * CH * PIX
+
+
+def tile_sralnet_pa_kernel(tc, x, centroids, out):
+    nc = tc.nc
+    with ExitStack() as ctx:
+        const = ctx.enter_context(tc.tile_pool(name="const", bufs=1))
+        xin = ctx.enter_context(tc.tile_pool(name="xin", bufs=3))
+        xgp = ctx.enter_context(tc.tile_pool(name="xgp", bufs=1))
+        xq1 = ctx.enter_context(tc.tile_pool(name="xq1", bufs=2))
+        xq2 = ctx.enter_context(tc.tile_pool(name="xq2", bufs=4))
+        zbp = ctx.enter_context(tc.tile_pool(name="zbp", bufs=5))
+        dp = ctx.enter_context(tc.tile_pool(name="dp", bufs=2))
+        tmp = ctx.enter_context(tc.tile_pool(name="tmp", bufs=1))
+        img = ctx.enter_context(tc.tile_pool(name="img", bufs=2))
+        mul = ctx.enter_context(tc.tile_pool(name="mul", bufs=4))
+        fin = ctx.enter_context(tc.tile_pool(name="fin", bufs=2))
+        pzm = ctx.enter_context(tc.psum_pool(name="pzm", bufs=3))
+        pz4 = ctx.enter_context(tc.psum_pool(name="pz4", bufs=2))
+        pmisc = ctx.enter_context(tc.psum_pool(name="pmisc", bufs=1))
+        pv = ctx.enter_context(tc.psum_pool(name="pv", bufs=1))
+        pms = ctx.enter_context(tc.psum_pool(name="pms", bufs=1))
+        ctx.enter_context(tc.manual_schedule())
+
+        cen = const.tile([P, S5 * CH], BF16, name="cen")
+        nc.sync.dma_start(out=cen[:], in_=centroids.rearrange("k s c -> k (s c)"))
+        xs = {}
+
+        def xload(n):
+            xs_n = xin.tile([P, 4 * PIX], BF16, name="xs_n", tag="xs")
+            nc.sync.dma_start(out=xs_n[:], in_=x[n].rearrange("(q j) h w -> q (j h w)", j=4))
+            xs[n] = xs_n
+
+        for n in range(3):
+            xload(n)
+
+        ident = const.tile([P, P], F32, name="ident")
+        make_identity(nc, ident[:])
+        ones = const.tile([P, P], F32, name="ones")
+        nc.vector.memset(ones[:], 1.0)
+        expo = const.tile([P, 16], F32, name="expo")
+        nc.vector.memset(expo[:, 0:8], 0.5)
+        nc.vector.memset(expo[:, 8:16], -0.5)
+        qcol = const.tile([P, 2], F32, name="qcol")
+        nc.vector.memset(qcol[:], 0.0)
+        junk_e = const.tile([P, P], F32, name="junk_e")
+        junk_w = const.tile([P, CH], F32, name="junk_w")
+
+        cenw = cen[:].bitcast(F32).rearrange("p (s q u) -> p s u q", s=S5, u=2)
+        wg = const.tile([P, 4 * M], BF16, name="wg", align_bytes=64)
+        for s in range(S5):
+            wt = pmisc.tile([P, 256], F32, name="wt", tag="misc")
+            for u in range(2):
+                nc.tensor.transpose(wt[:, u * P : (u + 1) * P], cenw[:, s, u], ident[:])
+            nc.vector.tensor_scalar(
+                out=wg[:, s * 512 : (s + 1) * 512].rearrange("p (k u e) -> p k u e", u=2, e=2),
+                in0=wt[:].bitcast(BF16).rearrange("p (u k e) -> p k u e", u=2, e=2),
+                scalar1=200.0,
+                scalar2=None,
+                op0=ALU.mult,
+            )
+        wc = const.tile([P, M], U32, name="wc", align_bytes=64)
+        wsc = const.tile([P, M], U8, name="wsc", align_bytes=64)
+        nc.vector.quantize_mx(out=wc[:, 0:512].bitcast(FP8X4), scales=wsc[:, 0:512], in_=wg[:, 0:2048])
+        nc.vector.quantize_mx(out=wc[:, 512:640].bitcast(FP8X4), scales=wsc[:, 512:640], in_=wg[:, 2048:2560])
+
+        n2 = const.tile([P, 8], F32, name="n2")
+        for s in range(S5):
+            nc.scalar.activation(
+                out=junk_w[:], in_=cen[:, s * CH : (s + 1) * CH], func=ACTF.Square, accum_out=n2[:, s : s + 1]
+            )
+        bcol = const.tile([P, 8], F32, name="bcol")
+        nc.gpsimd.tensor_tensor(out=bcol[:, 0:S5], in0=n2[:, 0:S5], in1=expo[:, 0:S5], op=ALU.pow)
+        brep = const.tile([P, M], F32, name="brep")
+        for s in range(S5):
+            nc.vector.tensor_scalar(
+                out=brep[:, s * P : (s + 1) * P],
+                in0=ones[:],
+                scalar1=bcol[:, s : s + 1],
+                scalar2=-100.0,
+                op0=ALU.mult,
+                op1=ALU.mult,
+            )
+        bb = const.tile([P, M], F32, name="bb")
+        bt0 = pmisc.tile([P, 512], F32, name="bt0", tag="misc")
+        for s in range(4):
+            nc.tensor.transpose(bt0[:, s * P : (s + 1) * P], brep[:, s * P : (s + 1) * P], ident[:])
+        nc.vector.tensor_copy(out=bb[:, 0:512], in_=bt0[:])
+        bt1 = pmisc.tile([P, P], F32, name="bt1", tag="misc")
+        nc.tensor.transpose(bt1[:], brep[:, 512:640], ident[:])
+        nc.vector.tensor_copy(out=bb[:, 512:640], in_=bt1[:])
+
+        xc1 = {}
+        xsc1 = {}
+        xc2 = {}
+        xsc2 = {}
+
+        xg2s = {}
+
+        def xprep_a(n):
+            xg1 = xgp.tile([P, 4 * PIX], BF16, name="xg1", tag="xg1", align_bytes=64)
+            src = xs[n][:].rearrange("p (j a r e) -> p e a r j", j=4, a=4, r=P, e=2)
+            dst = xg1[:].rearrange("p (a e r j) -> p e a r j", a=4, e=2, r=P, j=4)
+            for e in range(2):
+                nc.vector.tensor_copy(out=dst[:, e], in_=src[:, e])
+            c1 = xq1.tile([P, PIX], U32, name="c1", tag="c1", align_bytes=64)
+            s1 = xq1.tile([P, PIX], U8, name="s1", tag="s1", align_bytes=64)
+            nc.vector.quantize_mx(out=c1[:].bitcast(FP8X4), scales=s1[:], in_=xg1[:])
+            xc1[n] = c1
+            xsc1[n] = s1
+
+        def xprep_b(n):
+            xw = xs[n][:].bitcast(F32).rearrange("p (j a w) -> p j a w", j=4, a=4, w=P)
+            xg2 = xgp.tile([P, 4 * PIX], BF16, name="xg2", tag="xg2", align_bytes=64)
+            xg2s[n] = xg2
+            xg2w = xg2[:].bitcast(F32).rearrange("p (h jp c) -> p h jp c", h=2, jp=2)
+            for h in range(2):
+                for jp in range(2):
+                    xt = pmisc.tile([P, 512], F32, name="xt", tag="misc")
+                    for jl in range(2):
+                        for u in range(2):
+                            i = jl * 2 + u
+                            nc.tensor.transpose(xt[:, i * P : (i + 1) * P], xw[:, jp * 2 + jl, h * 2 + u], ident[:])
+                    nc.scalar.copy(
+                        out=xg2w[:, h, jp].rearrange("p (jl q u) -> p jl q u", jl=2, u=2),
+                        in_=xt[:].rearrange("p (jl u q) -> p jl q u", jl=2, u=2),
+                    )
+
+        def xprep_c(n):
+            xg2 = xg2s[n]
+            c2 = xq2.tile([P, PIX], U32, name="c2", tag="c2", align_bytes=64)
+            s2 = xq2.tile([P, PIX], U8, name="s2", tag="s2", align_bytes=64)
+            for h in range(2):
+                nc.vector.quantize_mx(
+                    out=c2[:, h * 512 : (h + 1) * 512].bitcast(FP8X4),
+                    scales=s2[:, h * 512 : (h + 1) * 512],
+                    in_=xg2[:, h * 2048 : (h + 1) * 2048],
+                )
+            xc2[n] = c2
+            xsc2[n] = s2
+
+        zm = {}
+        z4 = {}
+
+        def mm1(blk):
+            g = blk // 4
+            t = blk % 4
+            n = g // 2
+            c0 = (blk % 8) * P
+            if t == 0:
+                z4g = pz4.tile([P, 512], F32, name="z4g", tag="z4")
+                z4[g] = z4g
+            zmb = pzm.tile([P, 512], F32, name="zmb", tag="zm")
+            zm[blk] = zmb
+            nc.tensor.matmul_mx(
+                out=zmb[:],
+                lhsT=xc1[n][:, c0 : c0 + P].bitcast(FP8X4),
+                lhsT_scale=xsc1[n][:, c0 : c0 + P],
+                rhs=wc[:, 0:512].bitcast(FP8X4),
+                rhs_scale=wsc[:, 0:512],
+                start=True,
+                stop=True,
+            )
+            nc.tensor.matmul_mx(
+                out=z4[g][:, t * P : (t + 1) * P],
+                lhsT=xc1[n][:, c0 : c0 + P].bitcast(FP8X4),
+                lhsT_scale=xsc1[n][:, c0 : c0 + P],
+                rhs=wc[:, 512:640].bitcast(FP8X4),
+                rhs_scale=wsc[:, 512:640],
+                start=True,
+                stop=True,
+            )
+
+        zb = {}
+        dd = {}
+        nmk = {}
+        csum = {}
+        msx = {}
+        rsum = {}
+        beta = {}
+        acc = {}
+        mcod = {}
+        mscl = {}
+        msum = {}
+
+        def front(g):
+            i = g // 2
+            hh = g % 2
+            if hh == 0:
+                nmk_i = img.tile([P, 40], F32, name="nmk_i", tag="nmk")
+                csum_i = img.tile([P, 40], F32, name="csum_i", tag="csum")
+                msx_i = img.tile([P, PIX], F32, name="msx_i", tag="msx")
+                rsum_i = img.tile([P, PIX], F32, name="rsum_i", tag="rsum")
+                nmk[i] = nmk_i
+                csum[i] = csum_i
+                msx[i] = msx_i
+                rsum[i] = rsum_i
+            zbg = zbp.tile([P, 4 * M], F32, name="zbg", tag="zb")
+            zb[g] = zbg
+            zv = zbg[:].rearrange("p (t m) -> p t m", t=4)
+            for t in range(4):
+                nc.vector.tensor_tensor(out=zv[:, t, 0:512], in0=zm[4 * g + t][:], in1=bb[:, 0:512], op=ALU.add)
+                if 4 * g + t + 3 < 32:
+                    mm1(4 * g + t + 3)
+            nc.vector.tensor_tensor(
+                out=zv[:, :, 512:640],
+                in0=z4[g][:].rearrange("p (t k) -> p t k", t=4),
+                in1=bb[:, 512:640].unsqueeze(1).to_broadcast([P, 4, P]),
+                op=ALU.add,
+            )
+            nc.vector.tensor_reduce(
+                out=nmk[i][:, hh * 20 : hh * 20 + 20],
+                in_=zbg[:].rearrange("p (c k) -> p c k", k=P),
+                axis=AX.X,
+                op=ALU.max,
+                negate=True,
+            )
+            t1 = tmp.tile([P, 1024], F32, name="t1", tag="t1")
+            t1v = t1[:].rearrange("p (t m) -> p t m", t=4)
+            nc.vector.tensor_tensor(out=t1v, in0=zv[:, :, 0:256], in1=zv[:, :, 256:512], op=ALU.max)
+            t2 = tmp.tile([P, 512], F32, name="t2", tag="t2")
+            t2v = t2[:].rearrange("p (t k) -> p t k", t=4)
+            nc.vector.tensor_tensor(out=t2v, in0=t1v[:, :, 0:128], in1=t1v[:, :, 128:256], op=ALU.max)
+            msg = msx[i][:, hh * 512 : (hh + 1) * 512].rearrange("p (t k) -> p t k", t=4)
+            nc.vector.tensor_tensor(out=msg, in0=t2v, in1=zv[:, :, 512:640], op=ALU.max)
+            ddg = dp.tile([P, 4 * M], F32, name="ddg", tag="dd")
+            dd[g] = ddg
+            nc.vector.tensor_tensor(
+                out=ddg[:].rearrange("p (t s k) -> p t s k", t=4, s=S5),
+                in0=zbg[:].rearrange("p (t s k) -> p t s k", t=4, s=S5),
+                in1=msg.unsqueeze(2).to_broadcast([P, 4, S5, P]),
+                op=ALU.subtract,
+            )
+
+        def exps(g):
+            i = g // 2
+            hh = g % 2
+            nc.scalar.activation(out=dd[g][:], in_=dd[g][:], func=ACTF.Exp)
+            for c in range(20):
+                nc.scalar.activation(
+                    out=junk_e[:],
+                    in_=zb[g][:, c * P : (c + 1) * P],
+                    func=ACTF.Exp,
+                    bias=nmk[i][:, hh * 20 + c : hh * 20 + c + 1],
+                    scale=1.0,
+                    accum_out=csum[i][:, hh * 20 + c : hh * 20 + c + 1],
+                )
+
+        def rowsum(g):
+            i = g // 2
+            hh = g % 2
+            ev = dd[g][:].rearrange("p (t m) -> p t m", t=4)
+            r1 = tmp.tile([P, 1024], F32, name="r1", tag="r1")
+            r1v = r1[:].rearrange("p (t m) -> p t m", t=4)
+            nc.vector.tensor_tensor(out=r1v, in0=ev[:, :, 0:256], in1=ev[:, :, 256:512], op=ALU.add)
+            r2 = tmp.tile([P, 512], F32, name="r2", tag="r2")
+            r2v = r2[:].rearrange("p (t k) -> p t k", t=4)
+            nc.vector.tensor_tensor(out=r2v, in0=r1v[:, :, 0:128], in1=r1v[:, :, 128:256], op=ALU.add)
+            nc.vector.tensor_tensor(
+                out=rsum[i][:, hh * 512 : (hh + 1) * 512].rearrange("p (t k) -> p t k", t=4),
+                in0=r2v,
+                in1=ev[:, :, 512:640],
+                op=ALU.add,
+            )
+
+        def logs(i):
+            nc.scalar.activation(out=rsum[i][:], in_=rsum[i][:], func=ACTF.Ln)
+            nc.scalar.activation(out=csum[i][:], in_=csum[i][:], func=ACTF.Ln)
+
+        def lse(i):
+            nc.vector.tensor_tensor(out=rsum[i][:], in0=rsum[i][:], in1=msx[i][:], op=ALU.add)
+            beta_i = img.tile([P, 40], F32, name="beta_i", tag="beta")
+            beta[i] = beta_i
+            nc.vector.tensor_tensor(out=beta_i[:], in0=nmk[i][:], in1=csum[i][:], op=ALU.subtract)
+
+        def wpass(g):
+            i = g // 2
+            hh = g % 2
+            zv = zb[g][:].rearrange("p (t m) -> p t m", t=4)
+            lv = rsum[i][:, hh * 512 : (hh + 1) * 512].rearrange("p (t k) -> p t k", t=4)
+            for s in range(S5):
+                nc.vector.scalar_tensor_tensor(
+                    out=zv[:, :, s * P : (s + 1) * P],
+                    in0=zv[:, :, s * P : (s + 1) * P],
+                    scalar=2.0,
+                    in1=lv,
+                    op0=ALU.mult,
+                    op1=ALU.subtract,
+                )
+
+        def apass(g):
+            i = g // 2
+            hh = g % 2
+            for c in range(20):
+                nc.scalar.activation(
+                    out=zb[g][:, c * P : (c + 1) * P],
+                    in_=zb[g][:, c * P : (c + 1) * P],
+                    func=ACTF.Exp,
+                    bias=beta[i][:, hh * 20 + c : hh * 20 + c + 1],
+                    scale=1.0,
+                )
+
+        def prods(i):
+            pair = (2 * i, 2 * i + 1)
+            for g in pair:
+                accg = mul.tile([P, 512], F32, name="accg", tag="acc")
+                acc[g] = accg
+            for s in range(S5):
+                for g in pair:
+                    zv = zb[g][:].rearrange("p (t m) -> p t m", t=4)
+                    av = acc[g][:].rearrange("p (t k) -> p t k", t=4)
+                    if s == 0:
+                        nc.vector.tensor_scalar(
+                            out=av, in0=zv[:, :, 0:P], scalar1=1.0, scalar2=None, op0=ALU.add
+                        )
+                    else:
+                        nc.vector.scalar_tensor_tensor(
+                            out=av,
+                            in0=zv[:, :, s * P : (s + 1) * P],
+                            scalar=1.0,
+                            in1=av,
+                            op0=ALU.add,
+                            op1=ALU.mult,
+                        )
+            msp = pms.tile([P, 4], F32, name="msp", tag="ms")
+            msum[i] = msp
+            mgs = {}
+            for g in pair:
+                mg = mul.tile([P, 512], BF16, name="mg", tag="mg", align_bytes=64)
+                mgs[g] = mg
+                nc.scalar.copy(
+                    out=mg[:].rearrange("p (k t) -> p k t", t=4),
+                    in_=acc[g][:].rearrange("p (t k) -> p k t", t=4),
+                )
+                for t in range(4):
+                    nc.tensor.matmul(
+                        out=msp[:, 0:2],
+                        lhsT=acc[g][:, t * P : (t + 1) * P],
+                        rhs=ones[:, 0:2],
+                        start=(g == pair[0] and t == 0),
+                        stop=(g == pair[1] and t == 3),
+                    )
+            return mgs
+
+        def mquant(i, mgs):
+            for g in (2 * i, 2 * i + 1):
+                mc = mul.tile([P, P], U32, name="mc", tag="mc", align_bytes=64)
+                msc = mul.tile([P, P], U8, name="msc", tag="msc", align_bytes=64)
+                nc.vector.quantize_mx(out=mc[:].bitcast(FP8X4), scales=msc[:], in_=mgs[g][:])
+                mcod[g] = mc
+                mscl[g] = msc
+
+        fst = {}
+
+        def final_a(i):
+            v = pv.tile([P, CH], F32, name="v", tag="v")
+            for hh in range(2):
+                g = 2 * i + hh
+                nc.tensor.matmul_mx(
+                    out=v[:],
+                    lhsT=mcod[g][:].bitcast(FP8X4),
+                    lhsT_scale=mscl[g][:],
+                    rhs=xc2[i][:, hh * 512 : (hh + 1) * 512].bitcast(FP8X4),
+                    rhs_scale=xsc2[i][:, hh * 512 : (hh + 1) * 512],
+                    start=(hh == 0),
+                    stop=(hh == 1),
+                )
+            sm = fin.tile([P, 16], F32, name="sm", tag="sm")
+            ssq = fin.tile([P, 1], F32, name="ssq", tag="ssq")
+            nc.vector.tensor_scalar(
+                out=sm[:, 0:1], in0=msum[i][:, 0:1], scalar1=-1.0, scalar2=None, op0=ALU.mult
+            )
+            vp = fin.tile([P, CH], F32, name="vp", tag="vp")
+            nc.vector.scalar_tensor_tensor(
+                out=vp[:].rearrange("p (j q) -> p j q", j=4),
+                in0=cen[:, 0:CH].rearrange("p (q j) -> p j q", j=4),
+                scalar=sm[:, 0:1],
+                in1=v[:].rearrange("p (j q) -> p j q", j=4),
+                op0=ALU.mult,
+                op1=ALU.add,
+            )
+            nc.scalar.activation(out=junk_w[:], in_=vp[:], func=ACTF.Square, accum_out=ssq[:, 0:1])
+            pg = fin.tile([P, 16], F32, name="pg", tag="pg")
+            nc.gpsimd.tensor_scalar(out=pg[:, 0:1], in0=ssq[:, 0:1], scalar1=EPS2, scalar2=None, op0=ALU.max)
+            nc.gpsimd.tensor_tensor(out=pg[:, 1:2], in0=pg[:, 0:1], in1=expo[:, 8:9], op=ALU.pow)
+            nc.gpsimd.tensor_tensor(out=pg[:, 2:3], in0=ssq[:, 0:1], in1=pg[:, 1:2], op=ALU.mult)
+            nc.gpsimd.tensor_tensor(out=qcol[:, 0:1], in0=pg[:, 2:3], in1=pg[:, 1:2], op=ALU.mult)
+            fst[i] = (sm, pg, vp)
+
+        def final_b(i):
+            sm, pg, vp = fst[i]
+            nc.tensor.matmul(out=msum[i][:, 2:4], lhsT=ones[:], rhs=qcol[:], start=True, stop=True)
+            nc.vector.tensor_scalar(
+                out=sm[:, 1:2], in0=msum[i][:, 2:3], scalar1=EPS2, scalar2=None, op0=ALU.max
+            )
+            nc.gpsimd.tensor_tensor(out=pg[:, 3:4], in0=sm[:, 1:2], in1=expo[:, 8:9], op=ALU.pow)
+            nc.gpsimd.tensor_tensor(out=pg[:, 4:5], in0=pg[:, 3:4], in1=pg[:, 1:2], op=ALU.mult)
+            o = fin.tile([P, CH], F32, name="o", tag="o")
+            nc.scalar.activation(
+                out=o[:].rearrange("p (q j) -> p q j", j=4),
+                in_=vp[:].rearrange("p (j q) -> p q j", j=4),
+                func=ACTF.Copy,
+                scale=pg[:, 4:5],
+            )
+            nc.sync.dma_start(out=out[i].rearrange("(k c) -> k c", c=CH), in_=o[:])
+
+        xprep_a(0)
+        for blk in range(3):
+            mm1(blk)
+        for t in range(GROUPS + 3):
+            even = t % 2 == 0
+            if t < GROUPS:
+                front(t)
+            if even and t < GROUPS:
+                xprep_b(t // 2)
+            if t == 0:
+                xload(3)
+            if t < GROUPS:
+                exps(t)
+            if (not even) and t >= 5:
+                final_b((t - 5) // 2)
+            if 1 <= t <= GROUPS:
+                rowsum(t - 1)
+            if even and 2 <= t <= GROUPS:
+                logs((t - 2) // 2)
+            if (not even) and t >= 3:
+                lse((t - 3) // 2)
+                wpass(t - 3)
+                apass(t - 3)
+                wpass(t - 2)
+                apass(t - 2)
+            if (not even) and t < GROUPS:
+                xprep_c(t // 2)
+            if even and t >= 4:
+                mgs = prods((t - 4) // 2)
+                if t + 2 < GROUPS:
+                    xprep_a(t // 2 + 1)
+                mquant((t - 4) // 2, mgs)
+                final_a((t - 4) // 2)
+            elif even and t + 2 < GROUPS:
+                xprep_a(t // 2 + 1)
+        final_b(IMAGES - 1)

@@ -29,21 +29,22 @@ def tile_sralnet_pa_kernel(tc, x, centroids, out):
     nc = tc.nc
     with ExitStack() as ctx:
         const = ctx.enter_context(tc.tile_pool(name="const", bufs=1))
-        xin = ctx.enter_context(tc.tile_pool(name="xin", bufs=3))
+        xin = ctx.enter_context(tc.tile_pool(name="xin", bufs=4))
         xgp = ctx.enter_context(tc.tile_pool(name="xgp", bufs=1))
         xq1 = ctx.enter_context(tc.tile_pool(name="xq1", bufs=2))
         xq2 = ctx.enter_context(tc.tile_pool(name="xq2", bufs=4))
         zbp = ctx.enter_context(tc.tile_pool(name="zbp", bufs=5))
-        dp = ctx.enter_context(tc.tile_pool(name="dp", bufs=2))
+        dp = ctx.enter_context(tc.tile_pool(name="dp", bufs=1))
         tmp = ctx.enter_context(tc.tile_pool(name="tmp", bufs=1))
+        nmp = ctx.enter_context(tc.tile_pool(name="nmp", bufs=2))
         img = ctx.enter_context(tc.tile_pool(name="img", bufs=2))
         mul = ctx.enter_context(tc.tile_pool(name="mul", bufs=4))
         fin = ctx.enter_context(tc.tile_pool(name="fin", bufs=2))
         pzm = ctx.enter_context(tc.psum_pool(name="pzm", bufs=3))
-        pz4 = ctx.enter_context(tc.psum_pool(name="pz4", bufs=2))
+        pz4 = ctx.enter_context(tc.psum_pool(name="pz4", bufs=1))
+        pdt = ctx.enter_context(tc.psum_pool(name="pdt", bufs=2))
+        prb = ctx.enter_context(tc.psum_pool(name="prb", bufs=1))
         pmisc = ctx.enter_context(tc.psum_pool(name="pmisc", bufs=1))
-        pv = ctx.enter_context(tc.psum_pool(name="pv", bufs=1))
-        pms = ctx.enter_context(tc.psum_pool(name="pms", bufs=1))
         ctx.enter_context(tc.manual_schedule())
 
         cen = const.tile([P, S5 * CH], BF16, name="cen")
@@ -55,7 +56,7 @@ def tile_sralnet_pa_kernel(tc, x, centroids, out):
             nc.sync.dma_start(out=xs_n[:], in_=x[n].rearrange("(q j) h w -> q (j h w)", j=4))
             xs[n] = xs_n
 
-        for n in range(3):
+        for n in range(IMAGES):
             xload(n)
 
         ident = const.tile([P, P], F32, name="ident")
@@ -96,23 +97,25 @@ def tile_sralnet_pa_kernel(tc, x, centroids, out):
         bcol = const.tile([P, 8], F32, name="bcol")
         nc.gpsimd.tensor_tensor(out=bcol[:, 0:S5], in0=n2[:, 0:S5], in1=expo[:, 0:S5], op=ALU.pow)
         brep = const.tile([P, M], F32, name="brep")
-        for s in range(S5):
-            nc.vector.tensor_scalar(
-                out=brep[:, s * P : (s + 1) * P],
-                in0=ones[:],
-                scalar1=bcol[:, s : s + 1],
-                scalar2=-100.0,
-                op0=ALU.mult,
-                op1=ALU.mult,
-            )
         bb = const.tile([P, M], F32, name="bb")
-        bt0 = pmisc.tile([P, 512], F32, name="bt0", tag="misc")
-        for s in range(4):
-            nc.tensor.transpose(bt0[:, s * P : (s + 1) * P], brep[:, s * P : (s + 1) * P], ident[:])
-        nc.vector.tensor_copy(out=bb[:, 0:512], in_=bt0[:])
-        bt1 = pmisc.tile([P, P], F32, name="bt1", tag="misc")
-        nc.tensor.transpose(bt1[:], brep[:, 512:640], ident[:])
-        nc.vector.tensor_copy(out=bb[:, 512:640], in_=bt1[:])
+
+        def bias_spread():
+            for s in range(S5):
+                nc.vector.tensor_scalar(
+                    out=brep[:, s * P : (s + 1) * P],
+                    in0=ones[:],
+                    scalar1=bcol[:, s : s + 1],
+                    scalar2=-100.0,
+                    op0=ALU.mult,
+                    op1=ALU.mult,
+                )
+            bt0 = pmisc.tile([P, 512], F32, name="bt0", tag="misc")
+            for s in range(4):
+                nc.tensor.transpose(bt0[:, s * P : (s + 1) * P], brep[:, s * P : (s + 1) * P], ident[:])
+            nc.vector.tensor_copy(out=bb[:, 0:512], in_=bt0[:])
+            bt1 = pmisc.tile([P, P], F32, name="bt1", tag="misc")
+            nc.tensor.transpose(bt1[:], brep[:, 512:640], ident[:])
+            nc.vector.tensor_copy(out=bb[:, 512:640], in_=bt1[:])
 
         xc1 = {}
         xsc1 = {}
@@ -121,26 +124,31 @@ def tile_sralnet_pa_kernel(tc, x, centroids, out):
 
         xg2s = {}
 
-        def xprep_a(n):
+        def xprep_a_list(n):
             xg1 = xgp.tile([P, 4 * PIX], BF16, name="xg1", tag="xg1", align_bytes=64)
             src = xs[n][:].rearrange("p (j a r e) -> p e a r j", j=4, a=4, r=P, e=2)
             dst = xg1[:].rearrange("p (a e r j) -> p e a r j", a=4, e=2, r=P, j=4)
-            for e in range(2):
-                nc.vector.tensor_copy(out=dst[:, e], in_=src[:, e])
             c1 = xq1.tile([P, PIX], U32, name="c1", tag="c1", align_bytes=64)
             s1 = xq1.tile([P, PIX], U8, name="s1", tag="s1", align_bytes=64)
-            nc.vector.quantize_mx(out=c1[:].bitcast(FP8X4), scales=s1[:], in_=xg1[:])
             xc1[n] = c1
             xsc1[n] = s1
 
+            def regroup(e):
+                nc.vector.tensor_copy(out=dst[:, e], in_=src[:, e])
+
+            def quant():
+                nc.vector.quantize_mx(out=c1[:].bitcast(FP8X4), scales=s1[:], in_=xg1[:])
+
+            return [lambda: regroup(0), lambda: regroup(1), quant]
+
         def xprep_b(n):
             xw = xs[n][:].bitcast(F32).rearrange("p (j a w) -> p j a w", j=4, a=4, w=P)
-            xg2 = xgp.tile([P, 4 * PIX], BF16, name="xg2", tag="xg2", align_bytes=64)
+            xg2 = xgp.tile([P, 4 * PIX], BF16, name="xg2", tag="xg2", bufs=2, align_bytes=64)
             xg2s[n] = xg2
             xg2w = xg2[:].bitcast(F32).rearrange("p (h jp c) -> p h jp c", h=2, jp=2)
             for h in range(2):
                 for jp in range(2):
-                    xt = pmisc.tile([P, 512], F32, name="xt", tag="misc")
+                    xt = pdt.tile([P, 512], F32, name="xt", tag="dt")
                     for jl in range(2):
                         for u in range(2):
                             i = jl * 2 + u
@@ -150,23 +158,28 @@ def tile_sralnet_pa_kernel(tc, x, centroids, out):
                         in_=xt[:].rearrange("p (jl u q) -> p jl q u", jl=2, u=2),
                     )
 
-        def xprep_c(n):
+        def xprep_c_list(n):
             xg2 = xg2s[n]
             c2 = xq2.tile([P, PIX], U32, name="c2", tag="c2", align_bytes=64)
             s2 = xq2.tile([P, PIX], U8, name="s2", tag="s2", align_bytes=64)
-            for h in range(2):
+            xc2[n] = c2
+            xsc2[n] = s2
+
+            def quant(h):
                 nc.vector.quantize_mx(
                     out=c2[:, h * 512 : (h + 1) * 512].bitcast(FP8X4),
                     scales=s2[:, h * 512 : (h + 1) * 512],
                     in_=xg2[:, h * 2048 : (h + 1) * 2048],
                 )
-            xc2[n] = c2
-            xsc2[n] = s2
+
+            return [lambda: quant(0), lambda: quant(1)]
 
         zm = {}
         z4 = {}
 
         def mm1(blk):
+            if blk >= 4 * GROUPS:
+                return
             g = blk // 4
             t = blk % 4
             n = g // 2
@@ -196,113 +209,207 @@ def tile_sralnet_pa_kernel(tc, x, centroids, out):
             )
 
         zb = {}
-        dd = {}
         nmk = {}
-        csum = {}
         msx = {}
-        rsum = {}
+        nms = {}
+        rc = {}
+        rbs = {}
         beta = {}
         acc = {}
         mcod = {}
         mscl = {}
         msum = {}
 
-        def front(g):
+        def e1part(g, j):
             i = g // 2
             hh = g % 2
-            if hh == 0:
-                nmk_i = img.tile([P, 40], F32, name="nmk_i", tag="nmk")
-                csum_i = img.tile([P, 40], F32, name="csum_i", tag="csum")
-                msx_i = img.tile([P, PIX], F32, name="msx_i", tag="msx")
-                rsum_i = img.tile([P, PIX], F32, name="rsum_i", tag="rsum")
-                nmk[i] = nmk_i
-                csum[i] = csum_i
-                msx[i] = msx_i
-                rsum[i] = rsum_i
-            zbg = zbp.tile([P, 4 * M], F32, name="zbg", tag="zb")
-            zb[g] = zbg
-            zv = zbg[:].rearrange("p (t m) -> p t m", t=4)
-            for t in range(4):
-                nc.vector.tensor_tensor(out=zv[:, t, 0:512], in0=zm[4 * g + t][:], in1=bb[:, 0:512], op=ALU.add)
-                if 4 * g + t + 3 < 32:
-                    mm1(4 * g + t + 3)
-            nc.vector.tensor_tensor(
-                out=zv[:, :, 512:640],
-                in0=z4[g][:].rearrange("p (t k) -> p t k", t=4),
-                in1=bb[:, 512:640].unsqueeze(1).to_broadcast([P, 4, P]),
-                op=ALU.add,
-            )
-            nc.vector.tensor_reduce(
-                out=nmk[i][:, hh * 20 : hh * 20 + 20],
-                in_=zbg[:].rearrange("p (c k) -> p c k", k=P),
-                axis=AX.X,
-                op=ALU.max,
-                negate=True,
-            )
-            t1 = tmp.tile([P, 1024], F32, name="t1", tag="t1")
-            t1v = t1[:].rearrange("p (t m) -> p t m", t=4)
-            nc.vector.tensor_tensor(out=t1v, in0=zv[:, :, 0:256], in1=zv[:, :, 256:512], op=ALU.max)
-            t2 = tmp.tile([P, 512], F32, name="t2", tag="t2")
-            t2v = t2[:].rearrange("p (t k) -> p t k", t=4)
-            nc.vector.tensor_tensor(out=t2v, in0=t1v[:, :, 0:128], in1=t1v[:, :, 128:256], op=ALU.max)
-            msg = msx[i][:, hh * 512 : (hh + 1) * 512].rearrange("p (t k) -> p t k", t=4)
-            nc.vector.tensor_tensor(out=msg, in0=t2v, in1=zv[:, :, 512:640], op=ALU.max)
-            ddg = dp.tile([P, 4 * M], F32, name="ddg", tag="dd")
-            dd[g] = ddg
-            nc.vector.tensor_tensor(
-                out=ddg[:].rearrange("p (t s k) -> p t s k", t=4, s=S5),
-                in0=zbg[:].rearrange("p (t s k) -> p t s k", t=4, s=S5),
-                in1=msg.unsqueeze(2).to_broadcast([P, 4, S5, P]),
-                op=ALU.subtract,
-            )
-
-        def exps(g):
-            i = g // 2
-            hh = g % 2
-            nc.scalar.activation(out=dd[g][:], in_=dd[g][:], func=ACTF.Exp)
-            for c in range(20):
+            for c in range(4 * j, 4 * j + 4):
                 nc.scalar.activation(
                     out=junk_e[:],
                     in_=zb[g][:, c * P : (c + 1) * P],
                     func=ACTF.Exp,
                     bias=nmk[i][:, hh * 20 + c : hh * 20 + c + 1],
                     scale=1.0,
-                    accum_out=csum[i][:, hh * 20 + c : hh * 20 + c + 1],
+                    accum_out=rc[i][:, PIX + hh * 20 + c : PIX + hh * 20 + c + 1],
                 )
 
-        def rowsum(g):
-            i = g // 2
-            hh = g % 2
-            ev = dd[g][:].rearrange("p (t m) -> p t m", t=4)
-            r1 = tmp.tile([P, 1024], F32, name="r1", tag="r1")
-            r1v = r1[:].rearrange("p (t m) -> p t m", t=4)
-            nc.vector.tensor_tensor(out=r1v, in0=ev[:, :, 0:256], in1=ev[:, :, 256:512], op=ALU.add)
-            r2 = tmp.tile([P, 512], F32, name="r2", tag="r2")
-            r2v = r2[:].rearrange("p (t k) -> p t k", t=4)
-            nc.vector.tensor_tensor(out=r2v, in0=r1v[:, :, 0:128], in1=r1v[:, :, 128:256], op=ALU.add)
-            nc.vector.tensor_tensor(
-                out=rsum[i][:, hh * 512 : (hh + 1) * 512].rearrange("p (t k) -> p t k", t=4),
-                in0=r2v,
-                in1=ev[:, :, 512:640],
-                op=ALU.add,
-            )
+        e2s = {}
+
+        def dpart(g, s):
+            if s == 0:
+                e2 = dp.tile([P, 4 * M], F32, name="e2", tag="e2")
+                e2s[g] = e2
+            dt = pdt.tile([P, 512], F32, name="dt", tag="dt")
+            for t in range(4):
+                c = t * S5 + s
+                nc.tensor.matmul(
+                    out=dt[:, t * P : (t + 1) * P],
+                    lhsT=zb[g][:, c * P : (c + 1) * P],
+                    rhs=ident[:],
+                    is_transpose=True,
+                    start=True,
+                    stop=False,
+                )
+                nc.tensor.matmul(
+                    out=dt[:, t * P : (t + 1) * P],
+                    lhsT=nms[g][:, t * P : (t + 1) * P],
+                    rhs=ident[:],
+                    is_transpose=True,
+                    start=False,
+                    stop=True,
+                )
+            nc.scalar.activation(out=e2s[g][:, s * 512 : (s + 1) * 512], in_=dt[:], func=ACTF.Exp)
+
+        def rpart(g):
+            e2 = e2s[g]
+            rb = prb.tile([P, 512], F32, name="rb", tag="rb")
+            for t in range(4):
+                for s in range(S5):
+                    nc.tensor.matmul(
+                        out=rb[:, t * P : (t + 1) * P],
+                        lhsT=e2[:, s * 512 + t * P : s * 512 + (t + 1) * P],
+                        rhs=ident[:],
+                        is_transpose=True,
+                        start=(s == 0),
+                        stop=(s == S5 - 1),
+                    )
+            rbs[g] = rb
+
+        def hook(t, j):
+            if 1 <= t <= GROUPS:
+                if j < S5:
+                    dpart(t - 1, j)
+                    e1part(t - 1, j)
+                if j == 5:
+                    rpart(t - 1)
+                if j == 7:
+                    cpr(t - 1)
+                    if t % 2 == 0:
+                        logs((t - 2) // 2)
+            if t == 0 and j == 4:
+                xprep_b(2)
+            if t == 0 and j == 5:
+                xprep_b(3)
+
+        def cpr(g):
+            nc.scalar.copy(out=rc[g // 2][:, (g % 2) * 512 : (g % 2 + 1) * 512], in_=rbs[g][:])
 
         def logs(i):
-            nc.scalar.activation(out=rsum[i][:], in_=rsum[i][:], func=ACTF.Ln)
-            nc.scalar.activation(out=csum[i][:], in_=csum[i][:], func=ACTF.Ln)
+            nc.scalar.activation(out=rc[i][:], in_=rc[i][:], func=ACTF.Ln)
 
-        def lse(i):
-            nc.vector.tensor_tensor(out=rsum[i][:], in0=rsum[i][:], in1=msx[i][:], op=ALU.add)
-            beta_i = img.tile([P, 40], F32, name="beta_i", tag="beta")
-            beta[i] = beta_i
-            nc.vector.tensor_tensor(out=beta_i[:], in0=nmk[i][:], in1=csum[i][:], op=ALU.subtract)
+        def front_list(g):
+            i = g // 2
+            hh = g % 2
+            if hh == 0:
+                nmk_i = img.tile([P, 40], F32, name="nmk_i", tag="nmk")
+                msx_i = img.tile([P, PIX], F32, name="msx_i", tag="msx")
+                rc_i = img.tile([P, PIX + 40], F32, name="rc_i", tag="rc")
+                nmk[i] = nmk_i
+                msx[i] = msx_i
+                rc[i] = rc_i
+            zbg = zbp.tile([P, 4 * M], F32, name="zbg", tag="zb")
+            zb[g] = zbg
+            zv = zbg[:].rearrange("p (t m) -> p t m", t=4)
+            t1 = tmp.tile([P, 1024], F32, name="t1", tag="t1")
+            t1v = t1[:].rearrange("p (t m) -> p t m", t=4)
+            t2 = tmp.tile([P, 512], F32, name="t2", tag="t2")
+            t2v = t2[:].rearrange("p (t k) -> p t k", t=4)
+            msg = msx[i][:, hh * 512 : (hh + 1) * 512]
+            nmsg = nmp.tile([P, 512], F32, name="nmsg", tag="nms")
+            nms[g] = nmsg
 
-        def wpass(g):
+            def v1(t):
+                nc.vector.tensor_tensor(out=zv[:, t, 0:512], in0=zm[4 * g + t][:], in1=bb[:, 0:512], op=ALU.add)
+
+            def f0():
+                v1(0)
+                mm1(4 * g + 3)
+                hook(g, 0)
+
+            def f1():
+                v1(1)
+                hook(g, 1)
+
+            def f2():
+                v1(2)
+                hook(g, 2)
+
+            def f3():
+                v1(3)
+                hook(g, 3)
+
+            def f4():
+                nc.vector.tensor_tensor(
+                    out=zv[:, :, 512:640],
+                    in0=z4[g][:].rearrange("p (t k) -> p t k", t=4),
+                    in1=bb[:, 512:640].unsqueeze(1).to_broadcast([P, 4, P]),
+                    op=ALU.add,
+                )
+                mm1(4 * g + 4)
+                mm1(4 * g + 5)
+                mm1(4 * g + 6)
+                hook(g, 4)
+
+            def f5():
+                nc.vector.tensor_tensor(out=t1v, in0=zv[:, :, 0:256], in1=zv[:, :, 256:512], op=ALU.max)
+                hook(g, 5)
+
+            def f6():
+                nc.vector.tensor_reduce(
+                    out=nmk[i][:, hh * 20 : hh * 20 + 20],
+                    in_=zbg[:].rearrange("p (c k) -> p c k", k=P),
+                    axis=AX.X,
+                    op=ALU.max,
+                    negate=True,
+                )
+                hook(g, 6)
+
+            def f7():
+                nc.vector.tensor_tensor(out=t2v, in0=t1v[:, :, 0:128], in1=t1v[:, :, 128:256], op=ALU.max)
+                hook(g, 7)
+
+            def f8():
+                nc.vector.tensor_tensor(
+                    out=msg.rearrange("p (t k) -> p t k", t=4), in0=t2v, in1=zv[:, :, 512:640], op=ALU.max
+                )
+
+            def f9():
+                nc.vector.tensor_scalar(out=nmsg[:], in0=msg, scalar1=-1.0, scalar2=None, op0=ALU.mult)
+
+            return [f0, f1, f2, f3, f4, f5, f6, f7, f8, f9]
+
+        def lse_list(i):
+            def l0():
+                nc.vector.tensor_tensor(out=rc[i][:, 0:PIX], in0=rc[i][:, 0:PIX], in1=msx[i][:], op=ALU.add)
+
+            def l1():
+                beta_i = img.tile([P, 40], F32, name="beta_i", tag="beta")
+                beta[i] = beta_i
+                nc.vector.tensor_tensor(out=beta_i[:], in0=nmk[i][:], in1=rc[i][:, PIX : PIX + 40], op=ALU.subtract)
+
+            return [l0, l1]
+
+        def apass(g):
+            i = g // 2
+            hh = g % 2
+            for s in range(S5):
+                for t in range(4):
+                    c = t * S5 + s
+                    nc.scalar.activation(
+                        out=zb[g][:, c * P : (c + 1) * P],
+                        in_=zb[g][:, c * P : (c + 1) * P],
+                        func=ACTF.Exp,
+                        bias=beta[i][:, hh * 20 + c : hh * 20 + c + 1],
+                        scale=1.0,
+                    )
+
+        def w_list(g):
             i = g // 2
             hh = g % 2
             zv = zb[g][:].rearrange("p (t m) -> p t m", t=4)
-            lv = rsum[i][:, hh * 512 : (hh + 1) * 512].rearrange("p (t k) -> p t k", t=4)
-            for s in range(S5):
+            lv = rc[i][:, hh * 512 : (hh + 1) * 512].rearrange("p (t k) -> p t k", t=4)
+
+            def wone(s):
                 nc.vector.scalar_tensor_tensor(
                     out=zv[:, :, s * P : (s + 1) * P],
                     in0=zv[:, :, s * P : (s + 1) * P],
@@ -311,45 +418,40 @@ def tile_sralnet_pa_kernel(tc, x, centroids, out):
                     op0=ALU.mult,
                     op1=ALU.subtract,
                 )
+                if s == S5 - 1:
+                    apass(g)
 
-        def apass(g):
-            i = g // 2
-            hh = g % 2
-            for c in range(20):
-                nc.scalar.activation(
-                    out=zb[g][:, c * P : (c + 1) * P],
-                    in_=zb[g][:, c * P : (c + 1) * P],
-                    func=ACTF.Exp,
-                    bias=beta[i][:, hh * 20 + c : hh * 20 + c + 1],
-                    scale=1.0,
-                )
+            return [lambda s=s: wone(s) for s in range(S5)]
 
-        def prods(i):
+        mgs = {}
+
+        def prod_list(i):
             pair = (2 * i, 2 * i + 1)
             for g in pair:
                 accg = mul.tile([P, 512], F32, name="accg", tag="acc")
                 acc[g] = accg
-            for s in range(S5):
-                for g in pair:
-                    zv = zb[g][:].rearrange("p (t m) -> p t m", t=4)
-                    av = acc[g][:].rearrange("p (t k) -> p t k", t=4)
-                    if s == 0:
-                        nc.vector.tensor_scalar(
-                            out=av, in0=zv[:, :, 0:P], scalar1=1.0, scalar2=None, op0=ALU.add
-                        )
-                    else:
-                        nc.vector.scalar_tensor_tensor(
-                            out=av,
-                            in0=zv[:, :, s * P : (s + 1) * P],
-                            scalar=1.0,
-                            in1=av,
-                            op0=ALU.add,
-                            op1=ALU.mult,
-                        )
-            msp = pms.tile([P, 4], F32, name="msp", tag="ms")
-            msum[i] = msp
-            mgs = {}
-            for g in pair:
+
+            def pone(s, g):
+                zv = zb[g][:].rearrange("p (t m) -> p t m", t=4)
+                av = acc[g][:].rearrange("p (t k) -> p t k", t=4)
+                if s == 0:
+                    nc.vector.tensor_scalar(out=av, in0=zv[:, :, 0:P], scalar1=1.0, scalar2=None, op0=ALU.add)
+                else:
+                    nc.vector.scalar_tensor_tensor(
+                        out=av,
+                        in0=zv[:, :, s * P : (s + 1) * P],
+                        scalar=1.0,
+                        in1=av,
+                        op0=ALU.add,
+                        op1=ALU.mult,
+                    )
+                if s == S5 - 1:
+                    after(g)
+
+            def after(g):
+                if g == pair[0]:
+                    msp = pmisc.tile([P, 4], F32, name="msp", tag="misc")
+                    msum[i] = msp
                 mg = mul.tile([P, 512], BF16, name="mg", tag="mg", align_bytes=64)
                 mgs[g] = mg
                 nc.scalar.copy(
@@ -358,26 +460,29 @@ def tile_sralnet_pa_kernel(tc, x, centroids, out):
                 )
                 for t in range(4):
                     nc.tensor.matmul(
-                        out=msp[:, 0:2],
+                        out=msum[i][:, 0:2],
                         lhsT=acc[g][:, t * P : (t + 1) * P],
                         rhs=ones[:, 0:2],
                         start=(g == pair[0] and t == 0),
                         stop=(g == pair[1] and t == 3),
                     )
-            return mgs
 
-        def mquant(i, mgs):
-            for g in (2 * i, 2 * i + 1):
-                mc = mul.tile([P, P], U32, name="mc", tag="mc", align_bytes=64)
-                msc = mul.tile([P, P], U8, name="msc", tag="msc", align_bytes=64)
-                nc.vector.quantize_mx(out=mc[:].bitcast(FP8X4), scales=msc[:], in_=mgs[g][:])
-                mcod[g] = mc
-                mscl[g] = msc
+            return [lambda s=s, g=g: pone(s, g) for s in range(S5) for g in pair]
+
+        def mquant(g):
+            mc = mul.tile([P, P], U32, name="mc", tag="mc", align_bytes=64)
+            msc = mul.tile([P, P], U8, name="msc", tag="msc", align_bytes=64)
+            nc.vector.quantize_mx(out=mc[:].bitcast(FP8X4), scales=msc[:], in_=mgs[g][:])
+            mcod[g] = mc
+            mscl[g] = msc
 
         fst = {}
 
-        def final_a(i):
-            v = pv.tile([P, CH], F32, name="v", tag="v")
+        vts = {}
+
+        def final_mm(i):
+            v = prb.tile([P, CH], F32, name="v", tag="rb")
+            vts[i] = v
             for hh in range(2):
                 g = 2 * i + hh
                 nc.tensor.matmul_mx(
@@ -389,6 +494,9 @@ def tile_sralnet_pa_kernel(tc, x, centroids, out):
                     start=(hh == 0),
                     stop=(hh == 1),
                 )
+
+        def final_a(i):
+            v = vts[i]
             sm = fin.tile([P, 16], F32, name="sm", tag="sm")
             ssq = fin.tile([P, 1], F32, name="ssq", tag="ssq")
             nc.vector.tensor_scalar(
@@ -411,14 +519,19 @@ def tile_sralnet_pa_kernel(tc, x, centroids, out):
             nc.gpsimd.tensor_tensor(out=qcol[:, 0:1], in0=pg[:, 2:3], in1=pg[:, 1:2], op=ALU.mult)
             fst[i] = (sm, pg, vp)
 
+        def final_tot(i):
+            nc.tensor.matmul(out=msum[i][:, 2:4], lhsT=ones[:], rhs=qcol[:], start=True, stop=True)
+
         def final_b(i):
             sm, pg, vp = fst[i]
-            nc.tensor.matmul(out=msum[i][:, 2:4], lhsT=ones[:], rhs=qcol[:], start=True, stop=True)
             nc.vector.tensor_scalar(
                 out=sm[:, 1:2], in0=msum[i][:, 2:3], scalar1=EPS2, scalar2=None, op0=ALU.max
             )
             nc.gpsimd.tensor_tensor(out=pg[:, 3:4], in0=sm[:, 1:2], in1=expo[:, 8:9], op=ALU.pow)
             nc.gpsimd.tensor_tensor(out=pg[:, 4:5], in0=pg[:, 3:4], in1=pg[:, 1:2], op=ALU.mult)
+
+        def final_c(i):
+            sm, pg, vp = fst[i]
             o = fin.tile([P, CH], F32, name="o", tag="o")
             nc.scalar.activation(
                 out=o[:].rearrange("p (q j) -> p q j", j=4),
@@ -428,39 +541,63 @@ def tile_sralnet_pa_kernel(tc, x, centroids, out):
             )
             nc.sync.dma_start(out=out[i].rearrange("(k c) -> k c", c=CH), in_=o[:])
 
-        xprep_a(0)
-        for blk in range(3):
-            mm1(blk)
-        for t in range(GROUPS + 3):
-            even = t % 2 == 0
+        def zipped(a, b):
+            for j in range(max(len(a), len(b))):
+                if j < len(a):
+                    a[j]()
+                if j < len(b):
+                    b[j]()
+
+        for fn in xprep_a_list(0):
+            fn()
+        xprep_b(0)
+        bias_spread()
+        mm1(0)
+        mm1(1)
+        mm1(2)
+        xprep_b(1)
+        for t in range(GROUPS + 5):
+            fr = []
             if t < GROUPS:
-                front(t)
-            if even and t < GROUPS:
-                xprep_b(t // 2)
+                fr = front_list(t)
+            elif t == GROUPS:
+                fr = [lambda j=j: hook(GROUPS, j) for j in range(7)]
+            bk = []
             if t == 0:
-                xload(3)
-            if t < GROUPS:
-                exps(t)
-            if (not even) and t >= 5:
-                final_b((t - 5) // 2)
-            if 1 <= t <= GROUPS:
-                rowsum(t - 1)
-            if even and 2 <= t <= GROUPS:
-                logs((t - 2) // 2)
-            if (not even) and t >= 3:
-                lse((t - 3) // 2)
-                wpass(t - 3)
-                apass(t - 3)
-                wpass(t - 2)
-                apass(t - 2)
-            if (not even) and t < GROUPS:
-                xprep_c(t // 2)
-            if even and t >= 4:
-                mgs = prods((t - 4) // 2)
+                bk.extend(xprep_c_list(0))
+                bk.extend(xprep_c_list(1))
+            if t % 2 == 0:
+                pr = []
+                if 0 <= t - 4 < GROUPS:
+                    pr = prod_list((t - 4) // 2)
+                if 0 <= t - 6 < GROUPS:
+                    bk.append(lambda i=(t - 6) // 2: final_tot(i))
+                bk.extend(pr[0:2])
+                if 0 <= t - 6 < GROUPS:
+                    bk.append(lambda i=(t - 6) // 2: final_b(i))
+                bk.extend(pr[2:])
                 if t + 2 < GROUPS:
-                    xprep_a(t // 2 + 1)
-                mquant((t - 4) // 2, mgs)
-                final_a((t - 4) // 2)
-            elif even and t + 2 < GROUPS:
-                xprep_a(t // 2 + 1)
-        final_b(IMAGES - 1)
+                    bk.extend(xprep_a_list(t // 2 + 1))
+                if 0 <= t - 6 < GROUPS:
+                    bk.append(lambda i=(t - 6) // 2: final_c(i))
+            else:
+                qs = []
+                if 0 <= t - 5 < GROUPS:
+                    i = (t - 5) // 2
+                    qs = [
+                        lambda i=i: mquant(2 * i),
+                        lambda i=i: mquant(2 * i + 1),
+                        lambda i=i: final_mm(i),
+                        lambda i=i: final_a(i),
+                    ]
+                ws = []
+                if 0 <= t - 3 < GROUPS:
+                    i = (t - 3) // 2
+                    ws = lse_list(i) + w_list(2 * i) + w_list(2 * i + 1)
+                bk.extend(qs[0:3] + ws[0:1] + qs[3:4] + ws[1:])
+            if t == 1:
+                bk.extend(xprep_c_list(2))
+                bk.extend(xprep_c_list(3))
+            zipped(fr, bk)
+            if t == GROUPS:
+                hook(GROUPS, 7)

@@ -105,7 +105,7 @@ def tile_sralnet_pa_kernel(tc, x, centroids, out):
                     out=brep[:, s * P : (s + 1) * P],
                     in0=ones[:],
                     scalar1=bcol[:, s : s + 1],
-                    scalar2=-100.0,
+                    scalar2=-200.0,
                     op0=ALU.mult,
                     op1=ALU.mult,
                 )
@@ -229,7 +229,7 @@ def tile_sralnet_pa_kernel(tc, x, centroids, out):
                     in_=zb[g][:, c * P : (c + 1) * P],
                     func=ACTF.Exp,
                     bias=nmk[i][:, hh * 20 + c : hh * 20 + c + 1],
-                    scale=1.0,
+                    scale=0.5,
                     accum_out=rc[i][:, PIX + hh * 20 + c : PIX + hh * 20 + c + 1],
                 )
 
@@ -258,7 +258,7 @@ def tile_sralnet_pa_kernel(tc, x, centroids, out):
                     start=False,
                     stop=True,
                 )
-            nc.scalar.activation(out=e2s[g][:, s * 512 : (s + 1) * 512], in_=dt[:], func=ACTF.Exp)
+            nc.scalar.activation(out=e2s[g][:, s * 512 : (s + 1) * 512], in_=dt[:], func=ACTF.Exp, scale=0.5)
 
         def rpart(g):
             e2 = e2s[g]
@@ -317,9 +317,17 @@ def tile_sralnet_pa_kernel(tc, x, centroids, out):
             msg = msx[i][:, hh * 512 : (hh + 1) * 512]
             nmsg = nmp.tile([P, 512], F32, name="nmsg", tag="nms")
             nms[g] = nmsg
+            nmk2 = nmp.tile([P, 20], F32, name="nmk2", tag="nmk2")
 
             def v1(t):
-                nc.vector.tensor_tensor(out=zv[:, t, 0:512], in0=zm[4 * g + t][:], in1=bb[:, 0:512], op=ALU.add)
+                nc.vector.scalar_tensor_tensor(
+                    out=zv[:, t, 0:512],
+                    in0=zm[4 * g + t][:],
+                    scalar=2.0,
+                    in1=bb[:, 0:512],
+                    op0=ALU.mult,
+                    op1=ALU.add,
+                )
 
             def f0():
                 v1(0)
@@ -339,11 +347,13 @@ def tile_sralnet_pa_kernel(tc, x, centroids, out):
                 hook(g, 3)
 
             def f4():
-                nc.vector.tensor_tensor(
+                nc.vector.scalar_tensor_tensor(
                     out=zv[:, :, 512:640],
                     in0=z4[g][:].rearrange("p (t k) -> p t k", t=4),
+                    scalar=2.0,
                     in1=bb[:, 512:640].unsqueeze(1).to_broadcast([P, 4, P]),
-                    op=ALU.add,
+                    op0=ALU.mult,
+                    op1=ALU.add,
                 )
                 mm1(4 * g + 4)
                 mm1(4 * g + 5)
@@ -356,7 +366,7 @@ def tile_sralnet_pa_kernel(tc, x, centroids, out):
 
             def f6():
                 nc.vector.tensor_reduce(
-                    out=nmk[i][:, hh * 20 : hh * 20 + 20],
+                    out=nmk2[:],
                     in_=zbg[:].rearrange("p (c k) -> p c k", k=P),
                     axis=AX.X,
                     op=ALU.max,
@@ -376,11 +386,23 @@ def tile_sralnet_pa_kernel(tc, x, centroids, out):
             def f9():
                 nc.vector.tensor_scalar(out=nmsg[:], in0=msg, scalar1=-1.0, scalar2=None, op0=ALU.mult)
 
-            return [f0, f1, f2, f3, f4, f5, f6, f7, f8, f9]
+            def f10():
+                nc.vector.tensor_scalar(
+                    out=nmk[i][:, hh * 20 : hh * 20 + 20], in0=nmk2[:], scalar1=0.5, scalar2=None, op0=ALU.mult
+                )
+
+            return [f0, f1, f2, f3, f4, f5, f6, f7, f8, f10, f9]
 
         def lse_list(i):
             def l0():
-                nc.vector.tensor_tensor(out=rc[i][:, 0:PIX], in0=rc[i][:, 0:PIX], in1=msx[i][:], op=ALU.add)
+                nc.vector.scalar_tensor_tensor(
+                    out=rc[i][:, 0:PIX],
+                    in0=msx[i][:],
+                    scalar=0.5,
+                    in1=rc[i][:, 0:PIX],
+                    op0=ALU.mult,
+                    op1=ALU.add,
+                )
 
             def l1():
                 beta_i = img.tile([P, 40], F32, name="beta_i", tag="beta")
@@ -409,19 +431,16 @@ def tile_sralnet_pa_kernel(tc, x, centroids, out):
             zv = zb[g][:].rearrange("p (t m) -> p t m", t=4)
             lv = rc[i][:, hh * 512 : (hh + 1) * 512].rearrange("p (t k) -> p t k", t=4)
 
-            def wone(s):
-                nc.vector.scalar_tensor_tensor(
-                    out=zv[:, :, s * P : (s + 1) * P],
-                    in0=zv[:, :, s * P : (s + 1) * P],
-                    scalar=2.0,
-                    in1=lv,
-                    op0=ALU.mult,
-                    op1=ALU.subtract,
-                )
-                if s == S5 - 1:
-                    apass(g)
+            def wall():
+                for s in range(S5):
+                    nc.gpsimd.tensor_tensor(
+                        out=zv[:, :, s * P : (s + 1) * P],
+                        in0=zv[:, :, s * P : (s + 1) * P],
+                        in1=lv,
+                        op=ALU.subtract,
+                    )
 
-            return [lambda s=s: wone(s) for s in range(S5)]
+            return [wall]
 
         mgs = {}
 
@@ -594,7 +613,10 @@ def tile_sralnet_pa_kernel(tc, x, centroids, out):
                 if 0 <= t - 3 < GROUPS:
                     i = (t - 3) // 2
                     ws = lse_list(i) + w_list(2 * i) + w_list(2 * i + 1)
-                bk.extend(qs[0:3] + ws[0:1] + qs[3:4] + ws[1:])
+                    aps = [lambda i=i: apass(2 * i), lambda i=i: apass(2 * i + 1)]
+                else:
+                    aps = []
+                bk.extend(ws + aps[0:1] + qs + aps[1:2])
             if t == 1:
                 bk.extend(xprep_c_list(2))
                 bk.extend(xprep_c_list(3))

@@ -33,12 +33,11 @@ def tile_sralnet_pa_kernel(tc, x, centroids, out):
         xgp = ctx.enter_context(tc.tile_pool(name="xgp", bufs=1))
         xq1 = ctx.enter_context(tc.tile_pool(name="xq1", bufs=2))
         xq2 = ctx.enter_context(tc.tile_pool(name="xq2", bufs=4))
-        zbp = ctx.enter_context(tc.tile_pool(name="zbp", bufs=5))
+        zbp = ctx.enter_context(tc.tile_pool(name="zbp", bufs=3))
         dp = ctx.enter_context(tc.tile_pool(name="dp", bufs=1))
         tmp = ctx.enter_context(tc.tile_pool(name="tmp", bufs=1))
-        nmp = ctx.enter_context(tc.tile_pool(name="nmp", bufs=2))
         img = ctx.enter_context(tc.tile_pool(name="img", bufs=2))
-        mul = ctx.enter_context(tc.tile_pool(name="mul", bufs=4))
+        mul = ctx.enter_context(tc.tile_pool(name="mul", bufs=2))
         fin = ctx.enter_context(tc.tile_pool(name="fin", bufs=2))
         pzm = ctx.enter_context(tc.psum_pool(name="pzm", bufs=3))
         pz4 = ctx.enter_context(tc.psum_pool(name="pz4", bufs=1))
@@ -74,7 +73,7 @@ def tile_sralnet_pa_kernel(tc, x, centroids, out):
         cenw = cen[:].bitcast(F32).rearrange("p (s q u) -> p s u q", s=S5, u=2)
         wg = const.tile([P, 4 * M], BF16, name="wg", align_bytes=64)
         for s in range(S5):
-            wt = pmisc.tile([P, 256], F32, name="wt", tag="misc")
+            wt = pdt.tile([P, 256], F32, name="wt", tag="dt")
             for u in range(2):
                 nc.tensor.transpose(wt[:, u * P : (u + 1) * P], cenw[:, s, u], ident[:])
             nc.vector.tensor_scalar(
@@ -92,7 +91,11 @@ def tile_sralnet_pa_kernel(tc, x, centroids, out):
         n2 = const.tile([P, 8], F32, name="n2")
         for s in range(S5):
             nc.scalar.activation(
-                out=junk_w[:], in_=cen[:, s * CH : (s + 1) * CH], func=ACTF.Square, accum_out=n2[:, s : s + 1]
+                out=junk_w[:],
+                in_=cen[:, s * CH : (s + 1) * CH],
+                func=ACTF.Square,
+                scale=100.0,
+                accum_out=n2[:, s : s + 1],
             )
         bcol = const.tile([P, 8], F32, name="bcol")
         nc.gpsimd.tensor_tensor(out=bcol[:, 0:S5], in0=n2[:, 0:S5], in1=expo[:, 0:S5], op=ALU.pow)
@@ -101,21 +104,16 @@ def tile_sralnet_pa_kernel(tc, x, centroids, out):
 
         def bias_spread():
             for s in range(S5):
-                nc.vector.tensor_scalar(
-                    out=brep[:, s * P : (s + 1) * P],
-                    in0=ones[:],
-                    scalar1=bcol[:, s : s + 1],
-                    scalar2=-200.0,
-                    op0=ALU.mult,
-                    op1=ALU.mult,
+                nc.scalar.activation(
+                    out=brep[:, s * P : (s + 1) * P], in_=ones[:], func=ACTF.Copy, scale=bcol[:, s : s + 1]
                 )
             bt0 = pmisc.tile([P, 512], F32, name="bt0", tag="misc")
             for s in range(4):
                 nc.tensor.transpose(bt0[:, s * P : (s + 1) * P], brep[:, s * P : (s + 1) * P], ident[:])
-            nc.vector.tensor_copy(out=bb[:, 0:512], in_=bt0[:])
+            nc.scalar.copy(out=bb[:, 0:512], in_=bt0[:])
             bt1 = pmisc.tile([P, P], F32, name="bt1", tag="misc")
             nc.tensor.transpose(bt1[:], brep[:, 512:640], ident[:])
-            nc.vector.tensor_copy(out=bb[:, 512:640], in_=bt1[:])
+            nc.scalar.copy(out=bb[:, 512:640], in_=bt1[:])
 
         xc1 = {}
         xsc1 = {}
@@ -124,22 +122,33 @@ def tile_sralnet_pa_kernel(tc, x, centroids, out):
 
         xg2s = {}
 
-        def xprep_a_list(n):
+        def xprep_a_list(n, halves):
             xg1 = xgp.tile([P, 4 * PIX], BF16, name="xg1", tag="xg1", align_bytes=64)
-            src = xs[n][:].rearrange("p (j a r e) -> p e a r j", j=4, a=4, r=P, e=2)
-            dst = xg1[:].rearrange("p (a e r j) -> p e a r j", a=4, e=2, r=P, j=4)
             c1 = xq1.tile([P, PIX], U32, name="c1", tag="c1", align_bytes=64)
             s1 = xq1.tile([P, PIX], U8, name="s1", tag="s1", align_bytes=64)
             xc1[n] = c1
             xsc1[n] = s1
+            a = 4 // halves
+            src = xs[n][:].rearrange("p (j h a r e) -> p h e a r j", j=4, h=halves, a=a, r=P, e=2)
+            dst = xg1[:].rearrange("p (h a e r j) -> p h e a r j", h=halves, a=a, e=2, r=P, j=4)
+            wid = PIX // halves
 
-            def regroup(e):
-                nc.vector.tensor_copy(out=dst[:, e], in_=src[:, e])
+            def regroup(hf, e):
+                nc.vector.tensor_copy(out=dst[:, hf, e], in_=src[:, hf, e])
 
-            def quant():
-                nc.vector.quantize_mx(out=c1[:].bitcast(FP8X4), scales=s1[:], in_=xg1[:])
+            def quant(hf):
+                nc.vector.quantize_mx(
+                    out=c1[:, hf * wid : (hf + 1) * wid].bitcast(FP8X4),
+                    scales=s1[:, hf * wid : (hf + 1) * wid],
+                    in_=xg1[:, hf * 4 * wid : (hf + 1) * 4 * wid],
+                )
 
-            return [lambda: regroup(0), lambda: regroup(1), quant]
+            fns = []
+            for hf in range(halves):
+                fns.append(lambda hf=hf: regroup(hf, 0))
+                fns.append(lambda hf=hf: regroup(hf, 1))
+                fns.append(lambda hf=hf: quant(hf))
+            return fns
 
         def xprep_b(n):
             xw = xs[n][:].bitcast(F32).rearrange("p (j a w) -> p j a w", j=4, a=4, w=P)
@@ -209,6 +218,7 @@ def tile_sralnet_pa_kernel(tc, x, centroids, out):
             )
 
         zb = {}
+        zbim = {}
         nmk = {}
         msx = {}
         nms = {}
@@ -229,7 +239,7 @@ def tile_sralnet_pa_kernel(tc, x, centroids, out):
                     in_=zb[g][:, c * P : (c + 1) * P],
                     func=ACTF.Exp,
                     bias=nmk[i][:, hh * 20 + c : hh * 20 + c + 1],
-                    scale=0.5,
+                    scale=1.0,
                     accum_out=rc[i][:, PIX + hh * 20 + c : PIX + hh * 20 + c + 1],
                 )
 
@@ -258,7 +268,7 @@ def tile_sralnet_pa_kernel(tc, x, centroids, out):
                     start=False,
                     stop=True,
                 )
-            nc.scalar.activation(out=e2s[g][:, s * 512 : (s + 1) * 512], in_=dt[:], func=ACTF.Exp, scale=0.5)
+            nc.scalar.activation(out=e2s[g][:, s * 512 : (s + 1) * 512], in_=dt[:], func=ACTF.Exp)
 
         def rpart(g):
             e2 = e2s[g]
@@ -307,27 +317,22 @@ def tile_sralnet_pa_kernel(tc, x, centroids, out):
                 nmk[i] = nmk_i
                 msx[i] = msx_i
                 rc[i] = rc_i
-            zbg = zbp.tile([P, 4 * M], F32, name="zbg", tag="zb")
+                zbi = zbp.tile([P, 8 * M], F32, name="zbi", tag="zb")
+                zbim[i] = zbi
+            zbg = zbim[i][:, hh * 4 * M : (hh + 1) * 4 * M]
             zb[g] = zbg
-            zv = zbg[:].rearrange("p (t m) -> p t m", t=4)
+            zv = zbg.rearrange("p (t m) -> p t m", t=4)
+            nmsg = msx[i][:, hh * 512 : (hh + 1) * 512]
+            nms[g] = nmsg
             t1 = tmp.tile([P, 1024], F32, name="t1", tag="t1")
             t1v = t1[:].rearrange("p (t m) -> p t m", t=4)
             t2 = tmp.tile([P, 512], F32, name="t2", tag="t2")
             t2v = t2[:].rearrange("p (t k) -> p t k", t=4)
-            msg = msx[i][:, hh * 512 : (hh + 1) * 512]
-            nmsg = nmp.tile([P, 512], F32, name="nmsg", tag="nms")
-            nms[g] = nmsg
-            nmk2 = nmp.tile([P, 20], F32, name="nmk2", tag="nmk2")
+            t3 = tmp.tile([P, 512], F32, name="t3", tag="t3")
+            t3v = t3[:].rearrange("p (t k) -> p t k", t=4)
 
             def v1(t):
-                nc.vector.scalar_tensor_tensor(
-                    out=zv[:, t, 0:512],
-                    in0=zm[4 * g + t][:],
-                    scalar=2.0,
-                    in1=bb[:, 0:512],
-                    op0=ALU.mult,
-                    op1=ALU.add,
-                )
+                nc.vector.tensor_tensor(out=zv[:, t, 0:512], in0=zm[4 * g + t][:], in1=bb[:, 0:512], op=ALU.subtract)
 
             def f0():
                 v1(0)
@@ -347,13 +352,11 @@ def tile_sralnet_pa_kernel(tc, x, centroids, out):
                 hook(g, 3)
 
             def f4():
-                nc.vector.scalar_tensor_tensor(
+                nc.vector.tensor_tensor(
                     out=zv[:, :, 512:640],
                     in0=z4[g][:].rearrange("p (t k) -> p t k", t=4),
-                    scalar=2.0,
                     in1=bb[:, 512:640].unsqueeze(1).to_broadcast([P, 4, P]),
-                    op0=ALU.mult,
-                    op1=ALU.add,
+                    op=ALU.subtract,
                 )
                 mm1(4 * g + 4)
                 mm1(4 * g + 5)
@@ -366,8 +369,8 @@ def tile_sralnet_pa_kernel(tc, x, centroids, out):
 
             def f6():
                 nc.vector.tensor_reduce(
-                    out=nmk2[:],
-                    in_=zbg[:].rearrange("p (c k) -> p c k", k=P),
+                    out=nmk[i][:, hh * 20 : hh * 20 + 20],
+                    in_=zbg.rearrange("p (c k) -> p c k", k=P),
                     axis=AX.X,
                     op=ALU.max,
                     negate=True,
@@ -379,30 +382,16 @@ def tile_sralnet_pa_kernel(tc, x, centroids, out):
                 hook(g, 7)
 
             def f8():
-                nc.vector.tensor_tensor(
-                    out=msg.rearrange("p (t k) -> p t k", t=4), in0=t2v, in1=zv[:, :, 512:640], op=ALU.max
-                )
+                nc.vector.tensor_tensor(out=t3v, in0=t2v, in1=zv[:, :, 512:640], op=ALU.max)
 
             def f9():
-                nc.vector.tensor_scalar(out=nmsg[:], in0=msg, scalar1=-1.0, scalar2=None, op0=ALU.mult)
+                nc.vector.tensor_scalar(out=nmsg, in0=t3[:], scalar1=-1.0, scalar2=None, op0=ALU.mult)
 
-            def f10():
-                nc.vector.tensor_scalar(
-                    out=nmk[i][:, hh * 20 : hh * 20 + 20], in0=nmk2[:], scalar1=0.5, scalar2=None, op0=ALU.mult
-                )
-
-            return [f0, f1, f2, f3, f4, f5, f6, f7, f8, f10, f9]
+            return [f0, f1, f2, f3, f4, f5, f6, f7, f8, f9]
 
         def lse_list(i):
             def l0():
-                nc.vector.scalar_tensor_tensor(
-                    out=rc[i][:, 0:PIX],
-                    in0=msx[i][:],
-                    scalar=0.5,
-                    in1=rc[i][:, 0:PIX],
-                    op0=ALU.mult,
-                    op1=ALU.add,
-                )
+                nc.vector.tensor_tensor(out=rc[i][:, 0:PIX], in0=rc[i][:, 0:PIX], in1=msx[i][:], op=ALU.subtract)
 
             def l1():
                 beta_i = img.tile([P, 40], F32, name="beta_i", tag="beta")
@@ -411,48 +400,42 @@ def tile_sralnet_pa_kernel(tc, x, centroids, out):
 
             return [l0, l1]
 
-        def apass(g):
-            i = g // 2
-            hh = g % 2
-            for s in range(S5):
-                for t in range(4):
-                    c = t * S5 + s
-                    nc.scalar.activation(
-                        out=zb[g][:, c * P : (c + 1) * P],
-                        in_=zb[g][:, c * P : (c + 1) * P],
-                        func=ACTF.Exp,
-                        bias=beta[i][:, hh * 20 + c : hh * 20 + c + 1],
-                        scale=1.0,
-                    )
+        def apart(i, s):
+            for c8 in range(8):
+                c = c8 * S5 + s
+                nc.scalar.activation(
+                    out=zbim[i][:, c * P : (c + 1) * P],
+                    in_=zbim[i][:, c * P : (c + 1) * P],
+                    func=ACTF.Exp,
+                    bias=beta[i][:, c : c + 1],
+                    scale=1.0,
+                )
 
-        def w_list(g):
-            i = g // 2
-            hh = g % 2
-            zv = zb[g][:].rearrange("p (t m) -> p t m", t=4)
-            lv = rc[i][:, hh * 512 : (hh + 1) * 512].rearrange("p (t k) -> p t k", t=4)
+        def w_list(i):
+            zv = zbim[i][:].rearrange("p (t m) -> p t m", t=8)
+            lv = rc[i][:, 0:PIX].rearrange("p (t k) -> p t k", t=8)
 
-            def wall():
-                for s in range(S5):
-                    nc.gpsimd.tensor_tensor(
-                        out=zv[:, :, s * P : (s + 1) * P],
-                        in0=zv[:, :, s * P : (s + 1) * P],
-                        in1=lv,
-                        op=ALU.subtract,
-                    )
+            def wone(s):
+                nc.vector.scalar_tensor_tensor(
+                    out=zv[:, :, s * P : (s + 1) * P],
+                    in0=zv[:, :, s * P : (s + 1) * P],
+                    scalar=2.0,
+                    in1=lv,
+                    op0=ALU.mult,
+                    op1=ALU.subtract,
+                )
+                apart(i, s)
 
-            return [wall]
+            return [lambda s=s: wone(s) for s in range(S5)]
 
         mgs = {}
 
         def prod_list(i):
-            pair = (2 * i, 2 * i + 1)
-            for g in pair:
-                accg = mul.tile([P, 512], F32, name="accg", tag="acc")
-                acc[g] = accg
+            acci = mul.tile([P, PIX], F32, name="acci", tag="acc")
+            zv = zbim[i][:].rearrange("p (t m) -> p t m", t=8)
+            av = acci[:].rearrange("p (t k) -> p t k", t=8)
 
-            def pone(s, g):
-                zv = zb[g][:].rearrange("p (t m) -> p t m", t=4)
-                av = acc[g][:].rearrange("p (t k) -> p t k", t=4)
+            def pone(s):
                 if s == 0:
                     nc.vector.tensor_scalar(out=av, in0=zv[:, :, 0:P], scalar1=1.0, scalar2=None, op0=ALU.add)
                 else:
@@ -465,49 +448,46 @@ def tile_sralnet_pa_kernel(tc, x, centroids, out):
                         op1=ALU.mult,
                     )
                 if s == S5 - 1:
-                    after(g)
+                    after()
 
-            def after(g):
-                if g == pair[0]:
-                    msp = pmisc.tile([P, 4], F32, name="msp", tag="misc")
-                    msum[i] = msp
-                mg = mul.tile([P, 512], BF16, name="mg", tag="mg", align_bytes=64)
-                mgs[g] = mg
+            def after():
+                msp = pmisc.tile([P, 4], F32, name="msp", tag="misc")
+                msum[i] = msp
+                mg = mul.tile([P, PIX], BF16, name="mg", tag="mg", align_bytes=64)
+                mgs[i] = mg
                 nc.scalar.copy(
-                    out=mg[:].rearrange("p (k t) -> p k t", t=4),
-                    in_=acc[g][:].rearrange("p (t k) -> p k t", t=4),
+                    out=mg[:].rearrange("p (h k t) -> p h k t", h=2, t=4),
+                    in_=acci[:].rearrange("p (h t k) -> p h k t", h=2, t=4),
                 )
-                for t in range(4):
+                for t in range(8):
                     nc.tensor.matmul(
-                        out=msum[i][:, 0:2],
-                        lhsT=acc[g][:, t * P : (t + 1) * P],
+                        out=msp[:, 0:2],
+                        lhsT=acci[:, t * P : (t + 1) * P],
                         rhs=ones[:, 0:2],
-                        start=(g == pair[0] and t == 0),
-                        stop=(g == pair[1] and t == 3),
+                        start=(t == 0),
+                        stop=(t == 7),
                     )
 
-            return [lambda s=s, g=g: pone(s, g) for s in range(S5) for g in pair]
+            return [lambda s=s: pone(s) for s in range(S5)]
 
-        def mquant(g):
-            mc = mul.tile([P, P], U32, name="mc", tag="mc", align_bytes=64)
-            msc = mul.tile([P, P], U8, name="msc", tag="msc", align_bytes=64)
-            nc.vector.quantize_mx(out=mc[:].bitcast(FP8X4), scales=msc[:], in_=mgs[g][:])
-            mcod[g] = mc
-            mscl[g] = msc
+        def mquant(i):
+            mc = mul.tile([P, 2 * P], U32, name="mc", tag="mc", align_bytes=64)
+            msc = mul.tile([P, 2 * P], U8, name="msc", tag="msc", align_bytes=64)
+            nc.vector.quantize_mx(out=mc[:].bitcast(FP8X4), scales=msc[:], in_=mgs[i][:])
+            mcod[i] = mc
+            mscl[i] = msc
 
         fst = {}
-
         vts = {}
 
         def final_mm(i):
             v = prb.tile([P, CH], F32, name="v", tag="rb")
             vts[i] = v
             for hh in range(2):
-                g = 2 * i + hh
                 nc.tensor.matmul_mx(
                     out=v[:],
-                    lhsT=mcod[g][:].bitcast(FP8X4),
-                    lhsT_scale=mscl[g][:],
+                    lhsT=mcod[i][:, hh * P : (hh + 1) * P].bitcast(FP8X4),
+                    lhsT_scale=mscl[i][:, hh * P : (hh + 1) * P],
                     rhs=xc2[i][:, hh * 512 : (hh + 1) * 512].bitcast(FP8X4),
                     rhs_scale=xsc2[i][:, hh * 512 : (hh + 1) * 512],
                     start=(hh == 0),
@@ -567,13 +547,14 @@ def tile_sralnet_pa_kernel(tc, x, centroids, out):
                 if j < len(b):
                     b[j]()
 
-        for fn in xprep_a_list(0):
+        first = xprep_a_list(0, 2)
+        for fn in first[0:3]:
             fn()
-        xprep_b(0)
         bias_spread()
         mm1(0)
         mm1(1)
         mm1(2)
+        xprep_b(0)
         xprep_b(1)
         for t in range(GROUPS + 5):
             fr = []
@@ -583,20 +564,19 @@ def tile_sralnet_pa_kernel(tc, x, centroids, out):
                 fr = [lambda j=j: hook(GROUPS, j) for j in range(7)]
             bk = []
             if t == 0:
-                bk.extend(xprep_c_list(0))
-                bk.extend(xprep_c_list(1))
+                bk.extend(first[3:6])
             if t % 2 == 0:
                 pr = []
                 if 0 <= t - 4 < GROUPS:
                     pr = prod_list((t - 4) // 2)
                 if 0 <= t - 6 < GROUPS:
                     bk.append(lambda i=(t - 6) // 2: final_tot(i))
-                bk.extend(pr[0:2])
+                bk.extend(pr[0:1])
                 if 0 <= t - 6 < GROUPS:
                     bk.append(lambda i=(t - 6) // 2: final_b(i))
-                bk.extend(pr[2:])
+                bk.extend(pr[1:])
                 if t + 2 < GROUPS:
-                    bk.extend(xprep_a_list(t // 2 + 1))
+                    bk.extend(xprep_a_list(t // 2 + 1, 1))
                 if 0 <= t - 6 < GROUPS:
                     bk.append(lambda i=(t - 6) // 2: final_c(i))
             else:
@@ -604,19 +584,18 @@ def tile_sralnet_pa_kernel(tc, x, centroids, out):
                 if 0 <= t - 5 < GROUPS:
                     i = (t - 5) // 2
                     qs = [
-                        lambda i=i: mquant(2 * i),
-                        lambda i=i: mquant(2 * i + 1),
+                        lambda i=i: mquant(i),
                         lambda i=i: final_mm(i),
                         lambda i=i: final_a(i),
                     ]
                 ws = []
                 if 0 <= t - 3 < GROUPS:
                     i = (t - 3) // 2
-                    ws = lse_list(i) + w_list(2 * i) + w_list(2 * i + 1)
-                    aps = [lambda i=i: apass(2 * i), lambda i=i: apass(2 * i + 1)]
-                else:
-                    aps = []
-                bk.extend(ws + aps[0:1] + qs + aps[1:2])
+                    ws = lse_list(i) + w_list(i)
+                bk.extend(qs[0:2] + ws[0:1] + qs[2:3] + ws[1:])
+            if t == 0:
+                bk.extend(xprep_c_list(0))
+                bk.extend(xprep_c_list(1))
             if t == 1:
                 bk.extend(xprep_c_list(2))
                 bk.extend(xprep_c_list(3))

@@ -33,11 +33,12 @@ def tile_sralnet_pa_kernel(tc, x, centroids, out):
         xgp = ctx.enter_context(tc.tile_pool(name="xgp", bufs=1))
         xq1 = ctx.enter_context(tc.tile_pool(name="xq1", bufs=2))
         xq2 = ctx.enter_context(tc.tile_pool(name="xq2", bufs=4))
-        zbp = ctx.enter_context(tc.tile_pool(name="zbp", bufs=3))
+        zbp = ctx.enter_context(tc.tile_pool(name="zbp", bufs=5))
         dp = ctx.enter_context(tc.tile_pool(name="dp", bufs=1))
         tmp = ctx.enter_context(tc.tile_pool(name="tmp", bufs=1))
+        nmp = ctx.enter_context(tc.tile_pool(name="nmp", bufs=2))
         img = ctx.enter_context(tc.tile_pool(name="img", bufs=2))
-        mul = ctx.enter_context(tc.tile_pool(name="mul", bufs=2))
+        mul = ctx.enter_context(tc.tile_pool(name="mul", bufs=4))
         fin = ctx.enter_context(tc.tile_pool(name="fin", bufs=2))
         pzm = ctx.enter_context(tc.psum_pool(name="pzm", bufs=3))
         pz4 = ctx.enter_context(tc.psum_pool(name="pz4", bufs=1))
@@ -73,7 +74,7 @@ def tile_sralnet_pa_kernel(tc, x, centroids, out):
         cenw = cen[:].bitcast(F32).rearrange("p (s q u) -> p s u q", s=S5, u=2)
         wg = const.tile([P, 4 * M], BF16, name="wg", align_bytes=64)
         for s in range(S5):
-            wt = pdt.tile([P, 256], F32, name="wt", tag="dt")
+            wt = pmisc.tile([P, 256], F32, name="wt", tag="misc")
             for u in range(2):
                 nc.tensor.transpose(wt[:, u * P : (u + 1) * P], cenw[:, s, u], ident[:])
             nc.vector.tensor_scalar(
@@ -91,11 +92,7 @@ def tile_sralnet_pa_kernel(tc, x, centroids, out):
         n2 = const.tile([P, 8], F32, name="n2")
         for s in range(S5):
             nc.scalar.activation(
-                out=junk_w[:],
-                in_=cen[:, s * CH : (s + 1) * CH],
-                func=ACTF.Square,
-                scale=100.0,
-                accum_out=n2[:, s : s + 1],
+                out=junk_w[:], in_=cen[:, s * CH : (s + 1) * CH], func=ACTF.Square, accum_out=n2[:, s : s + 1]
             )
         bcol = const.tile([P, 8], F32, name="bcol")
         nc.gpsimd.tensor_tensor(out=bcol[:, 0:S5], in0=n2[:, 0:S5], in1=expo[:, 0:S5], op=ALU.pow)
@@ -104,16 +101,21 @@ def tile_sralnet_pa_kernel(tc, x, centroids, out):
 
         def bias_spread():
             for s in range(S5):
-                nc.scalar.activation(
-                    out=brep[:, s * P : (s + 1) * P], in_=ones[:], func=ACTF.Copy, scale=bcol[:, s : s + 1]
+                nc.vector.tensor_scalar(
+                    out=brep[:, s * P : (s + 1) * P],
+                    in0=ones[:],
+                    scalar1=bcol[:, s : s + 1],
+                    scalar2=-100.0,
+                    op0=ALU.mult,
+                    op1=ALU.mult,
                 )
             bt0 = pmisc.tile([P, 512], F32, name="bt0", tag="misc")
             for s in range(4):
                 nc.tensor.transpose(bt0[:, s * P : (s + 1) * P], brep[:, s * P : (s + 1) * P], ident[:])
-            nc.scalar.copy(out=bb[:, 0:512], in_=bt0[:])
+            nc.vector.tensor_copy(out=bb[:, 0:512], in_=bt0[:])
             bt1 = pmisc.tile([P, P], F32, name="bt1", tag="misc")
             nc.tensor.transpose(bt1[:], brep[:, 512:640], ident[:])
-            nc.scalar.copy(out=bb[:, 512:640], in_=bt1[:])
+            nc.vector.tensor_copy(out=bb[:, 512:640], in_=bt1[:])
 
         xc1 = {}
         xsc1 = {}
@@ -122,33 +124,22 @@ def tile_sralnet_pa_kernel(tc, x, centroids, out):
 
         xg2s = {}
 
-        def xprep_a_list(n, halves):
+        def xprep_a_list(n):
             xg1 = xgp.tile([P, 4 * PIX], BF16, name="xg1", tag="xg1", align_bytes=64)
+            src = xs[n][:].rearrange("p (j a r e) -> p e a r j", j=4, a=4, r=P, e=2)
+            dst = xg1[:].rearrange("p (a e r j) -> p e a r j", a=4, e=2, r=P, j=4)
             c1 = xq1.tile([P, PIX], U32, name="c1", tag="c1", align_bytes=64)
             s1 = xq1.tile([P, PIX], U8, name="s1", tag="s1", align_bytes=64)
             xc1[n] = c1
             xsc1[n] = s1
-            a = 4 // halves
-            src = xs[n][:].rearrange("p (j h a r e) -> p h e a r j", j=4, h=halves, a=a, r=P, e=2)
-            dst = xg1[:].rearrange("p (h a e r j) -> p h e a r j", h=halves, a=a, e=2, r=P, j=4)
-            wid = PIX // halves
 
-            def regroup(hf, e):
-                nc.vector.tensor_copy(out=dst[:, hf, e], in_=src[:, hf, e])
+            def regroup(e):
+                nc.vector.tensor_copy(out=dst[:, e], in_=src[:, e])
 
-            def quant(hf):
-                nc.vector.quantize_mx(
-                    out=c1[:, hf * wid : (hf + 1) * wid].bitcast(FP8X4),
-                    scales=s1[:, hf * wid : (hf + 1) * wid],
-                    in_=xg1[:, hf * 4 * wid : (hf + 1) * 4 * wid],
-                )
+            def quant():
+                nc.vector.quantize_mx(out=c1[:].bitcast(FP8X4), scales=s1[:], in_=xg1[:])
 
-            fns = []
-            for hf in range(halves):
-                fns.append(lambda hf=hf: regroup(hf, 0))
-                fns.append(lambda hf=hf: regroup(hf, 1))
-                fns.append(lambda hf=hf: quant(hf))
-            return fns
+            return [lambda: regroup(0), lambda: regroup(1), quant]
 
         def xprep_b(n):
             xw = xs[n][:].bitcast(F32).rearrange("p (j a w) -> p j a w", j=4, a=4, w=P)
@@ -218,7 +209,6 @@ def tile_sralnet_pa_kernel(tc, x, centroids, out):
             )
 
         zb = {}
-        zbim = {}
         nmk = {}
         msx = {}
         nms = {}
@@ -317,22 +307,19 @@ def tile_sralnet_pa_kernel(tc, x, centroids, out):
                 nmk[i] = nmk_i
                 msx[i] = msx_i
                 rc[i] = rc_i
-                zbi = zbp.tile([P, 8 * M], F32, name="zbi", tag="zb")
-                zbim[i] = zbi
-            zbg = zbim[i][:, hh * 4 * M : (hh + 1) * 4 * M]
+            zbg = zbp.tile([P, 4 * M], F32, name="zbg", tag="zb")
             zb[g] = zbg
-            zv = zbg.rearrange("p (t m) -> p t m", t=4)
-            nmsg = msx[i][:, hh * 512 : (hh + 1) * 512]
-            nms[g] = nmsg
+            zv = zbg[:].rearrange("p (t m) -> p t m", t=4)
             t1 = tmp.tile([P, 1024], F32, name="t1", tag="t1")
             t1v = t1[:].rearrange("p (t m) -> p t m", t=4)
             t2 = tmp.tile([P, 512], F32, name="t2", tag="t2")
             t2v = t2[:].rearrange("p (t k) -> p t k", t=4)
-            t3 = tmp.tile([P, 512], F32, name="t3", tag="t3")
-            t3v = t3[:].rearrange("p (t k) -> p t k", t=4)
+            msg = msx[i][:, hh * 512 : (hh + 1) * 512]
+            nmsg = nmp.tile([P, 512], F32, name="nmsg", tag="nms")
+            nms[g] = nmsg
 
             def v1(t):
-                nc.vector.tensor_tensor(out=zv[:, t, 0:512], in0=zm[4 * g + t][:], in1=bb[:, 0:512], op=ALU.subtract)
+                nc.vector.tensor_tensor(out=zv[:, t, 0:512], in0=zm[4 * g + t][:], in1=bb[:, 0:512], op=ALU.add)
 
             def f0():
                 v1(0)
@@ -356,7 +343,7 @@ def tile_sralnet_pa_kernel(tc, x, centroids, out):
                     out=zv[:, :, 512:640],
                     in0=z4[g][:].rearrange("p (t k) -> p t k", t=4),
                     in1=bb[:, 512:640].unsqueeze(1).to_broadcast([P, 4, P]),
-                    op=ALU.subtract,
+                    op=ALU.add,
                 )
                 mm1(4 * g + 4)
                 mm1(4 * g + 5)
@@ -370,7 +357,7 @@ def tile_sralnet_pa_kernel(tc, x, centroids, out):
             def f6():
                 nc.vector.tensor_reduce(
                     out=nmk[i][:, hh * 20 : hh * 20 + 20],
-                    in_=zbg.rearrange("p (c k) -> p c k", k=P),
+                    in_=zbg[:].rearrange("p (c k) -> p c k", k=P),
                     axis=AX.X,
                     op=ALU.max,
                     negate=True,
@@ -382,16 +369,18 @@ def tile_sralnet_pa_kernel(tc, x, centroids, out):
                 hook(g, 7)
 
             def f8():
-                nc.vector.tensor_tensor(out=t3v, in0=t2v, in1=zv[:, :, 512:640], op=ALU.max)
+                nc.vector.tensor_tensor(
+                    out=msg.rearrange("p (t k) -> p t k", t=4), in0=t2v, in1=zv[:, :, 512:640], op=ALU.max
+                )
 
             def f9():
-                nc.vector.tensor_scalar(out=nmsg, in0=t3[:], scalar1=-1.0, scalar2=None, op0=ALU.mult)
+                nc.gpsimd.tensor_scalar(out=nmsg[:], in0=msg, scalar1=-1.0, scalar2=0.0, op0=ALU.mult, op1=ALU.add)
 
             return [f0, f1, f2, f3, f4, f5, f6, f7, f8, f9]
 
         def lse_list(i):
             def l0():
-                nc.vector.tensor_tensor(out=rc[i][:, 0:PIX], in0=rc[i][:, 0:PIX], in1=msx[i][:], op=ALU.subtract)
+                nc.vector.tensor_tensor(out=rc[i][:, 0:PIX], in0=rc[i][:, 0:PIX], in1=msx[i][:], op=ALU.add)
 
             def l1():
                 beta_i = img.tile([P, 40], F32, name="beta_i", tag="beta")
@@ -400,20 +389,25 @@ def tile_sralnet_pa_kernel(tc, x, centroids, out):
 
             return [l0, l1]
 
-        def apart(i, s):
-            for c8 in range(8):
-                c = c8 * S5 + s
-                nc.scalar.activation(
-                    out=zbim[i][:, c * P : (c + 1) * P],
-                    in_=zbim[i][:, c * P : (c + 1) * P],
-                    func=ACTF.Exp,
-                    bias=beta[i][:, c : c + 1],
-                    scale=1.0,
-                )
+        def apass(g):
+            i = g // 2
+            hh = g % 2
+            for s in range(S5):
+                for t in range(4):
+                    c = t * S5 + s
+                    nc.scalar.activation(
+                        out=zb[g][:, c * P : (c + 1) * P],
+                        in_=zb[g][:, c * P : (c + 1) * P],
+                        func=ACTF.Exp,
+                        bias=beta[i][:, hh * 20 + c : hh * 20 + c + 1],
+                        scale=1.0,
+                    )
 
-        def w_list(i):
-            zv = zbim[i][:].rearrange("p (t m) -> p t m", t=8)
-            lv = rc[i][:, 0:PIX].rearrange("p (t k) -> p t k", t=8)
+        def w_list(g):
+            i = g // 2
+            hh = g % 2
+            zv = zb[g][:].rearrange("p (t m) -> p t m", t=4)
+            lv = rc[i][:, hh * 512 : (hh + 1) * 512].rearrange("p (t k) -> p t k", t=4)
 
             def wone(s):
                 nc.vector.scalar_tensor_tensor(
@@ -424,18 +418,22 @@ def tile_sralnet_pa_kernel(tc, x, centroids, out):
                     op0=ALU.mult,
                     op1=ALU.subtract,
                 )
-                apart(i, s)
+                if s == S5 - 1:
+                    apass(g)
 
             return [lambda s=s: wone(s) for s in range(S5)]
 
         mgs = {}
 
         def prod_list(i):
-            acci = mul.tile([P, PIX], F32, name="acci", tag="acc")
-            zv = zbim[i][:].rearrange("p (t m) -> p t m", t=8)
-            av = acci[:].rearrange("p (t k) -> p t k", t=8)
+            pair = (2 * i, 2 * i + 1)
+            for g in pair:
+                accg = mul.tile([P, 512], F32, name="accg", tag="acc")
+                acc[g] = accg
 
-            def pone(s):
+            def pone(s, g):
+                zv = zb[g][:].rearrange("p (t m) -> p t m", t=4)
+                av = acc[g][:].rearrange("p (t k) -> p t k", t=4)
                 if s == 0:
                     nc.vector.tensor_scalar(out=av, in0=zv[:, :, 0:P], scalar1=1.0, scalar2=None, op0=ALU.add)
                 else:
@@ -448,46 +446,53 @@ def tile_sralnet_pa_kernel(tc, x, centroids, out):
                         op1=ALU.mult,
                     )
                 if s == S5 - 1:
-                    after()
+                    after(g)
 
-            def after():
-                msp = pmisc.tile([P, 4], F32, name="msp", tag="misc")
-                msum[i] = msp
-                mg = mul.tile([P, PIX], BF16, name="mg", tag="mg", align_bytes=64)
-                mgs[i] = mg
-                nc.scalar.copy(
-                    out=mg[:].rearrange("p (h k t) -> p h k t", h=2, t=4),
-                    in_=acci[:].rearrange("p (h t k) -> p h k t", h=2, t=4),
+            def after(g):
+                if g == pair[0]:
+                    msp = pmisc.tile([P, 4], F32, name="msp", tag="misc")
+                    msum[i] = msp
+                mg = mul.tile([P, 512], BF16, name="mg", tag="mg", align_bytes=64)
+                mgs[g] = mg
+                nc.gpsimd.tensor_scalar(
+                    out=mg[:].rearrange("p (k t) -> p k t", t=4),
+                    in0=acc[g][:].rearrange("p (t k) -> p k t", t=4),
+                    scalar1=1.0,
+                    scalar2=0.0,
+                    op0=ALU.mult,
+                    op1=ALU.add,
                 )
-                for t in range(8):
+                for t in range(4):
                     nc.tensor.matmul(
-                        out=msp[:, 0:2],
-                        lhsT=acci[:, t * P : (t + 1) * P],
+                        out=msum[i][:, 0:2],
+                        lhsT=acc[g][:, t * P : (t + 1) * P],
                         rhs=ones[:, 0:2],
-                        start=(t == 0),
-                        stop=(t == 7),
+                        start=(g == pair[0] and t == 0),
+                        stop=(g == pair[1] and t == 3),
                     )
 
-            return [lambda s=s: pone(s) for s in range(S5)]
+            return [lambda s=s, g=g: pone(s, g) for s in range(S5) for g in pair]
 
-        def mquant(i):
-            mc = mul.tile([P, 2 * P], U32, name="mc", tag="mc", align_bytes=64)
-            msc = mul.tile([P, 2 * P], U8, name="msc", tag="msc", align_bytes=64)
-            nc.vector.quantize_mx(out=mc[:].bitcast(FP8X4), scales=msc[:], in_=mgs[i][:])
-            mcod[i] = mc
-            mscl[i] = msc
+        def mquant(g):
+            mc = mul.tile([P, P], U32, name="mc", tag="mc", align_bytes=64)
+            msc = mul.tile([P, P], U8, name="msc", tag="msc", align_bytes=64)
+            nc.vector.quantize_mx(out=mc[:].bitcast(FP8X4), scales=msc[:], in_=mgs[g][:])
+            mcod[g] = mc
+            mscl[g] = msc
 
         fst = {}
+
         vts = {}
 
         def final_mm(i):
             v = prb.tile([P, CH], F32, name="v", tag="rb")
             vts[i] = v
             for hh in range(2):
+                g = 2 * i + hh
                 nc.tensor.matmul_mx(
                     out=v[:],
-                    lhsT=mcod[i][:, hh * P : (hh + 1) * P].bitcast(FP8X4),
-                    lhsT_scale=mscl[i][:, hh * P : (hh + 1) * P],
+                    lhsT=mcod[g][:].bitcast(FP8X4),
+                    lhsT_scale=mscl[g][:],
                     rhs=xc2[i][:, hh * 512 : (hh + 1) * 512].bitcast(FP8X4),
                     rhs_scale=xsc2[i][:, hh * 512 : (hh + 1) * 512],
                     start=(hh == 0),
@@ -532,11 +537,13 @@ def tile_sralnet_pa_kernel(tc, x, centroids, out):
         def final_c(i):
             sm, pg, vp = fst[i]
             o = fin.tile([P, CH], F32, name="o", tag="o")
-            nc.scalar.activation(
+            nc.gpsimd.tensor_scalar(
                 out=o[:].rearrange("p (q j) -> p q j", j=4),
-                in_=vp[:].rearrange("p (j q) -> p q j", j=4),
-                func=ACTF.Copy,
-                scale=pg[:, 4:5],
+                in0=vp[:].rearrange("p (j q) -> p q j", j=4),
+                scalar1=pg[:, 4:5],
+                scalar2=0.0,
+                op0=ALU.mult,
+                op1=ALU.add,
             )
             nc.sync.dma_start(out=out[i].rearrange("(k c) -> k c", c=CH), in_=o[:])
 
@@ -547,14 +554,13 @@ def tile_sralnet_pa_kernel(tc, x, centroids, out):
                 if j < len(b):
                     b[j]()
 
-        first = xprep_a_list(0, 2)
-        for fn in first[0:3]:
+        for fn in xprep_a_list(0):
             fn()
+        xprep_b(0)
         bias_spread()
         mm1(0)
         mm1(1)
         mm1(2)
-        xprep_b(0)
         xprep_b(1)
         for t in range(GROUPS + 5):
             fr = []
@@ -564,19 +570,20 @@ def tile_sralnet_pa_kernel(tc, x, centroids, out):
                 fr = [lambda j=j: hook(GROUPS, j) for j in range(7)]
             bk = []
             if t == 0:
-                bk.extend(first[3:6])
+                bk.extend(xprep_c_list(0))
+                bk.extend(xprep_c_list(1))
             if t % 2 == 0:
                 pr = []
                 if 0 <= t - 4 < GROUPS:
                     pr = prod_list((t - 4) // 2)
                 if 0 <= t - 6 < GROUPS:
                     bk.append(lambda i=(t - 6) // 2: final_tot(i))
-                bk.extend(pr[0:1])
+                bk.extend(pr[0:2])
                 if 0 <= t - 6 < GROUPS:
                     bk.append(lambda i=(t - 6) // 2: final_b(i))
-                bk.extend(pr[1:])
+                bk.extend(pr[2:])
                 if t + 2 < GROUPS:
-                    bk.extend(xprep_a_list(t // 2 + 1, 1))
+                    bk.extend(xprep_a_list(t // 2 + 1))
                 if 0 <= t - 6 < GROUPS:
                     bk.append(lambda i=(t - 6) // 2: final_c(i))
             else:
@@ -584,18 +591,16 @@ def tile_sralnet_pa_kernel(tc, x, centroids, out):
                 if 0 <= t - 5 < GROUPS:
                     i = (t - 5) // 2
                     qs = [
-                        lambda i=i: mquant(i),
+                        lambda i=i: mquant(2 * i),
+                        lambda i=i: mquant(2 * i + 1),
                         lambda i=i: final_mm(i),
                         lambda i=i: final_a(i),
                     ]
                 ws = []
                 if 0 <= t - 3 < GROUPS:
                     i = (t - 3) // 2
-                    ws = lse_list(i) + w_list(i)
-                bk.extend(qs[0:2] + ws[0:1] + qs[2:3] + ws[1:])
-            if t == 0:
-                bk.extend(xprep_c_list(0))
-                bk.extend(xprep_c_list(1))
+                    ws = lse_list(i) + w_list(2 * i) + w_list(2 * i + 1)
+                bk.extend(qs[0:3] + ws[0:1] + qs[3:4] + ws[1:])
             if t == 1:
                 bk.extend(xprep_c_list(2))
                 bk.extend(xprep_c_list(3))

@@ -19,7 +19,9 @@ PIX = 1024
 K = 128
 S5 = 5
 M = K * S5
-GROUPS = 8
+GW = 512
+GROUPS = IMAGES * PIX // GW
+UNITS = GROUPS * S5
 EPS2 = 1e-24
 
 FLOPS = 2 * IMAGES * PIX * M * CH + 2 * IMAGES * K * CH * PIX
@@ -30,34 +32,37 @@ def tile_sralnet_pa_kernel(tc, x, centroids, out):
     with ExitStack() as ctx:
         const = ctx.enter_context(tc.tile_pool(name="const", bufs=1))
         xin = ctx.enter_context(tc.tile_pool(name="xin", bufs=4))
-        xgp = ctx.enter_context(tc.tile_pool(name="xgp", bufs=1))
+        xgp = ctx.enter_context(tc.tile_pool(name="xgp", bufs=2))
         xq1 = ctx.enter_context(tc.tile_pool(name="xq1", bufs=2))
-        xq2 = ctx.enter_context(tc.tile_pool(name="xq2", bufs=4))
-        zbp = ctx.enter_context(tc.tile_pool(name="zbp", bufs=5))
-        dp = ctx.enter_context(tc.tile_pool(name="dp", bufs=1))
+        xq2 = ctx.enter_context(tc.tile_pool(name="xq2", bufs=3))
+        zp = ctx.enter_context(tc.tile_pool(name="zp", bufs=6))
+        ep = ctx.enter_context(tc.tile_pool(name="ep", bufs=8))
+        ap_ = ctx.enter_context(tc.tile_pool(name="apool", bufs=4))
         tmp = ctx.enter_context(tc.tile_pool(name="tmp", bufs=1))
-        nmp = ctx.enter_context(tc.tile_pool(name="nmp", bufs=2))
+        nmp = ctx.enter_context(tc.tile_pool(name="nmp", bufs=3))
+        hmp = ctx.enter_context(tc.tile_pool(name="hmp", bufs=4))
         img = ctx.enter_context(tc.tile_pool(name="img", bufs=2))
-        mul = ctx.enter_context(tc.tile_pool(name="mul", bufs=4))
+        mul = ctx.enter_context(tc.tile_pool(name="mul", bufs=3))
         fin = ctx.enter_context(tc.tile_pool(name="fin", bufs=2))
-        pzm = ctx.enter_context(tc.psum_pool(name="pzm", bufs=3))
-        pz4 = ctx.enter_context(tc.psum_pool(name="pz4", bufs=1))
-        pdt = ctx.enter_context(tc.psum_pool(name="pdt", bufs=2))
-        prb = ctx.enter_context(tc.psum_pool(name="prb", bufs=1))
-        pmisc = ctx.enter_context(tc.psum_pool(name="pmisc", bufs=1))
+        pza = ctx.enter_context(tc.psum_pool(name="pza", bufs=2))
+        pdw = ctx.enter_context(tc.psum_pool(name="pdw", bufs=3))
+        pzt = ctx.enter_context(tc.psum_pool(name="pzt", bufs=1))
+        pmi = ctx.enter_context(tc.psum_pool(name="pmi", bufs=2))
         ctx.enter_context(tc.manual_schedule())
 
+        xs = {}
+        xs_0 = xin.tile([P, 4 * PIX], BF16, name="xs_0", tag="xs")
+        xs[0] = xs_0
+        x0v = xs_0[:].rearrange("p (j c) -> p j c", j=4)
+        x0d = x[0].rearrange("(q j) h w -> q j (h w)", j=4)
+        nc.sync.dma_start(out=x0v[:, :, 0:GW], in_=x0d[:, :, 0:GW])
         cen = const.tile([P, S5 * CH], BF16, name="cen")
         nc.sync.dma_start(out=cen[:], in_=centroids.rearrange("k s c -> k (s c)"))
-        xs = {}
-
-        def xload(n):
+        nc.sync.dma_start(out=x0v[:, :, GW:PIX], in_=x0d[:, :, GW:PIX])
+        for n in range(1, IMAGES):
             xs_n = xin.tile([P, 4 * PIX], BF16, name="xs_n", tag="xs")
             nc.sync.dma_start(out=xs_n[:], in_=x[n].rearrange("(q j) h w -> q (j h w)", j=4))
             xs[n] = xs_n
-
-        for n in range(IMAGES):
-            xload(n)
 
         ident = const.tile([P, P], F32, name="ident")
         make_identity(nc, ident[:])
@@ -71,421 +76,388 @@ def tile_sralnet_pa_kernel(tc, x, centroids, out):
         junk_e = const.tile([P, P], F32, name="junk_e")
         junk_w = const.tile([P, CH], F32, name="junk_w")
 
-        cenw = cen[:].bitcast(F32).rearrange("p (s q u) -> p s u q", s=S5, u=2)
-        wg = const.tile([P, 4 * M], BF16, name="wg", align_bytes=64)
-        for s in range(S5):
-            wt = pmisc.tile([P, 256], F32, name="wt", tag="misc")
-            for u in range(2):
-                nc.tensor.transpose(wt[:, u * P : (u + 1) * P], cenw[:, s, u], ident[:])
-            nc.vector.tensor_scalar(
-                out=wg[:, s * 512 : (s + 1) * 512].rearrange("p (k u e) -> p k u e", u=2, e=2),
-                in0=wt[:].bitcast(BF16).rearrange("p (u k e) -> p k u e", u=2, e=2),
-                scalar1=200.0,
-                scalar2=None,
-                op0=ALU.mult,
-            )
-        wc = const.tile([P, M], U32, name="wc", align_bytes=64)
-        wsc = const.tile([P, M], U8, name="wsc", align_bytes=64)
-        nc.vector.quantize_mx(out=wc[:, 0:512].bitcast(FP8X4), scales=wsc[:, 0:512], in_=wg[:, 0:2048])
-        nc.vector.quantize_mx(out=wc[:, 512:640].bitcast(FP8X4), scales=wsc[:, 512:640], in_=wg[:, 2048:2560])
-
-        n2 = const.tile([P, 8], F32, name="n2")
-        for s in range(S5):
-            nc.scalar.activation(
-                out=junk_w[:], in_=cen[:, s * CH : (s + 1) * CH], func=ACTF.Square, accum_out=n2[:, s : s + 1]
-            )
-        bcol = const.tile([P, 8], F32, name="bcol")
-        nc.gpsimd.tensor_tensor(out=bcol[:, 0:S5], in0=n2[:, 0:S5], in1=expo[:, 0:S5], op=ALU.pow)
-        brep = const.tile([P, M], F32, name="brep")
-        bb = const.tile([P, M], F32, name="bb")
-
-        def bias_spread():
-            for s in range(S5):
-                nc.vector.tensor_scalar(
-                    out=brep[:, s * P : (s + 1) * P],
-                    in0=ones[:],
-                    scalar1=bcol[:, s : s + 1],
-                    scalar2=-100.0,
-                    op0=ALU.mult,
-                    op1=ALU.mult,
-                )
-            bt0 = pmisc.tile([P, 512], F32, name="bt0", tag="misc")
-            for s in range(4):
-                nc.tensor.transpose(bt0[:, s * P : (s + 1) * P], brep[:, s * P : (s + 1) * P], ident[:])
-            nc.vector.tensor_copy(out=bb[:, 0:512], in_=bt0[:])
-            bt1 = pmisc.tile([P, P], F32, name="bt1", tag="misc")
-            nc.tensor.transpose(bt1[:], brep[:, 512:640], ident[:])
-            nc.vector.tensor_copy(out=bb[:, 512:640], in_=bt1[:])
-
         xc1 = {}
         xsc1 = {}
-        xc2 = {}
-        xsc2 = {}
+        xg1s = {}
 
-        xg2s = {}
-
-        def xprep_a_list(n):
-            xg1 = xgp.tile([P, 4 * PIX], BF16, name="xg1", tag="xg1", align_bytes=64)
+        def regroup(g, e):
+            n = g // 2
+            h = g % 2
+            if e == 0:
+                xg1 = xgp.tile([P, 4 * GW], BF16, name="xg1", tag="xg1", align_bytes=64)
+                xg1s[g] = xg1
             src = xs[n][:].rearrange("p (j a r e) -> p e a r j", j=4, a=4, r=P, e=2)
-            dst = xg1[:].rearrange("p (a e r j) -> p e a r j", a=4, e=2, r=P, j=4)
-            c1 = xq1.tile([P, PIX], U32, name="c1", tag="c1", align_bytes=64)
-            s1 = xq1.tile([P, PIX], U8, name="s1", tag="s1", align_bytes=64)
-            xc1[n] = c1
-            xsc1[n] = s1
+            dst = xg1s[g][:].rearrange("p (a e r j) -> p e a r j", a=2, e=2, r=P, j=4)
+            nc.vector.tensor_copy(out=dst[:, e], in_=src[:, e, 2 * h : 2 * h + 2])
 
-            def regroup(e):
-                nc.vector.tensor_copy(out=dst[:, e], in_=src[:, e])
+        def xquant(g):
+            n = g // 2
+            h = g % 2
+            if h == 0:
+                c1 = xq1.tile([P, PIX], U32, name="c1", tag="c1", align_bytes=64)
+                s1 = xq1.tile([P, PIX], U8, name="s1", tag="s1", align_bytes=64)
+                xc1[n] = c1
+                xsc1[n] = s1
+            nc.vector.quantize_mx(
+                out=xc1[n][:, h * GW : (h + 1) * GW].bitcast(FP8X4),
+                scales=xsc1[n][:, h * GW : (h + 1) * GW],
+                in_=xg1s[g][:],
+            )
 
-            def quant():
-                nc.vector.quantize_mx(out=c1[:].bitcast(FP8X4), scales=s1[:], in_=xg1[:])
+        wg = const.tile([P, 4 * M], BF16, name="wg", align_bytes=64)
+        wc = const.tile([P, M], U32, name="wc", align_bytes=64)
+        wsc = const.tile([P, M], U8, name="wsc", align_bytes=64)
+        n2 = const.tile([P, 8], F32, name="n2")
+        brt = const.tile([P, 8], F32, name="brt")
+        bcol = const.tile([P, 8], F32, name="bcol")
 
-            return [lambda: regroup(0), lambda: regroup(1), quant]
+        def wquant(s):
+            nc.vector.quantize_mx(
+                out=wc[:, s * P : (s + 1) * P].bitcast(FP8X4),
+                scales=wsc[:, s * P : (s + 1) * P],
+                in_=wg[:, s * 512 : (s + 1) * 512],
+            )
 
-        def xprep_b(n):
-            xw = xs[n][:].bitcast(F32).rearrange("p (j a w) -> p j a w", j=4, a=4, w=P)
-            xg2 = xgp.tile([P, 4 * PIX], BF16, name="xg2", tag="xg2", bufs=2, align_bytes=64)
-            xg2s[n] = xg2
-            xg2w = xg2[:].bitcast(F32).rearrange("p (h jp c) -> p h jp c", h=2, jp=2)
-            for h in range(2):
-                for jp in range(2):
-                    xt = pdt.tile([P, 512], F32, name="xt", tag="dt")
-                    for jl in range(2):
-                        for u in range(2):
-                            i = jl * 2 + u
-                            nc.tensor.transpose(xt[:, i * P : (i + 1) * P], xw[:, jp * 2 + jl, h * 2 + u], ident[:])
-                    nc.scalar.copy(
-                        out=xg2w[:, h, jp].rearrange("p (jl q u) -> p jl q u", jl=2, u=2),
-                        in_=xt[:].rearrange("p (jl u q) -> p jl q u", jl=2, u=2),
-                    )
+        def wprep():
+            cenw = cen[:].bitcast(F32).rearrange("p (s q u) -> p s u q", s=S5, u=2)
+            for s in range(S5):
+                wt = pmi.tile([P, 256], F32, name="wt", tag="mi")
+                for u in range(2):
+                    nc.tensor.transpose(wt[:, u * P : (u + 1) * P], cenw[:, s, u], ident[:])
+                nc.vector.tensor_scalar(
+                    out=wg[:, s * 512 : (s + 1) * 512].rearrange("p (k u e) -> p k u e", u=2, e=2),
+                    in0=wt[:].bitcast(BF16).rearrange("p (u k e) -> p k u e", u=2, e=2),
+                    scalar1=200.0,
+                    scalar2=None,
+                    op0=ALU.mult,
+                )
+                if s > 0:
+                    wquant(s - 1)
+            wquant(S5 - 1)
+            for s in range(S5):
+                nc.scalar.activation(
+                    out=junk_w[:], in_=cen[:, s * CH : (s + 1) * CH], func=ACTF.Square, accum_out=n2[:, s : s + 1]
+                )
+            nc.gpsimd.tensor_tensor(out=brt[:, 0:S5], in0=n2[:, 0:S5], in1=expo[:, 0:S5], op=ALU.pow)
+            nc.gpsimd.tensor_scalar(
+                out=bcol[:, 0:S5], in0=brt[:, 0:S5], scalar1=-100.0, scalar2=None, op0=ALU.mult
+            )
 
-        def xprep_c_list(n):
-            xg2 = xg2s[n]
-            c2 = xq2.tile([P, PIX], U32, name="c2", tag="c2", align_bytes=64)
-            s2 = xq2.tile([P, PIX], U8, name="s2", tag="s2", align_bytes=64)
-            xc2[n] = c2
-            xsc2[n] = s2
+        z = {}
+        COPY_S = 16
 
-            def quant(h):
-                nc.vector.quantize_mx(
-                    out=c2[:, h * 512 : (h + 1) * 512].bitcast(FP8X4),
-                    scales=s2[:, h * 512 : (h + 1) * 512],
-                    in_=xg2[:, h * 2048 : (h + 1) * 2048],
+        def zmx(v):
+            if not 0 <= v < UNITS:
+                return
+            g, s = divmod(v, S5)
+            n, h = divmod(g, 2)
+            if s == 0:
+                zg = zp.tile([P, S5 * GW], F32, name="zg", tag="z")
+                z[g] = zg
+            if g == 0:
+                zt = pdw.tile([P, GW], F32, name="zt0", tag="dw")
+            else:
+                zt = pzt.tile([P, GW], F32, name="zt", tag="zt")
+            nc.tensor.matmul_mx(
+                out=zt[:],
+                lhsT=wc[:, s * P : (s + 1) * P].bitcast(FP8X4),
+                lhsT_scale=wsc[:, s * P : (s + 1) * P],
+                rhs=xc1[n][:, h * GW : (h + 1) * GW].bitcast(FP8X4),
+                rhs_scale=xsc1[n][:, h * GW : (h + 1) * GW],
+                start=True,
+                stop=True,
+            )
+            dst = z[g][:, s * GW : (s + 1) * GW]
+            if (g == 0 and s % 2 == 1) or (g > 0 and v - 6 < COPY_S):
+                nc.scalar.activation(out=dst, in_=zt[:], func=ACTF.Identity, bias=bcol[:, s : s + 1], scale=1.0)
+            else:
+                nc.vector.tensor_scalar(
+                    out=dst, in0=zt[:], scalar1=bcol[:, s : s + 1], scalar2=None, op0=ALU.add
                 )
 
-            return [lambda: quant(0), lambda: quant(1)]
+        sm_t = {}
+        nm = {}
+        hm = {}
 
-        zm = {}
-        z4 = {}
-
-        def mm1(blk):
-            if blk >= 4 * GROUPS:
+        def smax(g, part):
+            if not 0 <= g < GROUPS:
                 return
-            g = blk // 4
-            t = blk % 4
-            n = g // 2
-            c0 = (blk % 8) * P
-            if t == 0:
-                z4g = pz4.tile([P, 512], F32, name="z4g", tag="z4")
-                z4[g] = z4g
-            zmb = pzm.tile([P, 512], F32, name="zmb", tag="zm")
-            zm[blk] = zmb
-            nc.tensor.matmul_mx(
-                out=zmb[:],
-                lhsT=xc1[n][:, c0 : c0 + P].bitcast(FP8X4),
-                lhsT_scale=xsc1[n][:, c0 : c0 + P],
-                rhs=wc[:, 0:512].bitcast(FP8X4),
-                rhs_scale=wsc[:, 0:512],
-                start=True,
-                stop=True,
-            )
-            nc.tensor.matmul_mx(
-                out=z4[g][:, t * P : (t + 1) * P],
-                lhsT=xc1[n][:, c0 : c0 + P].bitcast(FP8X4),
-                lhsT_scale=xsc1[n][:, c0 : c0 + P],
-                rhs=wc[:, 512:640].bitcast(FP8X4),
-                rhs_scale=wsc[:, 512:640],
-                start=True,
-                stop=True,
-            )
+            zg = z[g]
+            if part == 0:
+                t1 = tmp.tile([P, 2 * GW], F32, name="t1", tag="t1")
+                sm_t[g] = t1
+                nc.vector.tensor_tensor(out=t1[:], in0=zg[:, 0 : 2 * GW], in1=zg[:, 2 * GW : 4 * GW], op=ALU.max)
+            elif part == 1:
+                t1 = sm_t[g]
+                nc.vector.tensor_tensor(out=t1[:, 0:GW], in0=t1[:, 0:GW], in1=t1[:, GW : 2 * GW], op=ALU.max)
+            elif part == 2:
+                t1 = sm_t[g]
+                nc.vector.tensor_tensor(out=t1[:, GW : 2 * GW], in0=t1[:, 0:GW], in1=zg[:, 4 * GW : 5 * GW], op=ALU.max)
+            else:
+                t1 = sm_t[g]
+                nmg = nmp.tile([P, GW], F32, name="nmg", tag="nm")
+                hmg = hmp.tile([P, GW], F32, name="hmg", tag="hm")
+                nm[g] = nmg
+                hm[g] = hmg
+                nc.vector.tensor_scalar(out=nmg[:], in0=t1[:, GW : 2 * GW], scalar1=-1.0, scalar2=None, op0=ALU.mult)
+                nc.vector.tensor_scalar(out=hmg[:], in0=t1[:, GW : 2 * GW], scalar1=-0.5, scalar2=None, op0=ALU.mult)
 
-        zb = {}
         nmk = {}
-        msx = {}
-        nms = {}
         rc = {}
-        rbs = {}
-        beta = {}
-        acc = {}
-        mcod = {}
-        mscl = {}
-        msum = {}
+        zat = {}
 
-        def e1part(g, j):
-            i = g // 2
-            hh = g % 2
-            for c in range(4 * j, 4 * j + 4):
+        def za(v):
+            if not 0 <= v < UNITS:
+                return
+            g, s = divmod(v, S5)
+            i, hh = divmod(g, 2)
+            if hh == 0 and s == 0:
+                nmk_i = img.tile([P, 40], F32, name="nmk_i", tag="nmk")
+                rc_i = img.tile([P, PIX + 40], F32, name="rc_i", tag="rc")
+                nmk[i] = nmk_i
+                rc[i] = rc_i
+            zab = pza.tile([P, GW], F32, name="zab", tag="za")
+            zat[v] = zab
+            for t in range(4):
+                nc.tensor.transpose(
+                    zab[:, t * P : (t + 1) * P], z[g][:, s * GW + t * P : s * GW + (t + 1) * P], ident[:]
+                )
+
+        def kmax(v):
+            if not 0 <= v < UNITS:
+                return
+            g, s = divmod(v, S5)
+            i, hh = divmod(g, 2)
+            c = hh * 20 + s * 4
+            nc.vector.tensor_reduce(
+                out=nmk[i][:, c : c + 4],
+                in_=zat[v][:].rearrange("p (t k) -> p t k", t=4),
+                axis=AX.X,
+                op=ALU.max,
+                negate=True,
+            )
+
+        def e1(v):
+            if not 0 <= v < UNITS:
+                return
+            g, s = divmod(v, S5)
+            i, hh = divmod(g, 2)
+            for t in range(4):
+                c = hh * 20 + s * 4 + t
                 nc.scalar.activation(
                     out=junk_e[:],
-                    in_=zb[g][:, c * P : (c + 1) * P],
+                    in_=zat[v][:, t * P : (t + 1) * P],
                     func=ACTF.Exp,
-                    bias=nmk[i][:, hh * 20 + c : hh * 20 + c + 1],
+                    bias=nmk[i][:, c : c + 1],
                     scale=1.0,
-                    accum_out=rc[i][:, PIX + hh * 20 + c : PIX + hh * 20 + c + 1],
+                    accum_out=rc[i][:, PIX + c : PIX + c + 1],
                 )
 
-        e2s = {}
+        dat = {}
+        e2t = {}
+        cps = {}
 
-        def dpart(g, s):
-            if s == 0:
-                e2 = dp.tile([P, 4 * M], F32, name="e2", tag="e2")
-                e2s[g] = e2
-            dt = pdt.tile([P, 512], F32, name="dt", tag="dt")
+        def addt(out, in_a, in_b):
+            nc.tensor.matmul(out=out, lhsT=in_a, rhs=ident[:], is_transpose=True, start=True, stop=False)
+            nc.tensor.matmul(out=out, lhsT=in_b, rhs=ident[:], is_transpose=True, start=False, stop=True)
+
+        def da(v):
+            if not 0 <= v < UNITS:
+                return
+            g, s = divmod(v, S5)
+            dab = pdw.tile([P, GW], F32, name="dab", tag="dw")
+            dat[v] = dab
             for t in range(4):
-                c = t * S5 + s
-                nc.tensor.matmul(
-                    out=dt[:, t * P : (t + 1) * P],
-                    lhsT=zb[g][:, c * P : (c + 1) * P],
-                    rhs=ident[:],
-                    is_transpose=True,
-                    start=True,
-                    stop=False,
+                addt(
+                    dab[:, t * P : (t + 1) * P],
+                    z[g][:, s * GW + t * P : s * GW + (t + 1) * P],
+                    nm[g][:, t * P : (t + 1) * P],
                 )
-                nc.tensor.matmul(
-                    out=dt[:, t * P : (t + 1) * P],
-                    lhsT=nms[g][:, t * P : (t + 1) * P],
-                    rhs=ident[:],
-                    is_transpose=True,
-                    start=False,
-                    stop=True,
-                )
-            nc.scalar.activation(out=e2s[g][:, s * 512 : (s + 1) * 512], in_=dt[:], func=ACTF.Exp)
 
-        def rpart(g):
-            e2 = e2s[g]
-            rb = prb.tile([P, 512], F32, name="rb", tag="rb")
-            for t in range(4):
+        def e2(v):
+            if not 0 <= v < UNITS:
+                return
+            e2b = ep.tile([P, GW], F32, name="e2b", tag="e2")
+            e2t[v] = e2b
+            nc.scalar.activation(out=e2b[:], in_=dat[v][:], func=ACTF.Exp)
+
+        def cpart(g, ts):
+            if not 0 <= g < GROUPS:
+                return
+            if ts[0] == 0:
+                cb = pmi.tile([P, GW], F32, name="cb", tag="mi")
+                cps[g] = cb
+            for t in ts:
                 for s in range(S5):
                     nc.tensor.matmul(
-                        out=rb[:, t * P : (t + 1) * P],
-                        lhsT=e2[:, s * 512 + t * P : s * 512 + (t + 1) * P],
+                        out=cps[g][:, t * P : (t + 1) * P],
+                        lhsT=e2t[g * S5 + s][:, t * P : (t + 1) * P],
                         rhs=ident[:],
                         is_transpose=True,
                         start=(s == 0),
                         stop=(s == S5 - 1),
                     )
-            rbs[g] = rb
 
-        def hook(t, j):
-            if 1 <= t <= GROUPS:
-                if j < S5:
-                    dpart(t - 1, j)
-                    e1part(t - 1, j)
-                if j == 5:
-                    rpart(t - 1)
-                if j == 7:
-                    cpr(t - 1)
-                    if t % 2 == 0:
-                        logs((t - 2) // 2)
-            if t == 0 and j == 4:
-                xprep_b(2)
-            if t == 0 and j == 5:
-                xprep_b(3)
-
-        def cpr(g):
-            nc.scalar.copy(out=rc[g // 2][:, (g % 2) * 512 : (g % 2 + 1) * 512], in_=rbs[g][:])
+        def ccopy(g):
+            if not 0 <= g < GROUPS:
+                return
+            i, hh = divmod(g, 2)
+            nc.vector.tensor_copy(out=rc[i][:, hh * GW : (hh + 1) * GW], in_=cps[g][:])
 
         def logs(i):
             nc.scalar.activation(out=rc[i][:], in_=rc[i][:], func=ACTF.Ln)
 
-        def front_list(g):
-            i = g // 2
-            hh = g % 2
+        nhl = {}
+        beta = {}
+
+        def half_lse(g):
+            if not 0 <= g < GROUPS:
+                return
+            i, hh = divmod(g, 2)
             if hh == 0:
-                nmk_i = img.tile([P, 40], F32, name="nmk_i", tag="nmk")
-                msx_i = img.tile([P, PIX], F32, name="msx_i", tag="msx")
-                rc_i = img.tile([P, PIX + 40], F32, name="rc_i", tag="rc")
-                nmk[i] = nmk_i
-                msx[i] = msx_i
-                rc[i] = rc_i
-            zbg = zbp.tile([P, 4 * M], F32, name="zbg", tag="zb")
-            zb[g] = zbg
-            zv = zbg[:].rearrange("p (t m) -> p t m", t=4)
-            t1 = tmp.tile([P, 1024], F32, name="t1", tag="t1")
-            t1v = t1[:].rearrange("p (t m) -> p t m", t=4)
-            t2 = tmp.tile([P, 512], F32, name="t2", tag="t2")
-            t2v = t2[:].rearrange("p (t k) -> p t k", t=4)
-            msg = msx[i][:, hh * 512 : (hh + 1) * 512]
-            nmsg = nmp.tile([P, 512], F32, name="nmsg", tag="nms")
-            nms[g] = nmsg
-
-            def v1(t):
-                nc.vector.tensor_tensor(out=zv[:, t, 0:512], in0=zm[4 * g + t][:], in1=bb[:, 0:512], op=ALU.add)
-
-            def f0():
-                v1(0)
-                mm1(4 * g + 3)
-                hook(g, 0)
-
-            def f1():
-                v1(1)
-                hook(g, 1)
-
-            def f2():
-                v1(2)
-                hook(g, 2)
-
-            def f3():
-                v1(3)
-                hook(g, 3)
-
-            def f4():
-                nc.vector.tensor_tensor(
-                    out=zv[:, :, 512:640],
-                    in0=z4[g][:].rearrange("p (t k) -> p t k", t=4),
-                    in1=bb[:, 512:640].unsqueeze(1).to_broadcast([P, 4, P]),
-                    op=ALU.add,
-                )
-                mm1(4 * g + 4)
-                mm1(4 * g + 5)
-                mm1(4 * g + 6)
-                hook(g, 4)
-
-            def f5():
-                nc.vector.tensor_tensor(out=t1v, in0=zv[:, :, 0:256], in1=zv[:, :, 256:512], op=ALU.max)
-                hook(g, 5)
-
-            def f6():
-                nc.vector.tensor_reduce(
-                    out=nmk[i][:, hh * 20 : hh * 20 + 20],
-                    in_=zbg[:].rearrange("p (c k) -> p c k", k=P),
-                    axis=AX.X,
-                    op=ALU.max,
-                    negate=True,
-                )
-                hook(g, 6)
-
-            def f7():
-                nc.vector.tensor_tensor(out=t2v, in0=t1v[:, :, 0:128], in1=t1v[:, :, 128:256], op=ALU.max)
-                hook(g, 7)
-
-            def f8():
-                nc.vector.tensor_tensor(
-                    out=msg.rearrange("p (t k) -> p t k", t=4), in0=t2v, in1=zv[:, :, 512:640], op=ALU.max
-                )
-
-            def f9():
-                nc.gpsimd.tensor_scalar(out=nmsg[:], in0=msg, scalar1=-1.0, scalar2=0.0, op0=ALU.mult, op1=ALU.add)
-
-            return [f0, f1, f2, f3, f4, f5, f6, f7, f8, f9]
-
-        def lse_list(i):
-            def l0():
-                nc.vector.tensor_tensor(out=rc[i][:, 0:PIX], in0=rc[i][:, 0:PIX], in1=msx[i][:], op=ALU.add)
-
-            def l1():
                 beta_i = img.tile([P, 40], F32, name="beta_i", tag="beta")
                 beta[i] = beta_i
                 nc.vector.tensor_tensor(out=beta_i[:], in0=nmk[i][:], in1=rc[i][:, PIX : PIX + 40], op=ALU.subtract)
+            nhlg = nmp.tile([P, GW], F32, name="nhlg", tag="nhl")
+            nhl[g] = nhlg
+            nc.vector.scalar_tensor_tensor(
+                out=nhlg[:],
+                in0=rc[i][:, hh * GW : (hh + 1) * GW],
+                scalar=-0.5,
+                in1=hm[g][:],
+                op0=ALU.mult,
+                op1=ALU.add,
+            )
 
-            return [l0, l1]
+        wtt = {}
+        at = {}
+        acc = {}
 
-        def apass(g):
-            i = g // 2
-            hh = g % 2
-            for s in range(S5):
-                for t in range(4):
-                    c = t * S5 + s
-                    nc.scalar.activation(
-                        out=zb[g][:, c * P : (c + 1) * P],
-                        in_=zb[g][:, c * P : (c + 1) * P],
-                        func=ACTF.Exp,
-                        bias=beta[i][:, hh * 20 + c : hh * 20 + c + 1],
-                        scale=1.0,
-                    )
-
-        def w_list(g):
-            i = g // 2
-            hh = g % 2
-            zv = zb[g][:].rearrange("p (t m) -> p t m", t=4)
-            lv = rc[i][:, hh * 512 : (hh + 1) * 512].rearrange("p (t k) -> p t k", t=4)
-
-            def wone(s):
-                nc.vector.scalar_tensor_tensor(
-                    out=zv[:, :, s * P : (s + 1) * P],
-                    in0=zv[:, :, s * P : (s + 1) * P],
-                    scalar=2.0,
-                    in1=lv,
-                    op0=ALU.mult,
-                    op1=ALU.subtract,
+        def wt_(v):
+            if not 0 <= v < UNITS:
+                return
+            g, s = divmod(v, S5)
+            wb = pdw.tile([P, GW], F32, name="wb", tag="dw")
+            wtt[v] = wb
+            for t in range(4):
+                addt(
+                    wb[:, t * P : (t + 1) * P],
+                    z[g][:, s * GW + t * P : s * GW + (t + 1) * P],
+                    nhl[g][:, t * P : (t + 1) * P],
                 )
-                if s == S5 - 1:
-                    apass(g)
 
-            return [lambda s=s: wone(s) for s in range(S5)]
+        def apass(v):
+            if not 0 <= v < UNITS:
+                return
+            g, s = divmod(v, S5)
+            i, hh = divmod(g, 2)
+            ab = ap_.tile([P, GW], F32, name="ab", tag="ab")
+            at[v] = ab
+            for t in range(4):
+                c = hh * 20 + s * 4 + t
+                nc.scalar.activation(
+                    out=ab[:, t * P : (t + 1) * P],
+                    in_=wtt[v][:, t * P : (t + 1) * P],
+                    func=ACTF.Exp,
+                    bias=beta[i][:, c : c + 1],
+                    scale=2.0,
+                )
+
+        def prod(v):
+            if not 0 <= v < UNITS:
+                return
+            g, s = divmod(v, S5)
+            if s == 0:
+                accg = mul.tile([P, GW], F32, name="accg", tag="acc")
+                acc[g] = accg
+                nc.vector.tensor_scalar(out=accg[:], in0=at[v][:], scalar1=1.0, scalar2=None, op0=ALU.add)
+            else:
+                nc.vector.scalar_tensor_tensor(
+                    out=acc[g][:], in0=at[v][:], scalar=1.0, in1=acc[g][:], op0=ALU.add, op1=ALU.mult
+                )
 
         mgs = {}
+        mcod = {}
+        mscl = {}
 
-        def prod_list(i):
-            pair = (2 * i, 2 * i + 1)
-            for g in pair:
-                accg = mul.tile([P, 512], F32, name="accg", tag="acc")
-                acc[g] = accg
-
-            def pone(s, g):
-                zv = zb[g][:].rearrange("p (t m) -> p t m", t=4)
-                av = acc[g][:].rearrange("p (t k) -> p t k", t=4)
-                if s == 0:
-                    nc.vector.tensor_scalar(out=av, in0=zv[:, :, 0:P], scalar1=1.0, scalar2=None, op0=ALU.add)
-                else:
-                    nc.vector.scalar_tensor_tensor(
-                        out=av,
-                        in0=zv[:, :, s * P : (s + 1) * P],
-                        scalar=1.0,
-                        in1=av,
-                        op0=ALU.add,
-                        op1=ALU.mult,
-                    )
-                if s == S5 - 1:
-                    after(g)
-
-            def after(g):
-                if g == pair[0]:
-                    msp = pmisc.tile([P, 4], F32, name="msp", tag="misc")
-                    msum[i] = msp
-                mg = mul.tile([P, 512], BF16, name="mg", tag="mg", align_bytes=64)
-                mgs[g] = mg
-                nc.gpsimd.tensor_scalar(
-                    out=mg[:].rearrange("p (k t) -> p k t", t=4),
-                    in0=acc[g][:].rearrange("p (t k) -> p k t", t=4),
-                    scalar1=1.0,
-                    scalar2=0.0,
-                    op0=ALU.mult,
-                    op1=ALU.add,
-                )
-                for t in range(4):
-                    nc.tensor.matmul(
-                        out=msum[i][:, 0:2],
-                        lhsT=acc[g][:, t * P : (t + 1) * P],
-                        rhs=ones[:, 0:2],
-                        start=(g == pair[0] and t == 0),
-                        stop=(g == pair[1] and t == 3),
-                    )
-
-            return [lambda s=s, g=g: pone(s, g) for s in range(S5) for g in pair]
+        def cast(g):
+            if not 0 <= g < GROUPS:
+                return
+            mg = mul.tile([P, GW], BF16, name="mg", tag="mg", align_bytes=64)
+            mgs[g] = mg
+            dst = mg[:].rearrange("p (k t) -> p k t", t=4)
+            src = acc[g][:].rearrange("p (t k) -> p k t", t=4)
+            if g == GROUPS - 1:
+                nc.scalar.copy(out=dst, in_=src)
+            else:
+                nc.vector.tensor_copy(out=dst, in_=src)
 
         def mquant(g):
+            if not 0 <= g < GROUPS:
+                return
             mc = mul.tile([P, P], U32, name="mc", tag="mc", align_bytes=64)
             msc = mul.tile([P, P], U8, name="msc", tag="msc", align_bytes=64)
             nc.vector.quantize_mx(out=mc[:].bitcast(FP8X4), scales=msc[:], in_=mgs[g][:])
             mcod[g] = mc
             mscl[g] = msc
 
+        xg2s = {}
+        xc2 = {}
+        xsc2 = {}
+
+        def xt(n, b, eng):
+            h, jp = divmod(b, 2)
+            if b == 0:
+                xg2 = xgp.tile([P, 4 * PIX], BF16, name="xg2", tag="xg2", bufs=1, align_bytes=64)
+                xg2s[n] = xg2
+            xw = xs[n][:].bitcast(F32).rearrange("p (j a w) -> p j a w", j=4, a=4, w=P)
+            xg2w = xg2s[n][:].bitcast(F32).rearrange("p (h jp c) -> p h jp c", h=2, jp=2)
+            xtb = pmi.tile([P, GW], F32, name="xtb", tag="mi")
+            for jl in range(2):
+                for u in range(2):
+                    q = jl * 2 + u
+                    nc.tensor.transpose(xtb[:, q * P : (q + 1) * P], xw[:, jp * 2 + jl, h * 2 + u], ident[:])
+            dst = xg2w[:, h, jp].rearrange("p (jl q u) -> p jl q u", jl=2, u=2)
+            src = xtb[:].rearrange("p (jl u q) -> p jl q u", jl=2, u=2)
+            if eng == 0:
+                nc.scalar.copy(out=dst, in_=src)
+            else:
+                nc.vector.tensor_copy(out=dst, in_=src)
+
+        def x2quant(n, h):
+            if h == 0:
+                c2 = xq2.tile([P, PIX], U32, name="c2", tag="c2", align_bytes=64)
+                s2 = xq2.tile([P, PIX], U8, name="s2", tag="s2", align_bytes=64)
+                xc2[n] = c2
+                xsc2[n] = s2
+            nc.vector.quantize_mx(
+                out=xc2[n][:, h * 512 : (h + 1) * 512].bitcast(FP8X4),
+                scales=xsc2[n][:, h * 512 : (h + 1) * 512],
+                in_=xg2s[n][:, h * 2048 : (h + 1) * 2048],
+            )
+
+        smt = {}
+        vts = {}
         fst = {}
 
-        vts = {}
+        def msum(i):
+            ms = pmi.tile([P, 2], F32, name="ms", tag="mi")
+            for hh in range(2):
+                g = 2 * i + hh
+                for t in range(4):
+                    nc.tensor.matmul(
+                        out=ms[:],
+                        lhsT=acc[g][:, t * P : (t + 1) * P],
+                        rhs=ones[:, 0:2],
+                        start=(hh == 0 and t == 0),
+                        stop=(hh == 1 and t == 3),
+                    )
+            sm = fin.tile([P, 16], F32, name="sm", tag="sm")
+            smt[i] = sm
+            nc.vector.tensor_scalar(out=sm[:, 0:1], in0=ms[:, 0:1], scalar1=-1.0, scalar2=None, op0=ALU.mult)
 
         def final_mm(i):
-            v = prb.tile([P, CH], F32, name="v", tag="rb")
+            v = pmi.tile([P, CH], F32, name="v", tag="mi")
             vts[i] = v
             for hh in range(2):
                 g = 2 * i + hh
@@ -501,11 +473,8 @@ def tile_sralnet_pa_kernel(tc, x, centroids, out):
 
         def final_a(i):
             v = vts[i]
-            sm = fin.tile([P, 16], F32, name="sm", tag="sm")
+            sm = smt[i]
             ssq = fin.tile([P, 1], F32, name="ssq", tag="ssq")
-            nc.vector.tensor_scalar(
-                out=sm[:, 0:1], in0=msum[i][:, 0:1], scalar1=-1.0, scalar2=None, op0=ALU.mult
-            )
             vp = fin.tile([P, CH], F32, name="vp", tag="vp")
             nc.vector.scalar_tensor_tensor(
                 out=vp[:].rearrange("p (j q) -> p j q", j=4),
@@ -523,87 +492,85 @@ def tile_sralnet_pa_kernel(tc, x, centroids, out):
             nc.gpsimd.tensor_tensor(out=qcol[:, 0:1], in0=pg[:, 2:3], in1=pg[:, 1:2], op=ALU.mult)
             fst[i] = (sm, pg, vp)
 
-        def final_tot(i):
-            nc.tensor.matmul(out=msum[i][:, 2:4], lhsT=ones[:], rhs=qcol[:], start=True, stop=True)
-
         def final_b(i):
             sm, pg, vp = fst[i]
-            nc.vector.tensor_scalar(
-                out=sm[:, 1:2], in0=msum[i][:, 2:3], scalar1=EPS2, scalar2=None, op0=ALU.max
-            )
+            tot = pmi.tile([P, 2], F32, name="tot", tag="mi")
+            nc.tensor.matmul(out=tot[:], lhsT=ones[:], rhs=qcol[:], start=True, stop=True)
+            nc.vector.tensor_scalar(out=sm[:, 1:2], in0=tot[:, 0:1], scalar1=EPS2, scalar2=None, op0=ALU.max)
             nc.gpsimd.tensor_tensor(out=pg[:, 3:4], in0=sm[:, 1:2], in1=expo[:, 8:9], op=ALU.pow)
             nc.gpsimd.tensor_tensor(out=pg[:, 4:5], in0=pg[:, 3:4], in1=pg[:, 1:2], op=ALU.mult)
 
         def final_c(i):
             sm, pg, vp = fst[i]
             o = fin.tile([P, CH], F32, name="o", tag="o")
-            nc.gpsimd.tensor_scalar(
+            nc.vector.tensor_scalar(
                 out=o[:].rearrange("p (q j) -> p q j", j=4),
                 in0=vp[:].rearrange("p (j q) -> p q j", j=4),
                 scalar1=pg[:, 4:5],
-                scalar2=0.0,
+                scalar2=None,
                 op0=ALU.mult,
-                op1=ALU.add,
             )
             nc.sync.dma_start(out=out[i].rearrange("(k c) -> k c", c=CH), in_=o[:])
 
-        def zipped(a, b):
-            for j in range(max(len(a), len(b))):
-                if j < len(a):
-                    a[j]()
-                if j < len(b):
-                    b[j]()
+        XT = {}
+        for n, steps in enumerate(((1, 4, 6, 9), (11, 14, 16, 19), (41, 44, 45, 46), (47, 48, 51, 52))):
+            for b in range(4):
+                XT[steps[b]] = (n, b)
 
-        for fn in xprep_a_list(0):
-            fn()
-        xprep_b(0)
-        bias_spread()
-        mm1(0)
-        mm1(1)
-        mm1(2)
-        xprep_b(1)
-        for t in range(GROUPS + 5):
-            fr = []
-            if t < GROUPS:
-                fr = front_list(t)
-            elif t == GROUPS:
-                fr = [lambda j=j: hook(GROUPS, j) for j in range(7)]
-            bk = []
-            if t == 0:
-                bk.extend(xprep_c_list(0))
-                bk.extend(xprep_c_list(1))
-            if t % 2 == 0:
-                pr = []
-                if 0 <= t - 4 < GROUPS:
-                    pr = prod_list((t - 4) // 2)
-                if 0 <= t - 6 < GROUPS:
-                    bk.append(lambda i=(t - 6) // 2: final_tot(i))
-                bk.extend(pr[0:2])
-                if 0 <= t - 6 < GROUPS:
-                    bk.append(lambda i=(t - 6) // 2: final_b(i))
-                bk.extend(pr[2:])
-                if t + 2 < GROUPS:
-                    bk.extend(xprep_a_list(t // 2 + 1))
-                if 0 <= t - 6 < GROUPS:
-                    bk.append(lambda i=(t - 6) // 2: final_c(i))
-            else:
-                qs = []
-                if 0 <= t - 5 < GROUPS:
-                    i = (t - 5) // 2
-                    qs = [
-                        lambda i=i: mquant(2 * i),
-                        lambda i=i: mquant(2 * i + 1),
-                        lambda i=i: final_mm(i),
-                        lambda i=i: final_a(i),
-                    ]
-                ws = []
-                if 0 <= t - 3 < GROUPS:
-                    i = (t - 3) // 2
-                    ws = lse_list(i) + w_list(2 * i) + w_list(2 * i + 1)
-                bk.extend(qs[0:3] + ws[0:1] + qs[3:4] + ws[1:])
-            if t == 1:
-                bk.extend(xprep_c_list(2))
-                bk.extend(xprep_c_list(3))
-            zipped(fr, bk)
-            if t == GROUPS:
-                hook(GROUPS, 7)
+        for u in range(-9, UNITS + 27):
+            if (u + 9) % 5 < 3 and 0 <= (u + 9) // 5 < GROUPS:
+                if (u + 9) % 5 < 2:
+                    regroup((u + 9) // 5, (u + 9) % 5)
+                else:
+                    xquant((u + 9) // 5)
+            if u == -7:
+                wprep()
+            za(u + 1)
+            kmax(u + 1)
+            e1(u)
+            zmx(u + 6)
+            if u % 5 == 3:
+                smax((u + 2) // 5, 0)
+            if u % 5 == 4:
+                smax((u + 1) // 5, 1)
+            if u % 5 == 0:
+                smax(u // 5, 2)
+            da(u - 1)
+            if u % 5 == 0:
+                smax(u // 5, 3)
+            e2(u - 2)
+            if u % 5 == 2:
+                cpart((u - 7) // 5, (0, 1))
+            if u % 5 == 3:
+                cpart((u - 8) // 5, (2, 3))
+                ccopy((u - 8) // 5)
+            if u % 10 == 5:
+                half_lse(2 * ((u - 15) // 10))
+            if u % 10 == 6:
+                half_lse(2 * ((u - 16) // 10) + 1)
+            wt_(u - 15)
+            prod(u - 17)
+            if u % 5 == 2:
+                cast((u - 22) // 5)
+            if u % 5 == 3:
+                mquant((u - 23) // 5)
+            apass(u - 16)
+            if u % 10 == 4 and 0 <= (u - 14) // 10 < IMAGES:
+                logs((u - 14) // 10)
+            if u in XT:
+                n, b = XT[u]
+                xt(n, b, 1)
+                if b == 1:
+                    x2quant(n, 0)
+                if b == 3:
+                    x2quant(n, 1)
+            if u % 10 == 7 and 0 <= (u - 27) // 10 < IMAGES:
+                msum((u - 27) // 10)
+            if u % 10 == 9 and 0 <= (u - 29) // 10 < IMAGES:
+                final_mm((u - 29) // 10)
+            if u % 10 == 0 and 0 <= (u - 30) // 10 < IMAGES:
+                final_a((u - 30) // 10)
+            if u % 10 == 4 and 0 <= (u - 34) // 10 < IMAGES:
+                final_b((u - 34) // 10)
+            if u % 10 == 6 and 0 <= (u - 36) // 10 < IMAGES:
+                final_c((u - 36) // 10)

@@ -219,8 +219,13 @@ def tile_sralnet_pa_kernel(tc, x, centroids, out):
             zab = pza.tile([P, GW], F32, name="zab", tag="za")
             zat[v] = zab
             for t in range(4):
-                nc.tensor.transpose(
-                    zab[:, t * P : (t + 1) * P], z[g][:, s * GW + t * P : s * GW + (t + 1) * P], ident[:]
+                nc.tensor.matmul(
+                    out=zab[:, t * P : (t + 1) * P],
+                    lhsT=z[g][:, s * GW + t * P : s * GW + (t + 1) * P],
+                    rhs=ident[:],
+                    is_transpose=(t > 0),
+                    start=True,
+                    stop=True,
                 )
 
         def kmax(v):
@@ -257,8 +262,8 @@ def tile_sralnet_pa_kernel(tc, x, centroids, out):
         e2t = {}
         cps = {}
 
-        def addt(out, in_a, in_b):
-            nc.tensor.matmul(out=out, lhsT=in_a, rhs=ident[:], is_transpose=True, start=True, stop=False)
+        def addt(out, in_a, in_b, real=False):
+            nc.tensor.matmul(out=out, lhsT=in_a, rhs=ident[:], is_transpose=not real, start=True, stop=False)
             nc.tensor.matmul(out=out, lhsT=in_b, rhs=ident[:], is_transpose=True, start=False, stop=True)
 
         def da(v):
@@ -344,6 +349,7 @@ def tile_sralnet_pa_kernel(tc, x, centroids, out):
                     wb[:, t * P : (t + 1) * P],
                     z[g][:, s * GW + t * P : s * GW + (t + 1) * P],
                     nhl[g][:, t * P : (t + 1) * P],
+                    real=(t == 0 and v >= 8),
                 )
 
         def apass(v):

@@ -23,6 +23,25 @@ GW = 512
 GROUPS = IMAGES * PIX // GW
 UNITS = GROUPS * S5
 EPS2 = 1e-24
+REP = 1
+REPX = {}
+WADD = {1: 'g', 2: 'g', 4: 'g', 5: 'g', 7: 'g', 8: 'g', 10: 'g', 11: 'g', 13: 'g', 14: 'g', 16: 'v', 17: 'v', 18: 'v', 19: 'v', 20: 'v', 21: 'v', 22: 'v', 23: 'v', 24: 'v', 25: 'v'}
+DADD = {}
+REALZ = {}
+REALD = {0: 1, 1: 1, 2: 1, 3: 1, 4: 1, 5: 1, 6: 1, 7: 1, 8: 1, 9: 1, 10: 1, 11: 1, 12: 1, 13: 1, 14: 1, 15: 1, 16: 1, 17: 1, 18: 1, 19: 1, 20: 1, 21: 1, 22: 1, 23: 1, 24: 1, 25: 1, 26: 1, 27: 1, 28: 1, 29: 1, 30: 1, 31: 1, 32: 1, 33: 1, 34: 1, 35: 1}
+REALW = {0: 1, 1: 1, 2: 1, 3: 1, 4: 1, 5: 1, 6: 1, 7: 1, 8: 1, 9: 1, 10: 1, 11: 1, 12: 1, 13: 1, 14: 1, 15: 1, 16: 1, 17: 1, 18: 1, 19: 1}
+ZCOPY = {0: 'v', 1: 's', 2: 'v', 3: 's', 4: 'v', 5: 's', 6: 's', 7: 's', 8: 's', 9: 's', 10: 's', 11: 's', 12: 's', 13: 's', 14: 's', 15: 's', 16: 's', 17: 's', 18: 's', 19: 's', 20: 's', 21: 's', 22: 's', 23: 's', 24: 'v', 25: 'v', 26: 'v', 27: 'v', 28: 'v', 29: 'v', 30: 'v', 31: 'v', 32: 'v', 33: 'v', 34: 'v', 35: 'v', 36: 'v', 37: 'v', 38: 'v', 39: 'v'}
+LL = 15
+LH = 16
+LW = 17
+CC = 9
+FB = 16
+FC = 19
+XTE = 1
+XTS = [[1, 4, 6, 9], [11, 14, 16, 19], [39, 41, 44, 45], [46, 49, 51, 54]]
+ZP = 0
+YL = 1
+YB = 4
 
 FLOPS = 2 * IMAGES * PIX * M * CH + 2 * IMAGES * K * CH * PIX
 
@@ -42,6 +61,7 @@ def tile_sralnet_pa_kernel(tc, x, centroids, out):
         nmp = ctx.enter_context(tc.tile_pool(name="nmp", bufs=3))
         hmp = ctx.enter_context(tc.tile_pool(name="hmp", bufs=4))
         img = ctx.enter_context(tc.tile_pool(name="img", bufs=2))
+        ypool = ctx.enter_context(tc.tile_pool(name="ypool", bufs=YB))
         mul = ctx.enter_context(tc.tile_pool(name="mul", bufs=3))
         fin = ctx.enter_context(tc.tile_pool(name="fin", bufs=2))
         pza = ctx.enter_context(tc.psum_pool(name="pza", bufs=2))
@@ -144,7 +164,18 @@ def tile_sralnet_pa_kernel(tc, x, centroids, out):
             )
 
         z = {}
-        COPY_S = 16
+
+        def mx1(bank, g, s):
+            n, h = divmod(g, 2)
+            nc.tensor.matmul_mx(
+                out=bank[:],
+                lhsT=wc[:, s * P : (s + 1) * P].bitcast(FP8X4),
+                lhsT_scale=wsc[:, s * P : (s + 1) * P],
+                rhs=xc1[n][:, h * GW : (h + 1) * GW].bitcast(FP8X4),
+                rhs_scale=xsc1[n][:, h * GW : (h + 1) * GW],
+                start=True,
+                stop=True,
+            )
 
         def zmx(v):
             if not 0 <= v < UNITS:
@@ -158,17 +189,10 @@ def tile_sralnet_pa_kernel(tc, x, centroids, out):
                 zt = pdw.tile([P, GW], F32, name="zt0", tag="dw")
             else:
                 zt = pzt.tile([P, GW], F32, name="zt", tag="zt")
-            nc.tensor.matmul_mx(
-                out=zt[:],
-                lhsT=wc[:, s * P : (s + 1) * P].bitcast(FP8X4),
-                lhsT_scale=wsc[:, s * P : (s + 1) * P],
-                rhs=xc1[n][:, h * GW : (h + 1) * GW].bitcast(FP8X4),
-                rhs_scale=xsc1[n][:, h * GW : (h + 1) * GW],
-                start=True,
-                stop=True,
-            )
+            for again in range(REPX.get(v, REP)):
+                mx1(zt, g, s)
             dst = z[g][:, s * GW : (s + 1) * GW]
-            if (g == 0 and s % 2 == 1) or (g > 0 and v - 6 < COPY_S):
+            if ZCOPY.get(v) == "s":
                 nc.scalar.activation(out=dst, in_=zt[:], func=ACTF.Identity, bias=bcol[:, s : s + 1], scale=1.0)
             else:
                 nc.vector.tensor_scalar(
@@ -223,7 +247,7 @@ def tile_sralnet_pa_kernel(tc, x, centroids, out):
                     out=zab[:, t * P : (t + 1) * P],
                     lhsT=z[g][:, s * GW + t * P : s * GW + (t + 1) * P],
                     rhs=ident[:],
-                    is_transpose=(t > 0),
+                    is_transpose=not (t == 3 and REALZ.get(v)),
                     start=True,
                     stop=True,
                 )
@@ -266,18 +290,45 @@ def tile_sralnet_pa_kernel(tc, x, centroids, out):
             nc.tensor.matmul(out=out, lhsT=in_a, rhs=ident[:], is_transpose=not real, start=True, stop=False)
             nc.tensor.matmul(out=out, lhsT=in_b, rhs=ident[:], is_transpose=True, start=False, stop=True)
 
+        ys = {}
+
+        def yadd(kind, v, rows, eng):
+            if not 0 <= v < UNITS or not eng:
+                return
+            g, s = divmod(v, S5)
+            y = ypool.tile([P, GW], F32, name="y", tag="y")
+            ys[(kind, v)] = y
+            e = nc.vector if eng == "v" else nc.gpsimd
+            e.tensor_tensor(out=y[:], in0=z[g][:, s * GW : (s + 1) * GW], in1=rows[g][:], op=ALU.add)
+
+        def bring(bank, kind, v, zs, row, real):
+            if (kind, v) in ys:
+                y = ys[(kind, v)]
+                for t in range(4):
+                    nc.tensor.matmul(
+                        out=bank[:, t * P : (t + 1) * P],
+                        lhsT=y[:, t * P : (t + 1) * P],
+                        rhs=ident[:],
+                        is_transpose=not (real and t == 0),
+                        start=True,
+                        stop=True,
+                    )
+            else:
+                for t in range(4):
+                    addt(
+                        bank[:, t * P : (t + 1) * P],
+                        zs[:, t * P : (t + 1) * P],
+                        row[:, t * P : (t + 1) * P],
+                        real=(real and t == 0),
+                    )
+
         def da(v):
             if not 0 <= v < UNITS:
                 return
             g, s = divmod(v, S5)
             dab = pdw.tile([P, GW], F32, name="dab", tag="dw")
             dat[v] = dab
-            for t in range(4):
-                addt(
-                    dab[:, t * P : (t + 1) * P],
-                    z[g][:, s * GW + t * P : s * GW + (t + 1) * P],
-                    nm[g][:, t * P : (t + 1) * P],
-                )
+            bring(dab, "d", v, z[g][:, s * GW : (s + 1) * GW], nm[g], REALD.get(v))
 
         def e2(v):
             if not 0 <= v < UNITS:
@@ -344,13 +395,7 @@ def tile_sralnet_pa_kernel(tc, x, centroids, out):
             g, s = divmod(v, S5)
             wb = pdw.tile([P, GW], F32, name="wb", tag="dw")
             wtt[v] = wb
-            for t in range(4):
-                addt(
-                    wb[:, t * P : (t + 1) * P],
-                    z[g][:, s * GW + t * P : s * GW + (t + 1) * P],
-                    nhl[g][:, t * P : (t + 1) * P],
-                    real=(t == 0 and v >= 8),
-                )
+            bring(wb, "w", v, z[g][:, s * GW : (s + 1) * GW], nhl[g], REALW.get(v))
 
         def apass(v):
             if not 0 <= v < UNITS:
@@ -519,11 +564,12 @@ def tile_sralnet_pa_kernel(tc, x, centroids, out):
             nc.sync.dma_start(out=out[i].rearrange("(k c) -> k c", c=CH), in_=o[:])
 
         XT = {}
-        for n, steps in enumerate(((1, 4, 6, 9), (11, 14, 16, 19), (41, 44, 45, 46), (47, 48, 51, 52))):
+        for n, steps in enumerate(XTS):
             for b in range(4):
                 XT[steps[b]] = (n, b)
 
-        for u in range(-9, UNITS + 27):
+        PU = LW + 2
+        for u in range(-9, UNITS + LW + 16):
             if (u + 9) % 5 < 3 and 0 <= (u + 9) // 5 < GROUPS:
                 if (u + 9) % 5 < 2:
                     regroup((u + 9) // 5, (u + 9) % 5)
@@ -534,7 +580,8 @@ def tile_sralnet_pa_kernel(tc, x, centroids, out):
             za(u + 1)
             kmax(u + 1)
             e1(u)
-            zmx(u + 6)
+            if ZP == 0:
+                zmx(u + 6)
             if u % 5 == 3:
                 smax((u + 2) // 5, 0)
             if u % 5 == 4:
@@ -542,41 +589,49 @@ def tile_sralnet_pa_kernel(tc, x, centroids, out):
             if u % 5 == 0:
                 smax(u // 5, 2)
             da(u - 1)
+            if ZP == 1:
+                zmx(u + 6)
+            for i in range(IMAGES):
+                if u == 10 * i + LH:
+                    half_lse(2 * i)
+                if u == 10 * i + LH + 1:
+                    half_lse(2 * i + 1)
+            yadd("w", u - LW + YL, nhl, WADD.get(u - LW + YL))
             if u % 5 == 0:
                 smax(u // 5, 3)
+            yadd("d", u, nm, DADD.get(u))
             e2(u - 2)
             if u % 5 == 2:
                 cpart((u - 7) // 5, (0, 1))
             if u % 5 == 3:
                 cpart((u - 8) // 5, (2, 3))
-                ccopy((u - 8) // 5)
-            if u % 10 == 5:
-                half_lse(2 * ((u - 15) // 10))
-            if u % 10 == 6:
-                half_lse(2 * ((u - 16) // 10) + 1)
-            wt_(u - 15)
-            prod(u - 17)
-            if u % 5 == 2:
-                cast((u - 22) // 5)
-            if u % 5 == 3:
-                mquant((u - 23) // 5)
-            apass(u - 16)
-            if u % 10 == 4 and 0 <= (u - 14) // 10 < IMAGES:
-                logs((u - 14) // 10)
+            if u % 5 == CC % 5:
+                ccopy((u - CC) // 5)
+            for i in range(IMAGES):
+                if u == 10 * i + LL:
+                    logs(i)
+            wt_(u - LW)
+            prod(u - PU)
+            if (u - PU) % 5 == 0:
+                cast((u - PU - 5) // 5)
+            if (u - PU) % 5 == 1:
+                mquant((u - PU - 6) // 5)
+            apass(u - LW - 1)
             if u in XT:
                 n, b = XT[u]
-                xt(n, b, 1)
+                xt(n, b, XTE)
                 if b == 1:
                     x2quant(n, 0)
                 if b == 3:
                     x2quant(n, 1)
-            if u % 10 == 7 and 0 <= (u - 27) // 10 < IMAGES:
-                msum((u - 27) // 10)
-            if u % 10 == 9 and 0 <= (u - 29) // 10 < IMAGES:
-                final_mm((u - 29) // 10)
-            if u % 10 == 0 and 0 <= (u - 30) // 10 < IMAGES:
-                final_a((u - 30) // 10)
-            if u % 10 == 4 and 0 <= (u - 34) // 10 < IMAGES:
-                final_b((u - 34) // 10)
-            if u % 10 == 6 and 0 <= (u - 36) // 10 < IMAGES:
-                final_c((u - 36) // 10)
+            for i in range(IMAGES):
+                if u == 10 * i + PU + 10:
+                    msum(i)
+                if u == 10 * i + PU + 12:
+                    final_mm(i)
+                if u == 10 * i + PU + 13:
+                    final_a(i)
+                if u == 10 * i + PU + FB:
+                    final_b(i)
+                if u == 10 * i + PU + FC:
+                    final_c(i)

@@ -23,25 +23,32 @@ GW = 512
 GROUPS = IMAGES * PIX // GW
 UNITS = GROUPS * S5
 EPS2 = 1e-24
-REP = 1
-REPX = {}
-WADD = {1: 'g', 2: 'g', 4: 'g', 5: 'g', 7: 'g', 8: 'g', 10: 'g', 11: 'g', 13: 'g', 14: 'g', 16: 'v', 17: 'v', 18: 'v', 19: 'v', 20: 'v', 21: 'v', 22: 'v', 23: 'v', 24: 'v', 25: 'v'}
-DADD = {}
+REP = 2
+HO = 0
+RH = 0
+SB = 0
+DW = 2
+ZT = 2
 REALZ = {}
-REALD = {0: 1, 1: 1, 2: 1, 3: 1, 4: 1, 5: 1, 6: 1, 7: 1, 8: 1, 9: 1, 10: 1, 11: 1, 12: 1, 13: 1, 14: 1, 15: 1, 16: 1, 17: 1, 18: 1, 19: 1, 20: 1, 21: 1, 22: 1, 23: 1, 24: 1, 25: 1, 26: 1, 27: 1, 28: 1, 29: 1, 30: 1, 31: 1, 32: 1, 33: 1, 34: 1, 35: 1}
-REALW = {0: 1, 1: 1, 2: 1, 3: 1, 4: 1, 5: 1, 6: 1, 7: 1, 8: 1, 9: 1, 10: 1, 11: 1, 12: 1, 13: 1, 14: 1, 15: 1, 16: 1, 17: 1, 18: 1, 19: 1}
-ZCOPY = {0: 'v', 1: 's', 2: 'v', 3: 's', 4: 'v', 5: 's', 6: 's', 7: 's', 8: 's', 9: 's', 10: 's', 11: 's', 12: 's', 13: 's', 14: 's', 15: 's', 16: 's', 17: 's', 18: 's', 19: 's', 20: 's', 21: 's', 22: 's', 23: 's', 24: 'v', 25: 'v', 26: 'v', 27: 'v', 28: 'v', 29: 'v', 30: 'v', 31: 'v', 32: 'v', 33: 'v', 34: 'v', 35: 'v', 36: 'v', 37: 'v', 38: 'v', 39: 'v'}
-LL = 15
-LH = 16
-LW = 17
-CC = 9
-FB = 16
+REALD = {10: 1, 11: 1, 12: 1, 13: 1, 14: 1, 15: 1, 16: 1, 17: 1, 18: 1, 19: 1, 20: 1, 21: 1, 22: 1, 23: 1, 24: 1, 25: 1, 26: 1, 27: 1, 28: 1, 29: 1}
+KE = 2
+LE = 3
+LD = 2
+EB = 14
+UB = 16
+LQ = 10
+AL = 1
+CC = 11
+FB = 18
 FC = 19
-XTE = 1
-XTS = [[1, 4, 6, 9], [11, 14, 16, 19], [39, 41, 44, 45], [46, 49, 51, 54]]
-ZP = 0
-YL = 1
-YB = 4
+QP = 0
+CAST = 's'
+XTE = {0: 0, 1: 0, 2: 0, 3: 0}
+XTS = [[1, 2, 6, 7], [11, 12, 16, 17], [31, 32, 36, 37], [41, 42, 46, 47]]
+DADD = {}
+AMUL = {}
+REG = {6: 's', 7: 's'}
+ZCOPY = {0: 's', 1: 's', 2: 's', 3: 's', 4: 's', 5: 's', 6: 's', 7: 's', 8: 's', 9: 's', 10: 's', 11: 's', 12: 's', 13: 's', 14: 's', 15: 's', 16: 's', 17: 's', 18: 's', 19: 's', 20: 's', 21: 's', 22: 's', 23: 's', 24: 's', 25: 's', 26: 's', 27: 's', 28: 's', 29: 's', 30: 's', 31: 's', 32: 's', 33: 's', 34: 's', 35: 's', 36: 's', 37: 's', 38: 's', 39: 's'}
 
 FLOPS = 2 * IMAGES * PIX * M * CH + 2 * IMAGES * K * CH * PIX
 
@@ -54,19 +61,16 @@ def tile_sralnet_pa_kernel(tc, x, centroids, out):
         xgp = ctx.enter_context(tc.tile_pool(name="xgp", bufs=2))
         xq1 = ctx.enter_context(tc.tile_pool(name="xq1", bufs=2))
         xq2 = ctx.enter_context(tc.tile_pool(name="xq2", bufs=3))
-        zp = ctx.enter_context(tc.tile_pool(name="zp", bufs=6))
-        ep = ctx.enter_context(tc.tile_pool(name="ep", bufs=8))
-        ap_ = ctx.enter_context(tc.tile_pool(name="apool", bufs=4))
+        zp = ctx.enter_context(tc.tile_pool(name="zp", bufs=4))
+        ep = ctx.enter_context(tc.tile_pool(name="ep", bufs=EB))
+        up = ctx.enter_context(tc.tile_pool(name="up", bufs=UB))
         tmp = ctx.enter_context(tc.tile_pool(name="tmp", bufs=1))
-        nmp = ctx.enter_context(tc.tile_pool(name="nmp", bufs=3))
-        hmp = ctx.enter_context(tc.tile_pool(name="hmp", bufs=4))
-        img = ctx.enter_context(tc.tile_pool(name="img", bufs=2))
-        ypool = ctx.enter_context(tc.tile_pool(name="ypool", bufs=YB))
+        grp = ctx.enter_context(tc.tile_pool(name="grp", bufs=3))
         mul = ctx.enter_context(tc.tile_pool(name="mul", bufs=3))
         fin = ctx.enter_context(tc.tile_pool(name="fin", bufs=2))
         pza = ctx.enter_context(tc.psum_pool(name="pza", bufs=2))
-        pdw = ctx.enter_context(tc.psum_pool(name="pdw", bufs=3))
-        pzt = ctx.enter_context(tc.psum_pool(name="pzt", bufs=1))
+        ppt = ctx.enter_context(tc.psum_pool(name="ppt", bufs=DW))
+        pzt = ctx.enter_context(tc.psum_pool(name="pzt", bufs=ZT))
         pmi = ctx.enter_context(tc.psum_pool(name="pmi", bufs=2))
         ctx.enter_context(tc.manual_schedule())
 
@@ -75,9 +79,9 @@ def tile_sralnet_pa_kernel(tc, x, centroids, out):
         xs[0] = xs_0
         x0v = xs_0[:].rearrange("p (j c) -> p j c", j=4)
         x0d = x[0].rearrange("(q j) h w -> q j (h w)", j=4)
-        nc.sync.dma_start(out=x0v[:, :, 0:GW], in_=x0d[:, :, 0:GW])
         cen = const.tile([P, S5 * CH], BF16, name="cen")
         nc.sync.dma_start(out=cen[:], in_=centroids.rearrange("k s c -> k (s c)"))
+        nc.sync.dma_start(out=x0v[:, :, 0:GW], in_=x0d[:, :, 0:GW])
         nc.sync.dma_start(out=x0v[:, :, GW:PIX], in_=x0d[:, :, GW:PIX])
         for n in range(1, IMAGES):
             xs_n = xin.tile([P, 4 * PIX], BF16, name="xs_n", tag="xs")
@@ -90,11 +94,12 @@ def tile_sralnet_pa_kernel(tc, x, centroids, out):
         nc.vector.memset(ones[:], 1.0)
         expo = const.tile([P, 16], F32, name="expo")
         nc.vector.memset(expo[:, 0:8], 0.5)
-        nc.vector.memset(expo[:, 8:16], -0.5)
+        nc.vector.memset(expo[:, 8:9], -0.5)
+        nc.vector.memset(expo[:, 9:10], -1.0)
         qcol = const.tile([P, 2], F32, name="qcol")
         nc.vector.memset(qcol[:], 0.0)
-        junk_e = const.tile([P, P], F32, name="junk_e")
         junk_w = const.tile([P, CH], F32, name="junk_w")
+        nc.scalar.activation(out=junk_w[:, 0:1], in_=expo[:, 0:1], func=ACTF.Exp)
 
         xc1 = {}
         xsc1 = {}
@@ -108,7 +113,10 @@ def tile_sralnet_pa_kernel(tc, x, centroids, out):
                 xg1s[g] = xg1
             src = xs[n][:].rearrange("p (j a r e) -> p e a r j", j=4, a=4, r=P, e=2)
             dst = xg1s[g][:].rearrange("p (a e r j) -> p e a r j", a=2, e=2, r=P, j=4)
-            nc.vector.tensor_copy(out=dst[:, e], in_=src[:, e, 2 * h : 2 * h + 2])
+            if REG.get(g) == "s" or (g == 0 and e < RH):
+                nc.scalar.copy(out=dst[:, e], in_=src[:, e, 2 * h : 2 * h + 2])
+            else:
+                nc.vector.tensor_copy(out=dst[:, e], in_=src[:, e, 2 * h : 2 * h + 2])
 
         def xquant(g):
             n = g // 2
@@ -185,11 +193,8 @@ def tile_sralnet_pa_kernel(tc, x, centroids, out):
             if s == 0:
                 zg = zp.tile([P, S5 * GW], F32, name="zg", tag="z")
                 z[g] = zg
-            if g == 0:
-                zt = pdw.tile([P, GW], F32, name="zt0", tag="dw")
-            else:
-                zt = pzt.tile([P, GW], F32, name="zt", tag="zt")
-            for again in range(REPX.get(v, REP)):
+            zt = pzt.tile([P, GW], F32, name="zt", tag="zt")
+            for again in range(REP if g > 0 else 1):
                 mx1(zt, g, s)
             dst = z[g][:, s * GW : (s + 1) * GW]
             if ZCOPY.get(v) == "s":
@@ -201,14 +206,13 @@ def tile_sralnet_pa_kernel(tc, x, centroids, out):
 
         sm_t = {}
         nm = {}
-        hm = {}
 
         def smax(g, part):
             if not 0 <= g < GROUPS:
                 return
             zg = z[g]
             if part == 0:
-                t1 = tmp.tile([P, 2 * GW], F32, name="t1", tag="t1")
+                t1 = tmp.tile([P, 2 * GW], BF16 if SB else F32, name="t1", tag="t1")
                 sm_t[g] = t1
                 nc.vector.tensor_tensor(out=t1[:], in0=zg[:, 0 : 2 * GW], in1=zg[:, 2 * GW : 4 * GW], op=ALU.max)
             elif part == 1:
@@ -219,27 +223,25 @@ def tile_sralnet_pa_kernel(tc, x, centroids, out):
                 nc.vector.tensor_tensor(out=t1[:, GW : 2 * GW], in0=t1[:, 0:GW], in1=zg[:, 4 * GW : 5 * GW], op=ALU.max)
             else:
                 t1 = sm_t[g]
-                nmg = nmp.tile([P, GW], F32, name="nmg", tag="nm")
-                hmg = hmp.tile([P, GW], F32, name="hmg", tag="hm")
+                nmg = grp.tile([P, GW], F32, name="nmg", tag="nm")
                 nm[g] = nmg
-                hm[g] = hmg
                 nc.vector.tensor_scalar(out=nmg[:], in0=t1[:, GW : 2 * GW], scalar1=-1.0, scalar2=None, op0=ALU.mult)
-                nc.vector.tensor_scalar(out=hmg[:], in0=t1[:, GW : 2 * GW], scalar1=-0.5, scalar2=None, op0=ALU.mult)
 
         nmk = {}
-        rc = {}
+        rsum = {}
+        rinv = {}
         zat = {}
+        ut = {}
 
         def za(v):
             if not 0 <= v < UNITS:
                 return
             g, s = divmod(v, S5)
-            i, hh = divmod(g, 2)
-            if hh == 0 and s == 0:
-                nmk_i = img.tile([P, 40], F32, name="nmk_i", tag="nmk")
-                rc_i = img.tile([P, PIX + 40], F32, name="rc_i", tag="rc")
-                nmk[i] = nmk_i
-                rc[i] = rc_i
+            if s == 0:
+                nmk_g = grp.tile([P, 20], F32, name="nmk_g", tag="nmk")
+                rsum_g = grp.tile([P, 20], F32, name="rsum_g", tag="rsum")
+                nmk[g] = nmk_g
+                rsum[g] = rsum_g
             zab = pza.tile([P, GW], F32, name="zab", tag="za")
             zat[v] = zab
             for t in range(4):
@@ -256,10 +258,8 @@ def tile_sralnet_pa_kernel(tc, x, centroids, out):
             if not 0 <= v < UNITS:
                 return
             g, s = divmod(v, S5)
-            i, hh = divmod(g, 2)
-            c = hh * 20 + s * 4
             nc.vector.tensor_reduce(
-                out=nmk[i][:, c : c + 4],
+                out=nmk[g][:, s * 4 : s * 4 + 4],
                 in_=zat[v][:].rearrange("p (t k) -> p t k", t=4),
                 axis=AX.X,
                 op=ALU.max,
@@ -270,72 +270,83 @@ def tile_sralnet_pa_kernel(tc, x, centroids, out):
             if not 0 <= v < UNITS:
                 return
             g, s = divmod(v, S5)
-            i, hh = divmod(g, 2)
+            ub = up.tile([P, GW], F32, name="ub", tag="u")
+            ut[v] = ub
             for t in range(4):
-                c = hh * 20 + s * 4 + t
+                c = s * 4 + t
                 nc.scalar.activation(
-                    out=junk_e[:],
+                    out=ub[:, t * P : (t + 1) * P],
                     in_=zat[v][:, t * P : (t + 1) * P],
                     func=ACTF.Exp,
-                    bias=nmk[i][:, c : c + 1],
+                    bias=nmk[g][:, c : c + 1],
                     scale=1.0,
-                    accum_out=rc[i][:, PIX + c : PIX + c + 1],
+                    accum_out=rsum[g][:, c : c + 1],
                 )
 
-        dat = {}
-        e2t = {}
-        cps = {}
-
-        def addt(out, in_a, in_b, real=False):
-            nc.tensor.matmul(out=out, lhsT=in_a, rhs=ident[:], is_transpose=not real, start=True, stop=False)
-            nc.tensor.matmul(out=out, lhsT=in_b, rhs=ident[:], is_transpose=True, start=False, stop=True)
-
-        ys = {}
-
-        def yadd(kind, v, rows, eng):
-            if not 0 <= v < UNITS or not eng:
+        def rrecip(g):
+            if not 0 <= g < GROUPS:
                 return
-            g, s = divmod(v, S5)
-            y = ypool.tile([P, GW], F32, name="y", tag="y")
-            ys[(kind, v)] = y
-            e = nc.vector if eng == "v" else nc.gpsimd
-            e.tensor_tensor(out=y[:], in0=z[g][:, s * GW : (s + 1) * GW], in1=rows[g][:], op=ALU.add)
+            ri = grp.tile([P, 20], F32, name="ri", tag="ri")
+            rinv[g] = ri
+            nc.vector.reciprocal(out=ri[:], in_=rsum[g][:])
 
-        def bring(bank, kind, v, zs, row, real):
-            if (kind, v) in ys:
-                y = ys[(kind, v)]
-                for t in range(4):
-                    nc.tensor.matmul(
-                        out=bank[:, t * P : (t + 1) * P],
-                        lhsT=y[:, t * P : (t + 1) * P],
-                        rhs=ident[:],
-                        is_transpose=not (real and t == 0),
-                        start=True,
-                        stop=True,
-                    )
-            else:
-                for t in range(4):
-                    addt(
-                        bank[:, t * P : (t + 1) * P],
-                        zs[:, t * P : (t + 1) * P],
-                        row[:, t * P : (t + 1) * P],
-                        real=(real and t == 0),
-                    )
+        et = {}
+        ptt = {}
+        cps = {}
+        cinv = {}
 
-        def da(v):
+        def dadd(v):
             if not 0 <= v < UNITS:
                 return
             g, s = divmod(v, S5)
-            dab = pdw.tile([P, GW], F32, name="dab", tag="dw")
-            dat[v] = dab
-            bring(dab, "d", v, z[g][:, s * GW : (s + 1) * GW], nm[g], REALD.get(v))
+            eb = ep.tile([P, GW], F32, name="eb", tag="e")
+            et[v] = eb
+            if DADD.get(v):
+                yb = ep.tile([P, GW], F32, name="yb", tag="y", bufs=2)
+                e = nc.vector if DADD.get(v) == "v" else nc.gpsimd
+                e.tensor_tensor(out=yb[:], in0=z[g][:, s * GW : (s + 1) * GW], in1=nm[g][:], op=ALU.add)
+                yt[v] = yb
+        yt = {}
+
+        def dpe(v):
+            if not 0 <= v < UNITS:
+                return
+            g, s = divmod(v, S5)
+            pb = ppt.tile([P, GW], F32, name="pb", tag="pt")
+            ptt[v] = pb
+            for t in range(4):
+                real = t < REALD.get(v, 0)
+                if v in yt:
+                    nc.tensor.matmul(
+                        out=pb[:, t * P : (t + 1) * P],
+                        lhsT=yt[v][:, t * P : (t + 1) * P],
+                        rhs=ident[:],
+                        is_transpose=not real,
+                        start=True,
+                        stop=True,
+                    )
+                else:
+                    nc.tensor.matmul(
+                        out=pb[:, t * P : (t + 1) * P],
+                        lhsT=z[g][:, s * GW + t * P : s * GW + (t + 1) * P],
+                        rhs=ident[:],
+                        is_transpose=not real,
+                        start=True,
+                        stop=False,
+                    )
+                    nc.tensor.matmul(
+                        out=pb[:, t * P : (t + 1) * P],
+                        lhsT=nm[g][:, t * P : (t + 1) * P],
+                        rhs=ident[:],
+                        is_transpose=True,
+                        start=False,
+                        stop=True,
+                    )
 
         def e2(v):
             if not 0 <= v < UNITS:
                 return
-            e2b = ep.tile([P, GW], F32, name="e2b", tag="e2")
-            e2t[v] = e2b
-            nc.scalar.activation(out=e2b[:], in_=dat[v][:], func=ACTF.Exp)
+            nc.scalar.activation(out=et[v][:], in_=ptt[v][:], func=ACTF.Exp)
 
         def cpart(g, ts):
             if not 0 <= g < GROUPS:
@@ -347,72 +358,53 @@ def tile_sralnet_pa_kernel(tc, x, centroids, out):
                 for s in range(S5):
                     nc.tensor.matmul(
                         out=cps[g][:, t * P : (t + 1) * P],
-                        lhsT=e2t[g * S5 + s][:, t * P : (t + 1) * P],
+                        lhsT=et[g * S5 + s][:, t * P : (t + 1) * P],
                         rhs=ident[:],
                         is_transpose=True,
                         start=(s == 0),
                         stop=(s == S5 - 1),
                     )
 
+        cbs = {}
+
         def ccopy(g):
             if not 0 <= g < GROUPS:
                 return
-            i, hh = divmod(g, 2)
-            nc.vector.tensor_copy(out=rc[i][:, hh * GW : (hh + 1) * GW], in_=cps[g][:])
+            cs = grp.tile([P, GW], F32, name="cs", tag="cs")
+            cbs[g] = cs
+            nc.scalar.copy(out=cs[:], in_=cps[g][:])
 
-        def logs(i):
-            nc.scalar.activation(out=rc[i][:], in_=rc[i][:], func=ACTF.Ln)
-
-        nhl = {}
-        beta = {}
-
-        def half_lse(g):
+        def crecip(g):
             if not 0 <= g < GROUPS:
                 return
-            i, hh = divmod(g, 2)
-            if hh == 0:
-                beta_i = img.tile([P, 40], F32, name="beta_i", tag="beta")
-                beta[i] = beta_i
-                nc.vector.tensor_tensor(out=beta_i[:], in0=nmk[i][:], in1=rc[i][:, PIX : PIX + 40], op=ALU.subtract)
-            nhlg = nmp.tile([P, GW], F32, name="nhlg", tag="nhl")
-            nhl[g] = nhlg
-            nc.vector.scalar_tensor_tensor(
-                out=nhlg[:],
-                in0=rc[i][:, hh * GW : (hh + 1) * GW],
-                scalar=-0.5,
-                in1=hm[g][:],
-                op0=ALU.mult,
-                op1=ALU.add,
-            )
+            ca = pmi.tile([P, GW], F32, name="ca", tag="mi")
+            for t in range(4):
+                nc.tensor.transpose(ca[:, t * P : (t + 1) * P], cbs[g][:, t * P : (t + 1) * P], ident[:])
+            ci = grp.tile([P, GW], F32, name="ci", tag="ci")
+            cinv[g] = ci
+            nc.vector.reciprocal(out=ci[:], in_=ca[:])
 
-        wtt = {}
-        at = {}
         acc = {}
 
-        def wt_(v):
+        def qmul(v):
             if not 0 <= v < UNITS:
                 return
             g, s = divmod(v, S5)
-            wb = pdw.tile([P, GW], F32, name="wb", tag="dw")
-            wtt[v] = wb
-            bring(wb, "w", v, z[g][:, s * GW : (s + 1) * GW], nhl[g], REALW.get(v))
-
-        def apass(v):
-            if not 0 <= v < UNITS:
-                return
-            g, s = divmod(v, S5)
-            i, hh = divmod(g, 2)
-            ab = ap_.tile([P, GW], F32, name="ab", tag="ab")
-            at[v] = ab
             for t in range(4):
-                c = hh * 20 + s * 4 + t
-                nc.scalar.activation(
-                    out=ab[:, t * P : (t + 1) * P],
-                    in_=wtt[v][:, t * P : (t + 1) * P],
-                    func=ACTF.Exp,
-                    bias=beta[i][:, c : c + 1],
-                    scale=2.0,
+                nc.vector.scalar_tensor_tensor(
+                    out=ut[v][:, t * P : (t + 1) * P],
+                    in0=ut[v][:, t * P : (t + 1) * P],
+                    scalar=rinv[g][:, s * 4 + t : s * 4 + t + 1],
+                    in1=et[v][:, t * P : (t + 1) * P],
+                    op0=ALU.mult,
+                    op1=ALU.mult,
                 )
+
+        def amul(v):
+            if not 0 <= v < UNITS:
+                return
+            e = nc.gpsimd if AMUL.get(v) == "g" else nc.vector
+            e.tensor_tensor(out=ut[v][:], in0=ut[v][:], in1=cinv[v // S5][:], op=ALU.mult)
 
         def prod(v):
             if not 0 <= v < UNITS:
@@ -421,10 +413,10 @@ def tile_sralnet_pa_kernel(tc, x, centroids, out):
             if s == 0:
                 accg = mul.tile([P, GW], F32, name="accg", tag="acc")
                 acc[g] = accg
-                nc.vector.tensor_scalar(out=accg[:], in0=at[v][:], scalar1=1.0, scalar2=None, op0=ALU.add)
+                nc.vector.tensor_scalar(out=accg[:], in0=ut[v][:], scalar1=1.0, scalar2=None, op0=ALU.add)
             else:
                 nc.vector.scalar_tensor_tensor(
-                    out=acc[g][:], in0=at[v][:], scalar=1.0, in1=acc[g][:], op0=ALU.add, op1=ALU.mult
+                    out=acc[g][:], in0=ut[v][:], scalar=1.0, in1=acc[g][:], op0=ALU.add, op1=ALU.mult
                 )
 
         mgs = {}
@@ -438,7 +430,7 @@ def tile_sralnet_pa_kernel(tc, x, centroids, out):
             mgs[g] = mg
             dst = mg[:].rearrange("p (k t) -> p k t", t=4)
             src = acc[g][:].rearrange("p (t k) -> p k t", t=4)
-            if g == GROUPS - 1:
+            if CAST == "s":
                 nc.scalar.copy(out=dst, in_=src)
             else:
                 nc.vector.tensor_copy(out=dst, in_=src)
@@ -538,9 +530,9 @@ def tile_sralnet_pa_kernel(tc, x, centroids, out):
             nc.scalar.activation(out=junk_w[:], in_=vp[:], func=ACTF.Square, accum_out=ssq[:, 0:1])
             pg = fin.tile([P, 16], F32, name="pg", tag="pg")
             nc.gpsimd.tensor_scalar(out=pg[:, 0:1], in0=ssq[:, 0:1], scalar1=EPS2, scalar2=None, op0=ALU.max)
+            nc.gpsimd.tensor_tensor(out=pg[:, 2:3], in0=pg[:, 0:1], in1=expo[:, 9:10], op=ALU.pow)
+            nc.gpsimd.tensor_tensor(out=qcol[:, 0:1], in0=ssq[:, 0:1], in1=pg[:, 2:3], op=ALU.mult)
             nc.gpsimd.tensor_tensor(out=pg[:, 1:2], in0=pg[:, 0:1], in1=expo[:, 8:9], op=ALU.pow)
-            nc.gpsimd.tensor_tensor(out=pg[:, 2:3], in0=ssq[:, 0:1], in1=pg[:, 1:2], op=ALU.mult)
-            nc.gpsimd.tensor_tensor(out=qcol[:, 0:1], in0=pg[:, 2:3], in1=pg[:, 1:2], op=ALU.mult)
             fst[i] = (sm, pg, vp)
 
         def final_b(i):
@@ -549,7 +541,6 @@ def tile_sralnet_pa_kernel(tc, x, centroids, out):
             nc.tensor.matmul(out=tot[:], lhsT=ones[:], rhs=qcol[:], start=True, stop=True)
             nc.vector.tensor_scalar(out=sm[:, 1:2], in0=tot[:, 0:1], scalar1=EPS2, scalar2=None, op0=ALU.max)
             nc.gpsimd.tensor_tensor(out=pg[:, 3:4], in0=sm[:, 1:2], in1=expo[:, 8:9], op=ALU.pow)
-            nc.gpsimd.tensor_tensor(out=pg[:, 4:5], in0=pg[:, 3:4], in1=pg[:, 1:2], op=ALU.mult)
 
         def final_c(i):
             sm, pg, vp = fst[i]
@@ -557,9 +548,10 @@ def tile_sralnet_pa_kernel(tc, x, centroids, out):
             nc.vector.tensor_scalar(
                 out=o[:].rearrange("p (q j) -> p q j", j=4),
                 in0=vp[:].rearrange("p (j q) -> p q j", j=4),
-                scalar1=pg[:, 4:5],
-                scalar2=None,
+                scalar1=pg[:, 1:2],
+                scalar2=pg[:, 3:4],
                 op0=ALU.mult,
+                op1=ALU.mult,
             )
             nc.sync.dma_start(out=out[i].rearrange("(k c) -> k c", c=CH), in_=o[:])
 
@@ -568,70 +560,67 @@ def tile_sralnet_pa_kernel(tc, x, centroids, out):
             for b in range(4):
                 XT[steps[b]] = (n, b)
 
-        PU = LW + 2
-        for u in range(-9, UNITS + LW + 16):
+        PR = LQ + AL + 1
+        for u in range(-9, UNITS + PR + 16):
+            if HO == 1 and u == -9:
+                wprep()
             if (u + 9) % 5 < 3 and 0 <= (u + 9) // 5 < GROUPS:
                 if (u + 9) % 5 < 2:
                     regroup((u + 9) // 5, (u + 9) % 5)
                 else:
                     xquant((u + 9) // 5)
-            if u == -7:
+            if HO == 0 and u == -7:
                 wprep()
             za(u + 1)
             kmax(u + 1)
             e1(u)
-            if ZP == 0:
-                zmx(u + 6)
+            zmx(u + 6)
             if u % 5 == 3:
                 smax((u + 2) // 5, 0)
             if u % 5 == 4:
                 smax((u + 1) // 5, 1)
             if u % 5 == 0:
                 smax(u // 5, 2)
-            da(u - 1)
-            if ZP == 1:
-                zmx(u + 6)
-            for i in range(IMAGES):
-                if u == 10 * i + LH:
-                    half_lse(2 * i)
-                if u == 10 * i + LH + 1:
-                    half_lse(2 * i + 1)
-            yadd("w", u - LW + YL, nhl, WADD.get(u - LW + YL))
+            if QP == 0:
+                qmul(u - LQ)
             if u % 5 == 0:
                 smax(u // 5, 3)
-            yadd("d", u, nm, DADD.get(u))
-            e2(u - 2)
-            if u % 5 == 2:
-                cpart((u - 7) // 5, (0, 1))
-            if u % 5 == 3:
-                cpart((u - 8) // 5, (2, 3))
+            dadd(u - LD)
+            dpe(u - LE + 1)
+            e2(u - LE)
+            if (u - LE) % 5 == 0:
+                cpart((u - LE - 5) // 5, (0, 1))
+            if (u - LE) % 5 == 1:
+                cpart((u - LE - 6) // 5, (2, 3))
             if u % 5 == CC % 5:
-                ccopy((u - CC) // 5)
-            for i in range(IMAGES):
-                if u == 10 * i + LL:
-                    logs(i)
-            wt_(u - LW)
-            prod(u - PU)
-            if (u - PU) % 5 == 0:
-                cast((u - PU - 5) // 5)
-            if (u - PU) % 5 == 1:
-                mquant((u - PU - 6) // 5)
-            apass(u - LW - 1)
+                crecip((u - CC) // 5)
+            if u % 5 == 1:
+                rrecip((u - 6) // 5)
+            if QP == 1:
+                qmul(u - LQ)
+            if u % 5 == (CC - 1) % 5:
+                ccopy((u - CC + 1) // 5)
+            amul(u - LQ - AL)
+            prod(u - PR)
+            if (u - PR) % 5 == 0:
+                cast((u - PR - 5) // 5)
+            if (u - PR) % 5 == 1:
+                mquant((u - PR - 6) // 5)
             if u in XT:
                 n, b = XT[u]
-                xt(n, b, XTE)
+                xt(n, b, XTE.get(n, 0))
                 if b == 1:
                     x2quant(n, 0)
                 if b == 3:
                     x2quant(n, 1)
             for i in range(IMAGES):
-                if u == 10 * i + PU + 10:
+                if u == 10 * i + PR + 10:
                     msum(i)
-                if u == 10 * i + PU + 12:
+                if u == 10 * i + PR + 12:
                     final_mm(i)
-                if u == 10 * i + PU + 13:
+                if u == 10 * i + PR + 13:
                     final_a(i)
-                if u == 10 * i + PU + FB:
+                if u == 10 * i + PR + FB:
                     final_b(i)
-                if u == 10 * i + PU + FC:
+                if u == 10 * i + PR + FC:
                     final_c(i)

@@ -23,31 +23,44 @@ GW = 512
 GROUPS = IMAGES * PIX // GW
 UNITS = GROUPS * S5
 EPS2 = 1e-24
-REP = 2
+P0S = 1
+NES = 0
+RQ = {1: 4, 2: 4, 3: 4, 4: 4, 5: 4, 6: 4, 7: 4}
+IV = 3
+LA0 = 16
+PC = 11
+CD = 1
+CE = 2
+LA = 17
+CB = 's'
+REP = 1
 HO = 0
-RH = 0
+RH = 1
 SB = 0
+NZA = 2
 DW = 2
 ZT = 2
-REALZ = {}
-REALD = {10: 1, 11: 1, 12: 1, 13: 1, 14: 1, 15: 1, 16: 1, 17: 1, 18: 1, 19: 1, 20: 1, 21: 1, 22: 1, 23: 1, 24: 1, 25: 1, 26: 1, 27: 1, 28: 1, 29: 1}
+ZC = 0
+KL = 1
+REALZ = {0: 1, 1: 1, 2: 1, 3: 1, 4: 1, 5: 1, 6: 1, 7: 1, 8: 1, 9: 1, 10: 1, 11: 1, 12: 1, 13: 1, 14: 1, 15: 1, 16: 1, 17: 1, 18: 1, 19: 1, 20: 1, 21: 1, 22: 1, 23: 1, 24: 1, 25: 1, 26: 1, 27: 1, 28: 1, 29: 1, 30: 1, 31: 1, 32: 1, 33: 1, 34: 1, 35: 1}
+REALD = {10: 1, 11: 1, 12: 1, 13: 1, 14: 1, 15: 1, 16: 1, 17: 1, 18: 1, 19: 1}
 KE = 2
-LE = 3
+LE = 4
 LD = 2
-EB = 14
-UB = 16
-LQ = 10
-AL = 1
-CC = 11
+EB = 13
+UB = 19
+LQ = 7
+AL = 2
+CC = 10
 FB = 18
-FC = 19
+FC = 20
 QP = 0
 CAST = 's'
 XTE = {0: 0, 1: 0, 2: 0, 3: 0}
-XTS = [[1, 2, 6, 7], [11, 12, 16, 17], [31, 32, 36, 37], [41, 42, 46, 47]]
-DADD = {}
-AMUL = {}
-REG = {6: 's', 7: 's'}
+XTS = [[6, 8, 11, 13], [16, 18, 21, 23], [26, 28, 31, 33], [36, 38, 41, 43]]
+DADD = {0: 'g', 4: 'g', 8: 'g', 12: 'g', 16: 'g'}
+AMUL = {0: 'g', 4: 'g', 8: 'g', 12: 'g', 16: 'g'}
+RG = {0: 3, 1: 3, 2: 3, 3: 3, 4: 3, 5: 3, 6: 3, 7: 3}
 ZCOPY = {0: 's', 1: 's', 2: 's', 3: 's', 4: 's', 5: 's', 6: 's', 7: 's', 8: 's', 9: 's', 10: 's', 11: 's', 12: 's', 13: 's', 14: 's', 15: 's', 16: 's', 17: 's', 18: 's', 19: 's', 20: 's', 21: 's', 22: 's', 23: 's', 24: 's', 25: 's', 26: 's', 27: 's', 28: 's', 29: 's', 30: 's', 31: 's', 32: 's', 33: 's', 34: 's', 35: 's', 36: 's', 37: 's', 38: 's', 39: 's'}
 
 FLOPS = 2 * IMAGES * PIX * M * CH + 2 * IMAGES * K * CH * PIX
@@ -61,14 +74,15 @@ def tile_sralnet_pa_kernel(tc, x, centroids, out):
         xgp = ctx.enter_context(tc.tile_pool(name="xgp", bufs=2))
         xq1 = ctx.enter_context(tc.tile_pool(name="xq1", bufs=2))
         xq2 = ctx.enter_context(tc.tile_pool(name="xq2", bufs=3))
-        zp = ctx.enter_context(tc.tile_pool(name="zp", bufs=4))
+        zp = ctx.enter_context(tc.tile_pool(name="zp", bufs=3))
         ep = ctx.enter_context(tc.tile_pool(name="ep", bufs=EB))
         up = ctx.enter_context(tc.tile_pool(name="up", bufs=UB))
         tmp = ctx.enter_context(tc.tile_pool(name="tmp", bufs=1))
         grp = ctx.enter_context(tc.tile_pool(name="grp", bufs=3))
+        img = ctx.enter_context(tc.tile_pool(name="img", bufs=2))
         mul = ctx.enter_context(tc.tile_pool(name="mul", bufs=3))
         fin = ctx.enter_context(tc.tile_pool(name="fin", bufs=2))
-        pza = ctx.enter_context(tc.psum_pool(name="pza", bufs=2))
+        pza = ctx.enter_context(tc.psum_pool(name="pza", bufs=NZA))
         ppt = ctx.enter_context(tc.psum_pool(name="ppt", bufs=DW))
         pzt = ctx.enter_context(tc.psum_pool(name="pzt", bufs=ZT))
         pmi = ctx.enter_context(tc.psum_pool(name="pmi", bufs=2))
@@ -105,18 +119,21 @@ def tile_sralnet_pa_kernel(tc, x, centroids, out):
         xsc1 = {}
         xg1s = {}
 
-        def regroup(g, e):
+        def regroup(g, q):
             n = g // 2
             h = g % 2
-            if e == 0:
+            if q == 0:
                 xg1 = xgp.tile([P, 4 * GW], BF16, name="xg1", tag="xg1", align_bytes=64)
                 xg1s[g] = xg1
-            src = xs[n][:].rearrange("p (j a r e) -> p e a r j", j=4, a=4, r=P, e=2)
-            dst = xg1s[g][:].rearrange("p (a e r j) -> p e a r j", a=2, e=2, r=P, j=4)
-            if REG.get(g) == "s" or (g == 0 and e < RH):
-                nc.scalar.copy(out=dst[:, e], in_=src[:, e, 2 * h : 2 * h + 2])
+            a, e = divmod(q, 2)
+            src = xs[n][:].rearrange("p (j a r e) -> p a e r j", j=4, a=4, r=P, e=2)[:, 2 * h + a, e]
+            dst = xg1s[g][:].rearrange("p (a e r j) -> p a e r j", a=2, e=2, r=P, j=4)[:, a, e]
+            if g > 0 and q < RQ.get(g, 0):
+                nc.gpsimd.tensor_scalar(out=dst, in0=src, scalar1=1.0, scalar2=0.0, op0=ALU.mult, op1=ALU.add)
+            elif (g > 0 and q >= RG.get(g, 4)) or (g == 0 and q < RH):
+                nc.scalar.copy(out=dst, in_=src)
             else:
-                nc.vector.tensor_copy(out=dst[:, e], in_=src[:, e, 2 * h : 2 * h + 2])
+                nc.vector.tensor_copy(out=dst, in_=src)
 
         def xquant(g):
             n = g // 2
@@ -194,8 +211,17 @@ def tile_sralnet_pa_kernel(tc, x, centroids, out):
                 zg = zp.tile([P, S5 * GW], F32, name="zg", tag="z")
                 z[g] = zg
             zt = pzt.tile([P, GW], F32, name="zt", tag="zt")
+            ztt[v] = zt
             for again in range(REP if g > 0 else 1):
                 mx1(zt, g, s)
+
+        ztt = {}
+
+        def zcp(v):
+            if not 0 <= v < UNITS:
+                return
+            g, s = divmod(v, S5)
+            zt = ztt[v]
             dst = z[g][:, s * GW : (s + 1) * GW]
             if ZCOPY.get(v) == "s":
                 nc.scalar.activation(out=dst, in_=zt[:], func=ACTF.Identity, bias=bcol[:, s : s + 1], scale=1.0)
@@ -225,7 +251,10 @@ def tile_sralnet_pa_kernel(tc, x, centroids, out):
                 t1 = sm_t[g]
                 nmg = grp.tile([P, GW], F32, name="nmg", tag="nm")
                 nm[g] = nmg
-                nc.vector.tensor_scalar(out=nmg[:], in0=t1[:, GW : 2 * GW], scalar1=-1.0, scalar2=None, op0=ALU.mult)
+                if NES:
+                    nc.scalar.activation(out=nmg[:], in_=t1[:, GW : 2 * GW], func=ACTF.Copy, scale=-1.0)
+                else:
+                    nc.vector.tensor_scalar(out=nmg[:], in0=t1[:, GW : 2 * GW], scalar1=-1.0, scalar2=None, op0=ALU.mult)
 
         nmk = {}
         rsum = {}
@@ -365,24 +394,41 @@ def tile_sralnet_pa_kernel(tc, x, centroids, out):
                         stop=(s == S5 - 1),
                     )
 
-        cbs = {}
+        cli = {}
 
         def ccopy(g):
             if not 0 <= g < GROUPS:
                 return
-            cs = grp.tile([P, GW], F32, name="cs", tag="cs")
-            cbs[g] = cs
-            nc.scalar.copy(out=cs[:], in_=cps[g][:])
+            h = g % 2
+            if h == 0:
+                cl = img.tile([P, 2 * GW], F32, name="cl", tag="cl")
+                cli[g // 2] = cl
+            if h == 0 or g // 2 < IV:
+                nc.scalar.copy(out=cli[g // 2][:, h * GW : (h + 1) * GW], in_=cps[g][:])
 
-        def crecip(g):
+        def invert(i):
+            cl = cli[i]
+            nc.scalar.activation(out=cl[:, 0:GW], in_=cl[:, 0:GW], func=ACTF.Ln)
+            nc.scalar.activation(out=cl[:, GW : 2 * GW], in_=cps[2 * i + 1][:], func=ACTF.Ln)
+            nc.scalar.activation(out=cl[:], in_=cl[:], func=ACTF.Exp, scale=-1.0)
+
+        def cback(g):
             if not 0 <= g < GROUPS:
                 return
+            h = g % 2
             ca = pmi.tile([P, GW], F32, name="ca", tag="mi")
             for t in range(4):
-                nc.tensor.transpose(ca[:, t * P : (t + 1) * P], cbs[g][:, t * P : (t + 1) * P], ident[:])
+                nc.tensor.transpose(
+                    ca[:, t * P : (t + 1) * P], cli[g // 2][:, h * GW + t * P : h * GW + (t + 1) * P], ident[:]
+                )
             ci = grp.tile([P, GW], F32, name="ci", tag="ci")
             cinv[g] = ci
-            nc.vector.reciprocal(out=ci[:], in_=ca[:])
+            if g // 2 < IV:
+                nc.vector.reciprocal(out=ci[:], in_=ca[:])
+            elif CB == "v":
+                nc.vector.tensor_copy(out=ci[:], in_=ca[:])
+            else:
+                nc.scalar.copy(out=ci[:], in_=ca[:])
 
         acc = {}
 
@@ -413,7 +459,10 @@ def tile_sralnet_pa_kernel(tc, x, centroids, out):
             if s == 0:
                 accg = mul.tile([P, GW], F32, name="accg", tag="acc")
                 acc[g] = accg
-                nc.vector.tensor_scalar(out=accg[:], in0=ut[v][:], scalar1=1.0, scalar2=None, op0=ALU.add)
+                if P0S:
+                    nc.scalar.activation(out=accg[:], in_=ut[v][:], func=ACTF.Identity, bias=1.0, scale=1.0)
+                else:
+                    nc.vector.tensor_scalar(out=accg[:], in0=ut[v][:], scalar1=1.0, scalar2=None, op0=ALU.add)
             else:
                 nc.vector.scalar_tensor_tensor(
                     out=acc[g][:], in0=ut[v][:], scalar=1.0, in1=acc[g][:], op0=ALU.add, op1=ALU.mult
@@ -430,7 +479,9 @@ def tile_sralnet_pa_kernel(tc, x, centroids, out):
             mgs[g] = mg
             dst = mg[:].rearrange("p (k t) -> p k t", t=4)
             src = acc[g][:].rearrange("p (t k) -> p k t", t=4)
-            if CAST == "s":
+            if CAST == "g":
+                nc.gpsimd.tensor_scalar(out=dst, in0=src, scalar1=1.0, scalar2=0.0, op0=ALU.mult, op1=ALU.add)
+            elif CAST == "s":
                 nc.scalar.copy(out=dst, in_=src)
             else:
                 nc.vector.tensor_copy(out=dst, in_=src)
@@ -560,21 +611,33 @@ def tile_sralnet_pa_kernel(tc, x, centroids, out):
             for b in range(4):
                 XT[steps[b]] = (n, b)
 
-        PR = LQ + AL + 1
-        for u in range(-9, UNITS + PR + 16):
-            if HO == 1 and u == -9:
+        PR = LA + 1
+        for u in range(-11, UNITS + PR + 16):
+            if HO == 1 and u == -11:
                 wprep()
-            if (u + 9) % 5 < 3 and 0 <= (u + 9) // 5 < GROUPS:
-                if (u + 9) % 5 < 2:
-                    regroup((u + 9) // 5, (u + 9) % 5)
+            if 0 <= (u + 11) // 5 < GROUPS:
+                if (u + 11) % 5 < 4:
+                    regroup((u + 11) // 5, (u + 11) % 5)
                 else:
-                    xquant((u + 9) // 5)
+                    xquant((u + 11) // 5)
             if HO == 0 and u == -7:
                 wprep()
-            za(u + 1)
-            kmax(u + 1)
-            e1(u)
+            if u + KL >= 5:
+                za(u + KL)
+            if u + 1 >= 5:
+                kmax(u + 1)
+            if u >= 5:
+                e1(u)
+            if 0 <= u + KE + 1 < 5:
+                za(u + KE + 1)
+                kmax(u + KE + 1)
+            if 0 <= u + KE < 5:
+                e1(u + KE)
+            if ZC == 1 and u + 5 >= 5:
+                zcp(u + 5)
             zmx(u + 6)
+            if ZC == 0 or u + 6 < 5:
+                zcp(u + 6)
             if u % 5 == 3:
                 smax((u + 2) // 5, 0)
             if u % 5 == 4:
@@ -592,20 +655,33 @@ def tile_sralnet_pa_kernel(tc, x, centroids, out):
                 cpart((u - LE - 5) // 5, (0, 1))
             if (u - LE) % 5 == 1:
                 cpart((u - LE - 6) // 5, (2, 3))
-            if u % 5 == CC % 5:
-                crecip((u - CC) // 5)
+            for g in range(2 * IV):
+                if u == 5 * g + CC + 1:
+                    cback(g)
+            for i in range(IV, IMAGES):
+                if u == 10 * i + 5 + PC:
+                    invert(i)
+                if u == 10 * i + 5 + PC + CD:
+                    cback(2 * i)
+                if u == 10 * i + 5 + PC + CD + CE:
+                    cback(2 * i + 1)
             if u % 5 == 1:
                 rrecip((u - 6) // 5)
             if QP == 1:
                 qmul(u - LQ)
-            if u % 5 == (CC - 1) % 5:
-                ccopy((u - CC + 1) // 5)
-            amul(u - LQ - AL)
-            prod(u - PR)
-            if (u - PR) % 5 == 0:
-                cast((u - PR - 5) // 5)
-            if (u - PR) % 5 == 1:
-                mquant((u - PR - 6) // 5)
+            if u % 5 == CC % 5:
+                ccopy((u - CC) // 5)
+            for v in range(UNITS):
+                if u == v + (LA0 if v < 10 * IV else LA):
+                    amul(v)
+            for g in range(GROUPS):
+                p0 = 5 * g + (LA0 if g < 2 * IV else LA) + 1
+                if 0 <= u - p0 < 5:
+                    prod(5 * g + u - p0)
+                if u == p0 + 5:
+                    cast(g)
+                if u == p0 + 6:
+                    mquant(g)
             if u in XT:
                 n, b = XT[u]
                 xt(n, b, XTE.get(n, 0))
@@ -614,13 +690,14 @@ def tile_sralnet_pa_kernel(tc, x, centroids, out):
                 if b == 3:
                     x2quant(n, 1)
             for i in range(IMAGES):
-                if u == 10 * i + PR + 10:
+                p0 = 10 * i + (LA0 if i < IV else LA) + 1
+                if u == p0 + 10:
                     msum(i)
-                if u == 10 * i + PR + 12:
+                if u == p0 + 12:
                     final_mm(i)
-                if u == 10 * i + PR + 13:
+                if u == p0 + 13:
                     final_a(i)
-                if u == 10 * i + PR + FB:
+                if u == p0 + FB:
                     final_b(i)
-                if u == 10 * i + PR + FC:
+                if u == p0 + FC:
                     final_c(i)

@@ -23,45 +23,40 @@ GW = 512
 GROUPS = IMAGES * PIX // GW
 UNITS = GROUPS * S5
 EPS2 = 1e-24
-P0S = 1
-NES = 0
-RQ = {1: 4, 2: 4, 3: 4, 4: 4, 5: 4, 6: 4, 7: 4}
-IV = 3
-LA0 = 16
-PC = 11
-CD = 1
-CE = 2
-LA = 17
-CB = 's'
-REP = 1
-HO = 0
-RH = 1
-SB = 0
+SR = False
 NZA = 2
 DW = 2
 ZT = 2
+NMI = 1
+NRC = 1
+XTT = 1
+RQ = {}
+RG = {0: 3, 1: 3, 2: 2, 3: 2, 4: 2, 5: 2, 6: 2, 7: 2}
+RH = 2
+SB = 0
+P0S = 1
+NES = 0
+REP = 1
 ZC = 0
 KL = 1
-REALZ = {0: 1, 1: 1, 2: 1, 3: 1, 4: 1, 5: 1, 6: 1, 7: 1, 8: 1, 9: 1, 10: 1, 11: 1, 12: 1, 13: 1, 14: 1, 15: 1, 16: 1, 17: 1, 18: 1, 19: 1, 20: 1, 21: 1, 22: 1, 23: 1, 24: 1, 25: 1, 26: 1, 27: 1, 28: 1, 29: 1, 30: 1, 31: 1, 32: 1, 33: 1, 34: 1, 35: 1}
-REALD = {10: 1, 11: 1, 12: 1, 13: 1, 14: 1, 15: 1, 16: 1, 17: 1, 18: 1, 19: 1}
-KE = 2
-LE = 4
-LD = 2
-EB = 13
-UB = 19
-LQ = 7
-AL = 2
-CC = 10
-FB = 18
-FC = 20
-QP = 0
+KE = 0
+REALZ = {5: 1, 6: 1, 7: 1, 8: 1, 9: 1, 10: 1, 11: 1, 12: 1, 13: 1, 14: 1, 15: 1, 16: 1, 17: 1, 18: 1, 19: 1, 20: 1, 21: 1, 22: 1, 23: 1, 24: 1, 25: 1, 26: 1, 27: 1, 28: 1, 29: 1, 30: 1, 31: 1, 32: 1, 33: 1, 34: 1, 35: 1, 36: 1, 37: 1, 38: 1, 39: 1}
+REALD = {0: 1, 1: 1, 2: 1, 3: 1, 4: 1, 5: 1, 6: 1, 7: 1, 8: 1, 9: 1, 10: 1, 11: 1, 12: 1, 13: 1, 14: 1, 15: 1, 16: 1, 17: 1, 18: 1, 19: 1, 20: 1, 21: 1, 22: 1, 23: 1, 24: 1, 25: 1, 26: 1, 27: 1, 28: 1, 29: 1, 30: 1, 31: 1, 32: 1, 33: 1, 34: 1, 35: 1, 36: 1, 37: 1, 38: 1, 39: 1}
+LE = 3
+EB = 11
+UB = 17
+LQ = 6
+LA = 15
+PD = 1
+CC = 11
+CL = 1
+FB = 8
+FC = 11
 CAST = 's'
 XTE = {0: 0, 1: 0, 2: 0, 3: 0}
-XTS = [[6, 8, 11, 13], [16, 18, 21, 23], [26, 28, 31, 33], [36, 38, 41, 43]]
-DADD = {0: 'g', 4: 'g', 8: 'g', 12: 'g', 16: 'g'}
-AMUL = {0: 'g', 4: 'g', 8: 'g', 12: 'g', 16: 'g'}
-RG = {0: 3, 1: 3, 2: 3, 3: 3, 4: 3, 5: 3, 6: 3, 7: 3}
-ZCOPY = {0: 's', 1: 's', 2: 's', 3: 's', 4: 's', 5: 's', 6: 's', 7: 's', 8: 's', 9: 's', 10: 's', 11: 's', 12: 's', 13: 's', 14: 's', 15: 's', 16: 's', 17: 's', 18: 's', 19: 's', 20: 's', 21: 's', 22: 's', 23: 's', 24: 's', 25: 's', 26: 's', 27: 's', 28: 's', 29: 's', 30: 's', 31: 's', 32: 's', 33: 's', 34: 's', 35: 's', 36: 's', 37: 's', 38: 's', 39: 's'}
+XTS = [[1, 3, 6, 8], [11, 13, 16, 18], [21, 23, 26, 28], [31, 33, 36, 38]]
+ZCOPY = {0: 's', 1: 's', 2: 's', 3: 's', 4: 's', 5: 'v', 6: 's', 7: 's', 8: 'v', 9: 's', 10: 's', 11: 'v', 12: 's', 13: 's', 14: 's', 15: 's', 16: 's', 17: 's', 18: 's', 19: 's', 20: 's', 21: 's', 22: 's', 23: 's', 24: 's', 25: 's', 26: 's', 27: 's', 28: 's', 29: 's', 30: 's', 31: 's', 32: 's', 33: 's', 34: 's', 35: 's', 36: 's', 37: 's', 38: 's', 39: 's'}
+QE = {0: 'g', 1: 'g', 2: 'g', 3: 'v', 4: 'g', 5: 'g', 6: 'g', 7: 'v', 8: 'g', 9: 'g', 10: 'g', 11: 'g', 12: 'g', 13: 'g', 14: 'g', 15: 'g', 16: 'g', 17: 'g', 18: 'g', 19: 'g', 20: 'g', 21: 'g', 22: 'g', 23: 'g', 24: 'g', 25: 'g', 26: 'g', 27: 'g', 28: 'g', 29: 'g', 30: 'g', 31: 'g', 32: 'g', 33: 'g', 34: 'g', 35: 'g', 36: 'g', 37: 'g', 38: 'g', 39: 'g'}
 
 FLOPS = 2 * IMAGES * PIX * M * CH + 2 * IMAGES * K * CH * PIX
 
@@ -79,13 +74,13 @@ def tile_sralnet_pa_kernel(tc, x, centroids, out):
         up = ctx.enter_context(tc.tile_pool(name="up", bufs=UB))
         tmp = ctx.enter_context(tc.tile_pool(name="tmp", bufs=1))
         grp = ctx.enter_context(tc.tile_pool(name="grp", bufs=3))
-        img = ctx.enter_context(tc.tile_pool(name="img", bufs=2))
         mul = ctx.enter_context(tc.tile_pool(name="mul", bufs=3))
         fin = ctx.enter_context(tc.tile_pool(name="fin", bufs=2))
         pza = ctx.enter_context(tc.psum_pool(name="pza", bufs=NZA))
         ppt = ctx.enter_context(tc.psum_pool(name="ppt", bufs=DW))
         pzt = ctx.enter_context(tc.psum_pool(name="pzt", bufs=ZT))
-        pmi = ctx.enter_context(tc.psum_pool(name="pmi", bufs=2))
+        prc = ctx.enter_context(tc.psum_pool(name="prc", bufs=NRC))
+        pmi = ctx.enter_context(tc.psum_pool(name="pmi", bufs=NMI))
         ctx.enter_context(tc.manual_schedule())
 
         xs = {}
@@ -163,30 +158,85 @@ def tile_sralnet_pa_kernel(tc, x, centroids, out):
                 in_=wg[:, s * 512 : (s + 1) * 512],
             )
 
-        def wprep():
+        wts = {}
+
+        def wtrans(s):
             cenw = cen[:].bitcast(F32).rearrange("p (s q u) -> p s u q", s=S5, u=2)
-            for s in range(S5):
+            if s < 1:
                 wt = pmi.tile([P, 256], F32, name="wt", tag="mi")
-                for u in range(2):
-                    nc.tensor.transpose(wt[:, u * P : (u + 1) * P], cenw[:, s, u], ident[:])
-                nc.vector.tensor_scalar(
-                    out=wg[:, s * 512 : (s + 1) * 512].rearrange("p (k u e) -> p k u e", u=2, e=2),
-                    in0=wt[:].bitcast(BF16).rearrange("p (u k e) -> p k u e", u=2, e=2),
-                    scalar1=200.0,
-                    scalar2=None,
-                    op0=ALU.mult,
-                )
-                if s > 0:
-                    wquant(s - 1)
-            wquant(S5 - 1)
-            for s in range(S5):
+            elif s < 2:
+                wt = prc.tile([P, 256], F32, name="wt", tag="rc")
+            elif s < 4:
+                wt = ppt.tile([P, 256], F32, name="wt", tag="pt")
+            else:
+                wt = pza.tile([P, 256], F32, name="wt", tag="za")
+            wts[s] = wt
+            for u in range(2):
+                nc.tensor.transpose(wt[:, u * P : (u + 1) * P], cenw[:, s, u], ident[:])
+
+        def wcopy(s):
+            nc.vector.tensor_scalar(
+                out=wg[:, s * 512 : (s + 1) * 512].rearrange("p (k u e) -> p k u e", u=2, e=2),
+                in0=wts[s][:].bitcast(BF16).rearrange("p (u k e) -> p k u e", u=2, e=2),
+                scalar1=200.0,
+                scalar2=None,
+                op0=ALU.mult,
+            )
+
+        def bias(ss):
+            for s in ss:
                 nc.scalar.activation(
                     out=junk_w[:], in_=cen[:, s * CH : (s + 1) * CH], func=ACTF.Square, accum_out=n2[:, s : s + 1]
                 )
-            nc.gpsimd.tensor_tensor(out=brt[:, 0:S5], in0=n2[:, 0:S5], in1=expo[:, 0:S5], op=ALU.pow)
+            a, b = ss[0], ss[-1] + 1
+            nc.gpsimd.tensor_tensor(out=brt[:, a:b], in0=n2[:, a:b], in1=expo[:, a:b], op=ALU.pow)
             nc.gpsimd.tensor_scalar(
-                out=bcol[:, 0:S5], in0=brt[:, 0:S5], scalar1=-100.0, scalar2=None, op0=ALU.mult
+                out=bcol[:, a:b], in0=brt[:, a:b], scalar1=-100.0, scalar2=None, op0=ALU.mult
             )
+
+        def head():
+            for s in range(S5):
+                wtrans(s)
+            wcopy(0)
+            wcopy(1)
+            wquant(0)
+            bias((0, 1))
+            for q in range(4):
+                regroup(0, q)
+            wquant(1)
+            wcopy(2)
+            xquant(0)
+            bias((2, 3, 4))
+            zmx(0)
+            zmx(1)
+            wcopy(3)
+            wquant(2)
+            zcp(0)
+            wcopy(4)
+            wquant(3)
+            zcp(1)
+            wquant(4)
+            if KE > 0:
+                za(0)
+            zmx(2)
+            zcp(2)
+            regroup(1, 0)
+            regroup(1, 1)
+            regroup(1, 2)
+            if KE > 0:
+                kmax(0)
+                za(1)
+            zmx(3)
+            zcp(3)
+            regroup(1, 3)
+            if KE > 0:
+                e1(0)
+                kmax(1)
+            xquant(1)
+            zmx(4)
+            zcp(4)
+            if KE > 0:
+                e1(1)
 
         z = {}
 
@@ -210,7 +260,10 @@ def tile_sralnet_pa_kernel(tc, x, centroids, out):
             if s == 0:
                 zg = zp.tile([P, S5 * GW], F32, name="zg", tag="z")
                 z[g] = zg
-            zt = pzt.tile([P, GW], F32, name="zt", tag="zt")
+            if v in (1, 3):
+                zt = ppt.tile([P, GW], F32, name="zt", tag="pt")
+            else:
+                zt = pzt.tile([P, GW], F32, name="zt", tag="zt")
             ztt[v] = zt
             for again in range(REP if g > 0 else 1):
                 mx1(zt, g, s)
@@ -324,19 +377,6 @@ def tile_sralnet_pa_kernel(tc, x, centroids, out):
         cps = {}
         cinv = {}
 
-        def dadd(v):
-            if not 0 <= v < UNITS:
-                return
-            g, s = divmod(v, S5)
-            eb = ep.tile([P, GW], F32, name="eb", tag="e")
-            et[v] = eb
-            if DADD.get(v):
-                yb = ep.tile([P, GW], F32, name="yb", tag="y", bufs=2)
-                e = nc.vector if DADD.get(v) == "v" else nc.gpsimd
-                e.tensor_tensor(out=yb[:], in0=z[g][:, s * GW : (s + 1) * GW], in1=nm[g][:], op=ALU.add)
-                yt[v] = yb
-        yt = {}
-
         def dpe(v):
             if not 0 <= v < UNITS:
                 return
@@ -345,37 +385,29 @@ def tile_sralnet_pa_kernel(tc, x, centroids, out):
             ptt[v] = pb
             for t in range(4):
                 real = t < REALD.get(v, 0)
-                if v in yt:
-                    nc.tensor.matmul(
-                        out=pb[:, t * P : (t + 1) * P],
-                        lhsT=yt[v][:, t * P : (t + 1) * P],
-                        rhs=ident[:],
-                        is_transpose=not real,
-                        start=True,
-                        stop=True,
-                    )
-                else:
-                    nc.tensor.matmul(
-                        out=pb[:, t * P : (t + 1) * P],
-                        lhsT=z[g][:, s * GW + t * P : s * GW + (t + 1) * P],
-                        rhs=ident[:],
-                        is_transpose=not real,
-                        start=True,
-                        stop=False,
-                    )
-                    nc.tensor.matmul(
-                        out=pb[:, t * P : (t + 1) * P],
-                        lhsT=nm[g][:, t * P : (t + 1) * P],
-                        rhs=ident[:],
-                        is_transpose=True,
-                        start=False,
-                        stop=True,
-                    )
+                nc.tensor.matmul(
+                    out=pb[:, t * P : (t + 1) * P],
+                    lhsT=z[g][:, s * GW + t * P : s * GW + (t + 1) * P],
+                    rhs=ident[:],
+                    is_transpose=not real,
+                    start=True,
+                    stop=False,
+                )
+                nc.tensor.matmul(
+                    out=pb[:, t * P : (t + 1) * P],
+                    lhsT=nm[g][:, t * P : (t + 1) * P],
+                    rhs=ident[:],
+                    is_transpose=True,
+                    start=False,
+                    stop=True,
+                )
 
         def e2(v):
             if not 0 <= v < UNITS:
                 return
-            nc.scalar.activation(out=et[v][:], in_=ptt[v][:], func=ACTF.Exp)
+            eb = ep.tile([P, GW], F32, name="eb", tag="e")
+            et[v] = eb
+            nc.scalar.activation(out=eb[:], in_=ptt[v][:], func=ACTF.Exp)
 
         def cpart(g, ts):
             if not 0 <= g < GROUPS:
@@ -394,45 +426,28 @@ def tile_sralnet_pa_kernel(tc, x, centroids, out):
                         stop=(s == S5 - 1),
                     )
 
-        cli = {}
+        rcb = {}
 
-        def ccopy(g):
-            if not 0 <= g < GROUPS:
-                return
-            h = g % 2
-            if h == 0:
-                cl = img.tile([P, 2 * GW], F32, name="cl", tag="cl")
-                cli[g // 2] = cl
-            if h == 0 or g // 2 < IV:
-                nc.scalar.copy(out=cli[g // 2][:, h * GW : (h + 1) * GW], in_=cps[g][:])
-
-        def invert(i):
-            cl = cli[i]
-            nc.scalar.activation(out=cl[:, 0:GW], in_=cl[:, 0:GW], func=ACTF.Ln)
-            nc.scalar.activation(out=cl[:, GW : 2 * GW], in_=cps[2 * i + 1][:], func=ACTF.Ln)
-            nc.scalar.activation(out=cl[:], in_=cl[:], func=ACTF.Exp, scale=-1.0)
+        def crecip(g):
+            rb = grp.tile([P, GW], F32, name="rb", tag="rb")
+            rcb[g] = rb
+            nc.vector.reciprocal(out=rb[:], in_=cps[g][:])
 
         def cback(g):
-            if not 0 <= g < GROUPS:
-                return
-            h = g % 2
-            ca = pmi.tile([P, GW], F32, name="ca", tag="mi")
+            ca = prc.tile([P, GW], F32, name="ca", tag="rc")
+            cinv[g] = ca
             for t in range(4):
-                nc.tensor.transpose(
-                    ca[:, t * P : (t + 1) * P], cli[g // 2][:, h * GW + t * P : h * GW + (t + 1) * P], ident[:]
-                )
-            ci = grp.tile([P, GW], F32, name="ci", tag="ci")
-            cinv[g] = ci
-            if g // 2 < IV:
-                nc.vector.reciprocal(out=ci[:], in_=ca[:])
-            elif CB == "v":
-                nc.vector.tensor_copy(out=ci[:], in_=ca[:])
-            else:
-                nc.scalar.copy(out=ci[:], in_=ca[:])
+                nc.tensor.transpose(ca[:, t * P : (t + 1) * P], rcb[g][:, t * P : (t + 1) * P], ident[:])
 
         acc = {}
 
         def qmul(v):
+            if not 0 <= v < UNITS:
+                return
+            e = nc.vector if QE.get(v) == "v" else nc.gpsimd
+            e.tensor_tensor(out=ut[v][:], in0=ut[v][:], in1=et[v][:], op=ALU.mult)
+
+        def amul(v):
             if not 0 <= v < UNITS:
                 return
             g, s = divmod(v, S5)
@@ -441,16 +456,10 @@ def tile_sralnet_pa_kernel(tc, x, centroids, out):
                     out=ut[v][:, t * P : (t + 1) * P],
                     in0=ut[v][:, t * P : (t + 1) * P],
                     scalar=rinv[g][:, s * 4 + t : s * 4 + t + 1],
-                    in1=et[v][:, t * P : (t + 1) * P],
+                    in1=cinv[g][:, t * P : (t + 1) * P],
                     op0=ALU.mult,
                     op1=ALU.mult,
                 )
-
-        def amul(v):
-            if not 0 <= v < UNITS:
-                return
-            e = nc.gpsimd if AMUL.get(v) == "g" else nc.vector
-            e.tensor_tensor(out=ut[v][:], in0=ut[v][:], in1=cinv[v // S5][:], op=ALU.mult)
 
         def prod(v):
             if not 0 <= v < UNITS:
@@ -479,7 +488,9 @@ def tile_sralnet_pa_kernel(tc, x, centroids, out):
             mgs[g] = mg
             dst = mg[:].rearrange("p (k t) -> p k t", t=4)
             src = acc[g][:].rearrange("p (t k) -> p k t", t=4)
-            if CAST == "g":
+            if g == GROUPS - 1:
+                nc.vector.tensor_copy(out=dst, in_=src)
+            elif CAST == "g":
                 nc.gpsimd.tensor_scalar(out=dst, in0=src, scalar1=1.0, scalar2=0.0, op0=ALU.mult, op1=ALU.add)
             elif CAST == "s":
                 nc.scalar.copy(out=dst, in_=src)
@@ -506,7 +517,7 @@ def tile_sralnet_pa_kernel(tc, x, centroids, out):
                 xg2s[n] = xg2
             xw = xs[n][:].bitcast(F32).rearrange("p (j a w) -> p j a w", j=4, a=4, w=P)
             xg2w = xg2s[n][:].bitcast(F32).rearrange("p (h jp c) -> p h jp c", h=2, jp=2)
-            xtb = pmi.tile([P, GW], F32, name="xtb", tag="mi")
+            xtb = pzt.tile([P, GW], F32, name="xtb", tag="zt")
             for jl in range(2):
                 for u in range(2):
                     q = jl * 2 + u
@@ -535,7 +546,7 @@ def tile_sralnet_pa_kernel(tc, x, centroids, out):
         fst = {}
 
         def msum(i):
-            ms = pmi.tile([P, 2], F32, name="ms", tag="mi")
+            ms = pzt.tile([P, 2], F32, name="ms", tag="zt")
             for hh in range(2):
                 g = 2 * i + hh
                 for t in range(4):
@@ -551,7 +562,7 @@ def tile_sralnet_pa_kernel(tc, x, centroids, out):
             nc.vector.tensor_scalar(out=sm[:, 0:1], in0=ms[:, 0:1], scalar1=-1.0, scalar2=None, op0=ALU.mult)
 
         def final_mm(i):
-            v = pmi.tile([P, CH], F32, name="v", tag="mi")
+            v = pzt.tile([P, CH], F32, name="v", tag="zt")
             vts[i] = v
             for hh in range(2):
                 g = 2 * i + hh
@@ -580,15 +591,16 @@ def tile_sralnet_pa_kernel(tc, x, centroids, out):
             )
             nc.scalar.activation(out=junk_w[:], in_=vp[:], func=ACTF.Square, accum_out=ssq[:, 0:1])
             pg = fin.tile([P, 16], F32, name="pg", tag="pg")
+            nc.gpsimd.tensor_scalar(
+                out=qcol[:, 0:1], in0=ssq[:, 0:1], scalar1=1.0 / EPS2, scalar2=1.0, op0=ALU.mult, op1=ALU.min
+            )
             nc.gpsimd.tensor_scalar(out=pg[:, 0:1], in0=ssq[:, 0:1], scalar1=EPS2, scalar2=None, op0=ALU.max)
-            nc.gpsimd.tensor_tensor(out=pg[:, 2:3], in0=pg[:, 0:1], in1=expo[:, 9:10], op=ALU.pow)
-            nc.gpsimd.tensor_tensor(out=qcol[:, 0:1], in0=ssq[:, 0:1], in1=pg[:, 2:3], op=ALU.mult)
             nc.gpsimd.tensor_tensor(out=pg[:, 1:2], in0=pg[:, 0:1], in1=expo[:, 8:9], op=ALU.pow)
             fst[i] = (sm, pg, vp)
 
         def final_b(i):
             sm, pg, vp = fst[i]
-            tot = pmi.tile([P, 2], F32, name="tot", tag="mi")
+            tot = pzt.tile([P, 2], F32, name="tot", tag="zt")
             nc.tensor.matmul(out=tot[:], lhsT=ones[:], rhs=qcol[:], start=True, stop=True)
             nc.vector.tensor_scalar(out=sm[:, 1:2], in0=tot[:, 0:1], scalar1=EPS2, scalar2=None, op0=ALU.max)
             nc.gpsimd.tensor_tensor(out=pg[:, 3:4], in0=sm[:, 1:2], in1=expo[:, 8:9], op=ALU.pow)
@@ -611,77 +623,63 @@ def tile_sralnet_pa_kernel(tc, x, centroids, out):
             for b in range(4):
                 XT[steps[b]] = (n, b)
 
-        PR = LA + 1
-        for u in range(-11, UNITS + PR + 16):
-            if HO == 1 and u == -11:
-                wprep()
-            if 0 <= (u + 11) // 5 < GROUPS:
+        for u in range(-11, UNITS + LA + 18):
+            if u == -6:
+                head()
+            if u >= -5:
+                w = u + KE
+                if u + KL >= 5:
+                    za(u + KL)
+                if 2 * (KE > 0) <= w + 1 < 5:
+                    za(w + 1)
+                if u + 1 >= 5:
+                    kmax(u + 1)
+                if 2 * (KE > 0) <= w + 1 < 5:
+                    kmax(w + 1)
+                amul(u - LA)
+                if u >= 5:
+                    e1(u)
+                if 2 * (KE > 0) <= w < 5 and w >= 0:
+                    e1(w)
+                qmul(u - LQ)
+                if ZC == 1 and u + 5 >= 5:
+                    zcp(u + 5)
+                if u + 6 >= 5:
+                    zmx(u + 6)
+                    if ZC == 0:
+                        zcp(u + 6)
+                prod(u - LA - PD)
+                if u % 5 == 3:
+                    smax((u + 2) // 5, 0)
+                if u % 5 == 4:
+                    smax((u + 1) // 5, 1)
+                if u % 5 == 0:
+                    smax(u // 5, 2)
+            if 2 <= (u + 11) // 5 < GROUPS:
                 if (u + 11) % 5 < 4:
                     regroup((u + 11) // 5, (u + 11) % 5)
                 else:
                     xquant((u + 11) // 5)
-            if HO == 0 and u == -7:
-                wprep()
-            if u + KL >= 5:
-                za(u + KL)
-            if u + 1 >= 5:
-                kmax(u + 1)
-            if u >= 5:
-                e1(u)
-            if 0 <= u + KE + 1 < 5:
-                za(u + KE + 1)
-                kmax(u + KE + 1)
-            if 0 <= u + KE < 5:
-                e1(u + KE)
-            if ZC == 1 and u + 5 >= 5:
-                zcp(u + 5)
-            zmx(u + 6)
-            if ZC == 0 or u + 6 < 5:
-                zcp(u + 6)
-            if u % 5 == 3:
-                smax((u + 2) // 5, 0)
-            if u % 5 == 4:
-                smax((u + 1) // 5, 1)
-            if u % 5 == 0:
-                smax(u // 5, 2)
-            if QP == 0:
-                qmul(u - LQ)
             if u % 5 == 0:
                 smax(u // 5, 3)
-            dadd(u - LD)
-            dpe(u - LE + 1)
             e2(u - LE)
+            dpe(u - LE + 1)
             if (u - LE) % 5 == 0:
                 cpart((u - LE - 5) // 5, (0, 1))
             if (u - LE) % 5 == 1:
                 cpart((u - LE - 6) // 5, (2, 3))
-            for g in range(2 * IV):
-                if u == 5 * g + CC + 1:
+            for g in range(GROUPS):
+                if u == 5 * g + CC:
+                    crecip(g)
+                if u == 5 * g + LA - CL:
                     cback(g)
-            for i in range(IV, IMAGES):
-                if u == 10 * i + 5 + PC:
-                    invert(i)
-                if u == 10 * i + 5 + PC + CD:
-                    cback(2 * i)
-                if u == 10 * i + 5 + PC + CD + CE:
-                    cback(2 * i + 1)
+                p0 = 5 * g + LA + PD + 5
+                if u == p0:
+                    cast(g)
+                if u == p0 + 1:
+                    mquant(g)
             if u % 5 == 1:
                 rrecip((u - 6) // 5)
-            if QP == 1:
-                qmul(u - LQ)
-            if u % 5 == CC % 5:
-                ccopy((u - CC) // 5)
-            for v in range(UNITS):
-                if u == v + (LA0 if v < 10 * IV else LA):
-                    amul(v)
-            for g in range(GROUPS):
-                p0 = 5 * g + (LA0 if g < 2 * IV else LA) + 1
-                if 0 <= u - p0 < 5:
-                    prod(5 * g + u - p0)
-                if u == p0 + 5:
-                    cast(g)
-                if u == p0 + 6:
-                    mquant(g)
             if u in XT:
                 n, b = XT[u]
                 xt(n, b, XTE.get(n, 0))
@@ -690,12 +688,12 @@ def tile_sralnet_pa_kernel(tc, x, centroids, out):
                 if b == 3:
                     x2quant(n, 1)
             for i in range(IMAGES):
-                p0 = 10 * i + (LA0 if i < IV else LA) + 1
-                if u == p0 + 10:
+                p0 = 10 * i + 5 + LA + PD + 5
+                if u == p0:
                     msum(i)
-                if u == p0 + 12:
+                if u == p0 + 2:
                     final_mm(i)
-                if u == p0 + 13:
+                if u == p0 + 3:
                     final_a(i)
                 if u == p0 + FB:
                     final_b(i)

@@ -23,40 +23,44 @@ GW = 512
 GROUPS = IMAGES * PIX // GW
 UNITS = GROUPS * S5
 EPS2 = 1e-24
+ZM = 0
+SP = 0
+XQ = 1
+YV = 0
 SR = False
 NZA = 2
 DW = 2
 ZT = 2
 NMI = 1
 NRC = 1
-XTT = 1
-RQ = {}
-RG = {0: 3, 1: 3, 2: 2, 3: 2, 4: 2, 5: 2, 6: 2, 7: 2}
-RH = 2
+XTT = 0
+RQ = {2: 1, 3: 1, 4: 1, 5: 1, 6: 1, 7: 1}
+RG = {0: 4, 1: 4, 2: 4, 3: 3, 4: 3, 5: 3, 6: 3, 7: 3}
+RH = 1
 SB = 0
 P0S = 1
 NES = 0
 REP = 1
 ZC = 0
 KL = 1
-KE = 0
-REALZ = {5: 1, 6: 1, 7: 1, 8: 1, 9: 1, 10: 1, 11: 1, 12: 1, 13: 1, 14: 1, 15: 1, 16: 1, 17: 1, 18: 1, 19: 1, 20: 1, 21: 1, 22: 1, 23: 1, 24: 1, 25: 1, 26: 1, 27: 1, 28: 1, 29: 1, 30: 1, 31: 1, 32: 1, 33: 1, 34: 1, 35: 1, 36: 1, 37: 1, 38: 1, 39: 1}
-REALD = {0: 1, 1: 1, 2: 1, 3: 1, 4: 1, 5: 1, 6: 1, 7: 1, 8: 1, 9: 1, 10: 1, 11: 1, 12: 1, 13: 1, 14: 1, 15: 1, 16: 1, 17: 1, 18: 1, 19: 1, 20: 1, 21: 1, 22: 1, 23: 1, 24: 1, 25: 1, 26: 1, 27: 1, 28: 1, 29: 1, 30: 1, 31: 1, 32: 1, 33: 1, 34: 1, 35: 1, 36: 1, 37: 1, 38: 1, 39: 1}
+KE = 1
+REALZ = {0: 1, 1: 1, 2: 1, 3: 1, 4: 1, 5: 1, 6: 1, 7: 1, 8: 1, 9: 1, 10: 1, 11: 1, 12: 1, 13: 1, 14: 1, 15: 1, 16: 1, 17: 1, 18: 1, 19: 1, 20: 1, 21: 1, 22: 1, 23: 1, 24: 1, 25: 1, 26: 1, 27: 1, 28: 1, 29: 1, 30: 1, 31: 1, 32: 1, 33: 1, 34: 1, 35: 1, 36: 1, 37: 1, 38: 1, 39: 1}
+REALD = {10: 1, 11: 1, 12: 1, 13: 1, 14: 1, 15: 1, 16: 1, 17: 1, 18: 1, 19: 1, 20: 1, 21: 1, 22: 1, 23: 1, 24: 1, 25: 1, 26: 1, 27: 1, 28: 1, 29: 1, 30: 1, 31: 1, 32: 1, 33: 1, 34: 1, 35: 1}
 LE = 3
 EB = 11
-UB = 17
-LQ = 6
-LA = 15
-PD = 1
+UB = 18
+LQ = 4
+LA = 14
+PD = 2
 CC = 11
 CL = 1
 FB = 8
 FC = 11
 CAST = 's'
 XTE = {0: 0, 1: 0, 2: 0, 3: 0}
-XTS = [[1, 3, 6, 8], [11, 13, 16, 18], [21, 23, 26, 28], [31, 33, 36, 38]]
-ZCOPY = {0: 's', 1: 's', 2: 's', 3: 's', 4: 's', 5: 'v', 6: 's', 7: 's', 8: 'v', 9: 's', 10: 's', 11: 'v', 12: 's', 13: 's', 14: 's', 15: 's', 16: 's', 17: 's', 18: 's', 19: 's', 20: 's', 21: 's', 22: 's', 23: 's', 24: 's', 25: 's', 26: 's', 27: 's', 28: 's', 29: 's', 30: 's', 31: 's', 32: 's', 33: 's', 34: 's', 35: 's', 36: 's', 37: 's', 38: 's', 39: 's'}
-QE = {0: 'g', 1: 'g', 2: 'g', 3: 'v', 4: 'g', 5: 'g', 6: 'g', 7: 'v', 8: 'g', 9: 'g', 10: 'g', 11: 'g', 12: 'g', 13: 'g', 14: 'g', 15: 'g', 16: 'g', 17: 'g', 18: 'g', 19: 'g', 20: 'g', 21: 'g', 22: 'g', 23: 'g', 24: 'g', 25: 'g', 26: 'g', 27: 'g', 28: 'g', 29: 'g', 30: 'g', 31: 'g', 32: 'g', 33: 'g', 34: 'g', 35: 'g', 36: 'g', 37: 'g', 38: 'g', 39: 'g'}
+XTS = [[1, 2, 6, 7], [11, 12, 16, 17], [21, 22, 26, 27], [31, 32, 36, 37]]
+ZCOPY = {0: 's', 1: 's', 2: 's', 3: 's', 4: 's', 5: 's', 6: 's', 7: 's', 8: 's', 9: 's', 10: 's', 11: 's', 12: 's', 13: 's', 14: 's', 15: 's', 16: 's', 17: 's', 18: 's', 19: 's', 20: 's', 21: 's', 22: 's', 23: 's', 24: 's', 25: 's', 26: 's', 27: 's', 28: 's', 29: 's', 30: 's', 31: 's', 32: 's', 33: 's', 34: 's', 35: 's', 36: 's', 37: 's', 38: 's', 39: 's'}
+QE = {0: 'g', 1: 'g', 2: 'g', 3: 'g', 4: 'g', 5: 'g', 6: 'g', 7: 'g', 8: 'g', 9: 'g', 10: 'g', 11: 'g', 12: 'g', 13: 'g', 14: 'g', 15: 'g', 16: 'g', 17: 'g', 18: 'g', 19: 'g', 20: 'g', 21: 'g', 22: 'g', 23: 'g', 24: 'g', 25: 'g', 26: 'g', 27: 'g', 28: 'g', 29: 'g', 30: 'g', 31: 'g', 32: 'g', 33: 'g', 34: 'g', 35: 'g', 36: 'g', 37: 'g', 38: 'g', 39: 'g'}
 
 FLOPS = 2 * IMAGES * PIX * M * CH + 2 * IMAGES * K * CH * PIX
 
@@ -215,11 +219,13 @@ def tile_sralnet_pa_kernel(tc, x, centroids, out):
             wcopy(4)
             wquant(3)
             zcp(1)
+            zmaxp(1)
             wquant(4)
             if KE > 0:
                 za(0)
             zmx(2)
             zcp(2)
+            zmaxp(2)
             regroup(1, 0)
             regroup(1, 1)
             regroup(1, 2)
@@ -228,6 +234,7 @@ def tile_sralnet_pa_kernel(tc, x, centroids, out):
                 za(1)
             zmx(3)
             zcp(3)
+            zmaxp(3)
             regroup(1, 3)
             if KE > 0:
                 e1(0)
@@ -235,9 +242,11 @@ def tile_sralnet_pa_kernel(tc, x, centroids, out):
             xquant(1)
             zmx(4)
             zcp(4)
+            zmaxp(4)
             if KE > 0:
                 e1(1)
 
+        ztt = {}
         z = {}
 
         def mx1(bank, g, s):
@@ -268,8 +277,6 @@ def tile_sralnet_pa_kernel(tc, x, centroids, out):
             for again in range(REP if g > 0 else 1):
                 mx1(zt, g, s)
 
-        ztt = {}
-
         def zcp(v):
             if not 0 <= v < UNITS:
                 return
@@ -286,7 +293,37 @@ def tile_sralnet_pa_kernel(tc, x, centroids, out):
         sm_t = {}
         nm = {}
 
+        def zmaxp(v, done=0):
+            if not done <= v < UNITS or not SP:
+                return
+            g, s = divmod(v, S5)
+            if s == 0:
+                return
+            if s == 1:
+                t1 = tmp.tile([P, GW], F32, name="t1", tag="t1", bufs=2)
+                sm_t[g] = t1
+                prev = z[g][:, 0:GW]
+            else:
+                t1 = sm_t[g]
+                prev = t1[:]
+            nc.vector.scalar_tensor_tensor(
+                out=t1[:], in0=ztt[v][:], scalar=bcol[:, s : s + 1], in1=prev, op0=ALU.add, op1=ALU.max
+            )
+
         def smax(g, part):
+            if SP and 0 <= g < GROUPS:
+                if part < 3:
+                    return
+                nmg = grp.tile([P, GW], F32, name="nmg", tag="nm")
+                nm[g] = nmg
+                if NES:
+                    nc.scalar.activation(out=nmg[:], in_=sm_t[g][:], func=ACTF.Copy, scale=-1.0)
+                else:
+                    nc.vector.tensor_scalar(out=nmg[:], in0=sm_t[g][:], scalar1=-1.0, scalar2=None, op0=ALU.mult)
+                return
+            smax_sb(g, part)
+
+        def smax_sb(g, part):
             if not 0 <= g < GROUPS:
                 return
             zg = z[g]
@@ -377,6 +414,16 @@ def tile_sralnet_pa_kernel(tc, x, centroids, out):
         cps = {}
         cinv = {}
 
+        yt = {}
+
+        def yadd(v):
+            if not 0 <= v < YV:
+                return
+            g, s = divmod(v, S5)
+            yb = ep.tile([P, GW], F32, name="yb", tag="y", bufs=2)
+            yt[v] = yb
+            nc.vector.tensor_tensor(out=yb[:], in0=z[g][:, s * GW : (s + 1) * GW], in1=nm[g][:], op=ALU.add)
+
         def dpe(v):
             if not 0 <= v < UNITS:
                 return
@@ -385,22 +432,21 @@ def tile_sralnet_pa_kernel(tc, x, centroids, out):
             ptt[v] = pb
             for t in range(4):
                 real = t < REALD.get(v, 0)
-                nc.tensor.matmul(
-                    out=pb[:, t * P : (t + 1) * P],
-                    lhsT=z[g][:, s * GW + t * P : s * GW + (t + 1) * P],
-                    rhs=ident[:],
-                    is_transpose=not real,
-                    start=True,
-                    stop=False,
-                )
-                nc.tensor.matmul(
-                    out=pb[:, t * P : (t + 1) * P],
-                    lhsT=nm[g][:, t * P : (t + 1) * P],
-                    rhs=ident[:],
-                    is_transpose=True,
-                    start=False,
-                    stop=True,
-                )
+                if v in yt:
+                    nc.tensor.matmul(
+                        out=pb[:, t * P : (t + 1) * P],
+                        lhsT=yt[v][:, t * P : (t + 1) * P],
+                        rhs=ident[:],
+                        is_transpose=not real,
+                        start=True,
+                        stop=True,
+                    )
+                else:
+                    dpair(pb[:, t * P : (t + 1) * P], z[g][:, s * GW + t * P : s * GW + (t + 1) * P], nm[g][:, t * P : (t + 1) * P], real)
+
+        def dpair(o, a, b, real):
+            nc.tensor.matmul(out=o, lhsT=a, rhs=ident[:], is_transpose=not real, start=True, stop=False)
+            nc.tensor.matmul(out=o, lhsT=b, rhs=ident[:], is_transpose=True, start=False, stop=True)
 
         def e2(v):
             if not 0 <= v < UNITS:
@@ -648,6 +694,7 @@ def tile_sralnet_pa_kernel(tc, x, centroids, out):
                     zmx(u + 6)
                     if ZC == 0:
                         zcp(u + 6)
+                    zmaxp(u + 6 - ZM, 5)
                 prod(u - LA - PD)
                 if u % 5 == 3:
                     smax((u + 2) // 5, 0)
@@ -660,8 +707,11 @@ def tile_sralnet_pa_kernel(tc, x, centroids, out):
                     regroup((u + 11) // 5, (u + 11) % 5)
                 else:
                     xquant((u + 11) // 5)
-            if u % 5 == 0:
+            if SP == 0 and u % 5 == 0:
                 smax(u // 5, 3)
+            if SP == 1 and u % 5 == 4:
+                smax((u + 1) // 5, 3)
+            yadd(u - LE + 2)
             e2(u - LE)
             dpe(u - LE + 1)
             if (u - LE) % 5 == 0:
@@ -683,6 +733,8 @@ def tile_sralnet_pa_kernel(tc, x, centroids, out):
             if u in XT:
                 n, b = XT[u]
                 xt(n, b, XTE.get(n, 0))
+            if u - XQ in XT:
+                n, b = XT[u - XQ]
                 if b == 1:
                     x2quant(n, 0)
                 if b == 3:

@@ -19,735 +19,579 @@ PIX = 1024
 K = 128
 S5 = 5
 M = K * S5
-GW = 512
-GROUPS = IMAGES * PIX // GW
-UNITS = GROUPS * S5
+HALF = PIX // 2
+BLKS = HALF // P
+GROUPS = 2 * IMAGES
+TILES = GROUPS * S5
+
+ALPHA = 100.0
 EPS2 = 1e-24
-ZM = 0
-SP = 0
-XQ = 1
-YV = 0
-SR = False
-NZA = 2
-DW = 2
-ZT = 2
-NMI = 1
-NRC = 1
-XTT = 0
-RQ = {2: 1, 3: 1, 4: 1, 5: 1, 6: 1, 7: 1}
-RG = {0: 4, 1: 4, 2: 4, 3: 3, 4: 3, 5: 3, 6: 3, 7: 3}
-RH = 1
-SB = 0
-P0S = 1
-NES = 0
-REP = 1
-ZC = 0
-KL = 1
-KE = 1
-REALZ = {0: 1, 1: 1, 2: 1, 3: 1, 4: 1, 5: 1, 6: 1, 7: 1, 8: 1, 9: 1, 10: 1, 11: 1, 12: 1, 13: 1, 14: 1, 15: 1, 16: 1, 17: 1, 18: 1, 19: 1, 20: 1, 21: 1, 22: 1, 23: 1, 24: 1, 25: 1, 26: 1, 27: 1, 28: 1, 29: 1, 30: 1, 31: 1, 32: 1, 33: 1, 34: 1, 35: 1, 36: 1, 37: 1, 38: 1, 39: 1}
-REALD = {10: 1, 11: 1, 12: 1, 13: 1, 14: 1, 15: 1, 16: 1, 17: 1, 18: 1, 19: 1, 20: 1, 21: 1, 22: 1, 23: 1, 24: 1, 25: 1, 26: 1, 27: 1, 28: 1, 29: 1, 30: 1, 31: 1, 32: 1, 33: 1, 34: 1, 35: 1}
-LE = 3
-EB = 11
-UB = 18
-LQ = 4
-LA = 14
-PD = 2
-CC = 11
-CL = 1
-FB = 8
-FC = 11
-CAST = 's'
-XTE = {0: 0, 1: 0, 2: 0, 3: 0}
-XTS = [[1, 2, 6, 7], [11, 12, 16, 17], [21, 22, 26, 27], [31, 32, 36, 37]]
-ZCOPY = {0: 's', 1: 's', 2: 's', 3: 's', 4: 's', 5: 's', 6: 's', 7: 's', 8: 's', 9: 's', 10: 's', 11: 's', 12: 's', 13: 's', 14: 's', 15: 's', 16: 's', 17: 's', 18: 's', 19: 's', 20: 's', 21: 's', 22: 's', 23: 's', 24: 's', 25: 's', 26: 's', 27: 's', 28: 's', 29: 's', 30: 's', 31: 's', 32: 's', 33: 's', 34: 's', 35: 's', 36: 's', 37: 's', 38: 's', 39: 's'}
-QE = {0: 'g', 1: 'g', 2: 'g', 3: 'g', 4: 'g', 5: 'g', 6: 'g', 7: 'g', 8: 'g', 9: 'g', 10: 'g', 11: 'g', 12: 'g', 13: 'g', 14: 'g', 15: 'g', 16: 'g', 17: 'g', 18: 'g', 19: 'g', 20: 'g', 21: 'g', 22: 'g', 23: 'g', 24: 'g', 25: 'g', 26: 'g', 27: 'g', 28: 'g', 29: 'g', 30: 'g', 31: 'g', 32: 'g', 33: 'g', 34: 'g', 35: 'g', 36: 'g', 37: 'g', 38: 'g', 39: 'g'}
 
 FLOPS = 2 * IMAGES * PIX * M * CH + 2 * IMAGES * K * CH * PIX
+
+MM_LEAD = 5
+EXP2_LAG = 4
+UP_LAG = 5
+SOFT_LAG = 15
+PROD_LAG = 17
+
+CLOCK_FROM = 4
 
 
 def tile_sralnet_pa_kernel(tc, x, centroids, out):
     nc = tc.nc
     with ExitStack() as ctx:
         const = ctx.enter_context(tc.tile_pool(name="const", bufs=1))
-        xin = ctx.enter_context(tc.tile_pool(name="xin", bufs=4))
+        xin = ctx.enter_context(tc.tile_pool(name="xin", bufs=IMAGES))
         xgp = ctx.enter_context(tc.tile_pool(name="xgp", bufs=2))
         xq1 = ctx.enter_context(tc.tile_pool(name="xq1", bufs=2))
         xq2 = ctx.enter_context(tc.tile_pool(name="xq2", bufs=3))
         zp = ctx.enter_context(tc.tile_pool(name="zp", bufs=3))
-        ep = ctx.enter_context(tc.tile_pool(name="ep", bufs=EB))
-        up = ctx.enter_context(tc.tile_pool(name="up", bufs=UB))
+        pp = ctx.enter_context(tc.tile_pool(name="pp", bufs=EXP2_LAG + 7))
+        up = ctx.enter_context(tc.tile_pool(name="up", bufs=PROD_LAG + 1))
         tmp = ctx.enter_context(tc.tile_pool(name="tmp", bufs=1))
         grp = ctx.enter_context(tc.tile_pool(name="grp", bufs=3))
         mul = ctx.enter_context(tc.tile_pool(name="mul", bufs=3))
         fin = ctx.enter_context(tc.tile_pool(name="fin", bufs=2))
-        pza = ctx.enter_context(tc.psum_pool(name="pza", bufs=NZA))
-        ppt = ctx.enter_context(tc.psum_pool(name="ppt", bufs=DW))
-        pzt = ctx.enter_context(tc.psum_pool(name="pzt", bufs=ZT))
-        prc = ctx.enter_context(tc.psum_pool(name="prc", bufs=NRC))
-        pmi = ctx.enter_context(tc.psum_pool(name="pmi", bufs=NMI))
+        pza = ctx.enter_context(tc.psum_pool(name="pza", bufs=2))
+        pdf = ctx.enter_context(tc.psum_pool(name="pdf", bufs=2))
+        pmm = ctx.enter_context(tc.psum_pool(name="pmm", bufs=2))
+        psc = ctx.enter_context(tc.psum_pool(name="psc", bufs=1))
+        prc = ctx.enter_context(tc.psum_pool(name="prc", bufs=1))
         ctx.enter_context(tc.manual_schedule())
 
-        xs = {}
-        xs_0 = xin.tile([P, 4 * PIX], BF16, name="xs_0", tag="xs")
-        xs[0] = xs_0
-        x0v = xs_0[:].rearrange("p (j c) -> p j c", j=4)
-        x0d = x[0].rearrange("(q j) h w -> q j (h w)", j=4)
         cen = const.tile([P, S5 * CH], BF16, name="cen")
         nc.sync.dma_start(out=cen[:], in_=centroids.rearrange("k s c -> k (s c)"))
-        nc.sync.dma_start(out=x0v[:, :, 0:GW], in_=x0d[:, :, 0:GW])
-        nc.sync.dma_start(out=x0v[:, :, GW:PIX], in_=x0d[:, :, GW:PIX])
-        for n in range(1, IMAGES):
-            xs_n = xin.tile([P, 4 * PIX], BF16, name="xs_n", tag="xs")
-            nc.sync.dma_start(out=xs_n[:], in_=x[n].rearrange("(q j) h w -> q (j h w)", j=4))
-            xs[n] = xs_n
+        xs = []
+        for n in range(IMAGES):
+            x_n = xin.tile([P, 4 * PIX], BF16, name="x_n", tag="x")
+            xs.append(x_n)
+            if n == 0:
+                sb = x_n[:].rearrange("p (j c) -> p j c", j=4)
+                hbm = x[n].rearrange("(q j) h w -> q j (h w)", j=4)
+                nc.sync.dma_start(out=sb[:, :, 0:HALF], in_=hbm[:, :, 0:HALF])
+                nc.sync.dma_start(out=sb[:, :, HALF:PIX], in_=hbm[:, :, HALF:PIX])
+            else:
+                nc.sync.dma_start(out=x_n[:], in_=x[n].rearrange("(q j) h w -> q (j h w)", j=4))
 
         ident = const.tile([P, P], F32, name="ident")
         make_identity(nc, ident[:])
         ones = const.tile([P, P], F32, name="ones")
         nc.vector.memset(ones[:], 1.0)
-        expo = const.tile([P, 16], F32, name="expo")
-        nc.vector.memset(expo[:, 0:8], 0.5)
-        nc.vector.memset(expo[:, 8:9], -0.5)
-        nc.vector.memset(expo[:, 9:10], -1.0)
-        qcol = const.tile([P, 2], F32, name="qcol")
-        nc.vector.memset(qcol[:], 0.0)
-        junk_w = const.tile([P, CH], F32, name="junk_w")
-        nc.scalar.activation(out=junk_w[:, 0:1], in_=expo[:, 0:1], func=ACTF.Exp)
+        plus_half = const.tile([P, S5], F32, name="plus_half")
+        nc.vector.memset(plus_half[:], 0.5)
+        minus_half = const.tile([P, 1], F32, name="minus_half")
+        nc.vector.memset(minus_half[:], -0.5)
+        share = const.tile([P, 2], F32, name="share")
+        nc.vector.memset(share[:], 0.0)
+        junk = const.tile([P, CH], F32, name="junk")
+        nc.scalar.activation(out=junk[:, 0:1], in_=plus_half[:, 0:1], func=ACTF.Exp)
 
+        wg = const.tile([P, 4 * M], BF16, name="wg", align_bytes=64)
+        wc = const.tile([P, M], U32, name="wc", align_bytes=64)
+        wsc = const.tile([P, M], U8, name="wsc", align_bytes=64)
+        n2 = const.tile([P, S5], F32, name="n2")
+        norm = const.tile([P, S5], F32, name="norm")
+        bias = const.tile([P, S5], F32, name="bias")
+        wts = {}
+
+        def w_transpose(s):
+            pool, tag = ((psc, "c"), (prc, "rc"), (pdf, "df"), (pdf, "df"), (pza, "za"))[s]
+            wt = pool.tile([P, 2 * P], F32, name="wt", tag=tag)
+            wts[s] = wt
+            words = cen[:].bitcast(F32).rearrange("p (s q u) -> p s u q", s=S5, u=2)
+            for u in range(2):
+                nc.tensor.transpose(wt[:, u * P : (u + 1) * P], words[:, s, u], ident[:])
+
+        def w_scale(s):
+            nc.vector.tensor_scalar(
+                out=wg[:, s * 4 * K : (s + 1) * 4 * K].rearrange("p (k u e) -> p k u e", u=2, e=2),
+                in0=wts[s][:].bitcast(BF16).rearrange("p (u k e) -> p k u e", u=2, e=2),
+                scalar1=2 * ALPHA,
+                scalar2=None,
+                op0=ALU.mult,
+            )
+
+        def w_quant(s):
+            nc.vector.quantize_mx(
+                out=wc[:, s * K : (s + 1) * K].bitcast(FP8X4),
+                scales=wsc[:, s * K : (s + 1) * K],
+                in_=wg[:, s * 4 * K : (s + 1) * 4 * K],
+            )
+
+        def make_bias(lo, hi):
+            for s in range(lo, hi):
+                nc.scalar.activation(
+                    out=junk[:], in_=cen[:, s * CH : (s + 1) * CH], func=ACTF.Square, accum_out=n2[:, s : s + 1]
+                )
+            nc.gpsimd.tensor_tensor(out=norm[:, lo:hi], in0=n2[:, lo:hi], in1=plus_half[:, lo:hi], op=ALU.pow)
+            nc.gpsimd.tensor_scalar(out=bias[:, lo:hi], in0=norm[:, lo:hi], scalar1=-ALPHA, scalar2=None, op0=ALU.mult)
+
+        xg1 = {}
         xc1 = {}
         xsc1 = {}
-        xg1s = {}
 
         def regroup(g, q):
-            n = g // 2
-            h = g % 2
-            if q == 0:
-                xg1 = xgp.tile([P, 4 * GW], BF16, name="xg1", tag="xg1", align_bytes=64)
-                xg1s[g] = xg1
+            n, h = divmod(g, 2)
             a, e = divmod(q, 2)
+            if q == 0:
+                xg1_g = xgp.tile([P, 4 * HALF], BF16, name="xg1_g", tag="xg1", align_bytes=64)
+                xg1[g] = xg1_g
             src = xs[n][:].rearrange("p (j a r e) -> p a e r j", j=4, a=4, r=P, e=2)[:, 2 * h + a, e]
-            dst = xg1s[g][:].rearrange("p (a e r j) -> p a e r j", a=2, e=2, r=P, j=4)[:, a, e]
-            if g > 0 and q < RQ.get(g, 0):
+            dst = xg1[g][:].rearrange("p (a e r j) -> p a e r j", a=2, e=2, r=P, j=4)[:, a, e]
+            if g > 1 and q == 0:
                 nc.gpsimd.tensor_scalar(out=dst, in0=src, scalar1=1.0, scalar2=0.0, op0=ALU.mult, op1=ALU.add)
-            elif (g > 0 and q >= RG.get(g, 4)) or (g == 0 and q < RH):
+            elif (g > 1 and q == 3) or (g == 0 and q == 0):
                 nc.scalar.copy(out=dst, in_=src)
             else:
                 nc.vector.tensor_copy(out=dst, in_=src)
 
-        def xquant(g):
-            n = g // 2
-            h = g % 2
+        def x1_quant(g):
+            n, h = divmod(g, 2)
             if h == 0:
                 c1 = xq1.tile([P, PIX], U32, name="c1", tag="c1", align_bytes=64)
                 s1 = xq1.tile([P, PIX], U8, name="s1", tag="s1", align_bytes=64)
                 xc1[n] = c1
                 xsc1[n] = s1
-            nc.vector.quantize_mx(
-                out=xc1[n][:, h * GW : (h + 1) * GW].bitcast(FP8X4),
-                scales=xsc1[n][:, h * GW : (h + 1) * GW],
-                in_=xg1s[g][:],
-            )
+            cols = slice(h * HALF, (h + 1) * HALF)
+            nc.vector.quantize_mx(out=xc1[n][:, cols].bitcast(FP8X4), scales=xsc1[n][:, cols], in_=xg1[g][:])
 
-        wg = const.tile([P, 4 * M], BF16, name="wg", align_bytes=64)
-        wc = const.tile([P, M], U32, name="wc", align_bytes=64)
-        wsc = const.tile([P, M], U8, name="wsc", align_bytes=64)
-        n2 = const.tile([P, 8], F32, name="n2")
-        brt = const.tile([P, 8], F32, name="brt")
-        bcol = const.tile([P, 8], F32, name="bcol")
-
-        def wquant(s):
-            nc.vector.quantize_mx(
-                out=wc[:, s * P : (s + 1) * P].bitcast(FP8X4),
-                scales=wsc[:, s * P : (s + 1) * P],
-                in_=wg[:, s * 512 : (s + 1) * 512],
-            )
-
-        wts = {}
-
-        def wtrans(s):
-            cenw = cen[:].bitcast(F32).rearrange("p (s q u) -> p s u q", s=S5, u=2)
-            if s < 1:
-                wt = pmi.tile([P, 256], F32, name="wt", tag="mi")
-            elif s < 2:
-                wt = prc.tile([P, 256], F32, name="wt", tag="rc")
-            elif s < 4:
-                wt = ppt.tile([P, 256], F32, name="wt", tag="pt")
-            else:
-                wt = pza.tile([P, 256], F32, name="wt", tag="za")
-            wts[s] = wt
-            for u in range(2):
-                nc.tensor.transpose(wt[:, u * P : (u + 1) * P], cenw[:, s, u], ident[:])
-
-        def wcopy(s):
-            nc.vector.tensor_scalar(
-                out=wg[:, s * 512 : (s + 1) * 512].rearrange("p (k u e) -> p k u e", u=2, e=2),
-                in0=wts[s][:].bitcast(BF16).rearrange("p (u k e) -> p k u e", u=2, e=2),
-                scalar1=200.0,
-                scalar2=None,
-                op0=ALU.mult,
-            )
-
-        def bias(ss):
-            for s in ss:
-                nc.scalar.activation(
-                    out=junk_w[:], in_=cen[:, s * CH : (s + 1) * CH], func=ACTF.Square, accum_out=n2[:, s : s + 1]
-                )
-            a, b = ss[0], ss[-1] + 1
-            nc.gpsimd.tensor_tensor(out=brt[:, a:b], in0=n2[:, a:b], in1=expo[:, a:b], op=ALU.pow)
-            nc.gpsimd.tensor_scalar(
-                out=bcol[:, a:b], in0=brt[:, a:b], scalar1=-100.0, scalar2=None, op0=ALU.mult
-            )
-
-        def head():
-            for s in range(S5):
-                wtrans(s)
-            wcopy(0)
-            wcopy(1)
-            wquant(0)
-            bias((0, 1))
-            for q in range(4):
-                regroup(0, q)
-            wquant(1)
-            wcopy(2)
-            xquant(0)
-            bias((2, 3, 4))
-            zmx(0)
-            zmx(1)
-            wcopy(3)
-            wquant(2)
-            zcp(0)
-            wcopy(4)
-            wquant(3)
-            zcp(1)
-            zmaxp(1)
-            wquant(4)
-            if KE > 0:
-                za(0)
-            zmx(2)
-            zcp(2)
-            zmaxp(2)
-            regroup(1, 0)
-            regroup(1, 1)
-            regroup(1, 2)
-            if KE > 0:
-                kmax(0)
-                za(1)
-            zmx(3)
-            zcp(3)
-            zmaxp(3)
-            regroup(1, 3)
-            if KE > 0:
-                e1(0)
-                kmax(1)
-            xquant(1)
-            zmx(4)
-            zcp(4)
-            zmaxp(4)
-            if KE > 0:
-                e1(1)
-
-        ztt = {}
+        zbank = {}
         z = {}
 
-        def mx1(bank, g, s):
+        def first_mm(v):
+            g, s = divmod(v, S5)
             n, h = divmod(g, 2)
+            if s == 0:
+                z_g = zp.tile([P, S5 * HALF], F32, name="z_g", tag="z")
+                z[g] = z_g
+            pool, tag = (pdf, "df") if v in (1, 3) else (pmm, "mm")
+            zb = pool.tile([P, HALF], F32, name="zb", tag=tag)
+            zbank[v] = zb
+            cols = slice(h * HALF, (h + 1) * HALF)
             nc.tensor.matmul_mx(
-                out=bank[:],
-                lhsT=wc[:, s * P : (s + 1) * P].bitcast(FP8X4),
-                lhsT_scale=wsc[:, s * P : (s + 1) * P],
-                rhs=xc1[n][:, h * GW : (h + 1) * GW].bitcast(FP8X4),
-                rhs_scale=xsc1[n][:, h * GW : (h + 1) * GW],
+                out=zb[:],
+                lhsT=wc[:, s * K : (s + 1) * K].bitcast(FP8X4),
+                lhsT_scale=wsc[:, s * K : (s + 1) * K],
+                rhs=xc1[n][:, cols].bitcast(FP8X4),
+                rhs_scale=xsc1[n][:, cols],
                 start=True,
                 stop=True,
             )
 
-        def zmx(v):
-            if not 0 <= v < UNITS:
-                return
+        def add_bias(v):
             g, s = divmod(v, S5)
-            n, h = divmod(g, 2)
-            if s == 0:
-                zg = zp.tile([P, S5 * GW], F32, name="zg", tag="z")
-                z[g] = zg
-            if v in (1, 3):
-                zt = ppt.tile([P, GW], F32, name="zt", tag="pt")
-            else:
-                zt = pzt.tile([P, GW], F32, name="zt", tag="zt")
-            ztt[v] = zt
-            for again in range(REP if g > 0 else 1):
-                mx1(zt, g, s)
-
-        def zcp(v):
-            if not 0 <= v < UNITS:
-                return
-            g, s = divmod(v, S5)
-            zt = ztt[v]
-            dst = z[g][:, s * GW : (s + 1) * GW]
-            if ZCOPY.get(v) == "s":
-                nc.scalar.activation(out=dst, in_=zt[:], func=ACTF.Identity, bias=bcol[:, s : s + 1], scale=1.0)
-            else:
-                nc.vector.tensor_scalar(
-                    out=dst, in0=zt[:], scalar1=bcol[:, s : s + 1], scalar2=None, op0=ALU.add
-                )
-
-        sm_t = {}
-        nm = {}
-
-        def zmaxp(v, done=0):
-            if not done <= v < UNITS or not SP:
-                return
-            g, s = divmod(v, S5)
-            if s == 0:
-                return
-            if s == 1:
-                t1 = tmp.tile([P, GW], F32, name="t1", tag="t1", bufs=2)
-                sm_t[g] = t1
-                prev = z[g][:, 0:GW]
-            else:
-                t1 = sm_t[g]
-                prev = t1[:]
-            nc.vector.scalar_tensor_tensor(
-                out=t1[:], in0=ztt[v][:], scalar=bcol[:, s : s + 1], in1=prev, op0=ALU.add, op1=ALU.max
+            nc.scalar.activation(
+                out=z[g][:, s * HALF : (s + 1) * HALF],
+                in_=zbank.pop(v)[:],
+                func=ACTF.Identity,
+                bias=bias[:, s : s + 1],
+                scale=1.0,
             )
 
-        def smax(g, part):
-            if SP and 0 <= g < GROUPS:
-                if part < 3:
-                    return
-                nmg = grp.tile([P, GW], F32, name="nmg", tag="nm")
-                nm[g] = nmg
-                if NES:
-                    nc.scalar.activation(out=nmg[:], in_=sm_t[g][:], func=ACTF.Copy, scale=-1.0)
-                else:
-                    nc.vector.tensor_scalar(out=nmg[:], in0=sm_t[g][:], scalar1=-1.0, scalar2=None, op0=ALU.mult)
-                return
-            smax_sb(g, part)
+        zmax = {}
+        neg_max = {}
 
-        def smax_sb(g, part):
-            if not 0 <= g < GROUPS:
-                return
+        def centroid_max(g, part):
             zg = z[g]
             if part == 0:
-                t1 = tmp.tile([P, 2 * GW], BF16 if SB else F32, name="t1", tag="t1")
-                sm_t[g] = t1
-                nc.vector.tensor_tensor(out=t1[:], in0=zg[:, 0 : 2 * GW], in1=zg[:, 2 * GW : 4 * GW], op=ALU.max)
-            elif part == 1:
-                t1 = sm_t[g]
-                nc.vector.tensor_tensor(out=t1[:, 0:GW], in0=t1[:, 0:GW], in1=t1[:, GW : 2 * GW], op=ALU.max)
+                zm = tmp.tile([P, 2 * HALF], F32, name="zm", tag="zm")
+                zmax[g] = zm
+                nc.vector.tensor_tensor(out=zm[:], in0=zg[:, 0 : 2 * HALF], in1=zg[:, 2 * HALF : 4 * HALF], op=ALU.max)
+                return
+            lo = zmax[g][:, 0:HALF]
+            hi = zmax[g][:, HALF : 2 * HALF]
+            if part == 1:
+                nc.vector.tensor_tensor(out=lo, in0=lo, in1=hi, op=ALU.max)
             elif part == 2:
-                t1 = sm_t[g]
-                nc.vector.tensor_tensor(out=t1[:, GW : 2 * GW], in0=t1[:, 0:GW], in1=zg[:, 4 * GW : 5 * GW], op=ALU.max)
+                nc.vector.tensor_tensor(out=hi, in0=lo, in1=zg[:, 4 * HALF : 5 * HALF], op=ALU.max)
             else:
-                t1 = sm_t[g]
-                nmg = grp.tile([P, GW], F32, name="nmg", tag="nm")
-                nm[g] = nmg
-                if NES:
-                    nc.scalar.activation(out=nmg[:], in_=t1[:, GW : 2 * GW], func=ACTF.Copy, scale=-1.0)
-                else:
-                    nc.vector.tensor_scalar(out=nmg[:], in0=t1[:, GW : 2 * GW], scalar1=-1.0, scalar2=None, op0=ALU.mult)
+                nm = grp.tile([P, HALF], F32, name="nm", tag="nm")
+                neg_max[g] = nm
+                nc.vector.tensor_scalar(out=nm[:], in0=hi, scalar1=-1.0, scalar2=None, op0=ALU.mult)
 
-        nmk = {}
+        zab = {}
+        neg_kmax = {}
         rsum = {}
         rinv = {}
-        zat = {}
-        ut = {}
+        u = {}
 
-        def za(v):
-            if not 0 <= v < UNITS:
-                return
+        def z_transpose(v):
             g, s = divmod(v, S5)
             if s == 0:
-                nmk_g = grp.tile([P, 20], F32, name="nmk_g", tag="nmk")
-                rsum_g = grp.tile([P, 20], F32, name="rsum_g", tag="rsum")
-                nmk[g] = nmk_g
-                rsum[g] = rsum_g
-            zab = pza.tile([P, GW], F32, name="zab", tag="za")
-            zat[v] = zab
-            for t in range(4):
+                nk = grp.tile([P, S5 * BLKS], F32, name="nk", tag="nk")
+                rs = grp.tile([P, S5 * BLKS], F32, name="rs", tag="rs")
+                neg_kmax[g] = nk
+                rsum[g] = rs
+            za = pza.tile([P, HALF], F32, name="za", tag="za")
+            zab[v] = za
+            for t in range(BLKS):
                 nc.tensor.matmul(
-                    out=zab[:, t * P : (t + 1) * P],
-                    lhsT=z[g][:, s * GW + t * P : s * GW + (t + 1) * P],
+                    out=za[:, t * P : (t + 1) * P],
+                    lhsT=z[g][:, s * HALF + t * P : s * HALF + (t + 1) * P],
                     rhs=ident[:],
-                    is_transpose=not (t == 3 and REALZ.get(v)),
+                    is_transpose=t < BLKS - 1 or v < CLOCK_FROM,
                     start=True,
                     stop=True,
                 )
 
-        def kmax(v):
-            if not 0 <= v < UNITS:
-                return
+        def cluster_max(v):
             g, s = divmod(v, S5)
             nc.vector.tensor_reduce(
-                out=nmk[g][:, s * 4 : s * 4 + 4],
-                in_=zat[v][:].rearrange("p (t k) -> p t k", t=4),
+                out=neg_kmax[g][:, s * BLKS : (s + 1) * BLKS],
+                in_=zab[v][:].rearrange("p (t k) -> p t k", t=BLKS),
                 axis=AX.X,
                 op=ALU.max,
                 negate=True,
             )
 
-        def e1(v):
-            if not 0 <= v < UNITS:
-                return
+        def exp1(v):
             g, s = divmod(v, S5)
-            ub = up.tile([P, GW], F32, name="ub", tag="u")
-            ut[v] = ub
-            for t in range(4):
-                c = s * 4 + t
+            ub = up.tile([P, HALF], F32, name="ub", tag="u")
+            u[v] = ub
+            za = zab.pop(v)
+            for t in range(BLKS):
+                c = s * BLKS + t
                 nc.scalar.activation(
                     out=ub[:, t * P : (t + 1) * P],
-                    in_=zat[v][:, t * P : (t + 1) * P],
+                    in_=za[:, t * P : (t + 1) * P],
                     func=ACTF.Exp,
-                    bias=nmk[g][:, c : c + 1],
+                    bias=neg_kmax[g][:, c : c + 1],
                     scale=1.0,
                     accum_out=rsum[g][:, c : c + 1],
                 )
 
-        def rrecip(g):
-            if not 0 <= g < GROUPS:
-                return
-            ri = grp.tile([P, 20], F32, name="ri", tag="ri")
+        def invert_r(g):
+            ri = grp.tile([P, S5 * BLKS], F32, name="ri", tag="ri")
             rinv[g] = ri
             nc.vector.reciprocal(out=ri[:], in_=rsum[g][:])
 
-        et = {}
-        ptt = {}
-        cps = {}
+        dbank = {}
+        p = {}
+        csum = {}
         cinv = {}
+        cinv_t = {}
 
-        yt = {}
-
-        def yadd(v):
-            if not 0 <= v < YV:
-                return
+        def diff(v):
             g, s = divmod(v, S5)
-            yb = ep.tile([P, GW], F32, name="yb", tag="y", bufs=2)
-            yt[v] = yb
-            nc.vector.tensor_tensor(out=yb[:], in0=z[g][:, s * GW : (s + 1) * GW], in1=nm[g][:], op=ALU.add)
+            db = pdf.tile([P, HALF], F32, name="db", tag="df")
+            dbank[v] = db
+            for t in range(BLKS):
+                nc.tensor.matmul(
+                    out=db[:, t * P : (t + 1) * P],
+                    lhsT=z[g][:, s * HALF + t * P : s * HALF + (t + 1) * P],
+                    rhs=ident[:],
+                    is_transpose=t > 0 or v < CLOCK_FROM,
+                    start=True,
+                    stop=False,
+                )
+                nc.tensor.matmul(
+                    out=db[:, t * P : (t + 1) * P],
+                    lhsT=neg_max[g][:, t * P : (t + 1) * P],
+                    rhs=ident[:],
+                    is_transpose=True,
+                    start=False,
+                    stop=True,
+                )
 
-        def dpe(v):
-            if not 0 <= v < UNITS:
-                return
-            g, s = divmod(v, S5)
-            pb = ppt.tile([P, GW], F32, name="pb", tag="pt")
-            ptt[v] = pb
-            for t in range(4):
-                real = t < REALD.get(v, 0)
-                if v in yt:
-                    nc.tensor.matmul(
-                        out=pb[:, t * P : (t + 1) * P],
-                        lhsT=yt[v][:, t * P : (t + 1) * P],
-                        rhs=ident[:],
-                        is_transpose=not real,
-                        start=True,
-                        stop=True,
-                    )
-                else:
-                    dpair(pb[:, t * P : (t + 1) * P], z[g][:, s * GW + t * P : s * GW + (t + 1) * P], nm[g][:, t * P : (t + 1) * P], real)
+        def exp2(v):
+            pb = pp.tile([P, HALF], F32, name="pb", tag="p")
+            p[v] = pb
+            nc.scalar.activation(out=pb[:], in_=dbank.pop(v)[:], func=ACTF.Exp)
 
-        def dpair(o, a, b, real):
-            nc.tensor.matmul(out=o, lhsT=a, rhs=ident[:], is_transpose=not real, start=True, stop=False)
-            nc.tensor.matmul(out=o, lhsT=b, rhs=ident[:], is_transpose=True, start=False, stop=True)
-
-        def e2(v):
-            if not 0 <= v < UNITS:
-                return
-            eb = ep.tile([P, GW], F32, name="eb", tag="e")
-            et[v] = eb
-            nc.scalar.activation(out=eb[:], in_=ptt[v][:], func=ACTF.Exp)
-
-        def cpart(g, ts):
-            if not 0 <= g < GROUPS:
-                return
-            if ts[0] == 0:
-                cb = pmi.tile([P, GW], F32, name="cb", tag="mi")
-                cps[g] = cb
-            for t in ts:
+        def sum_c(g, blocks):
+            if blocks[0] == 0:
+                cs = psc.tile([P, HALF], F32, name="cs", tag="c")
+                csum[g] = cs
+            for t in blocks:
                 for s in range(S5):
                     nc.tensor.matmul(
-                        out=cps[g][:, t * P : (t + 1) * P],
-                        lhsT=et[g * S5 + s][:, t * P : (t + 1) * P],
+                        out=csum[g][:, t * P : (t + 1) * P],
+                        lhsT=p[g * S5 + s][:, t * P : (t + 1) * P],
                         rhs=ident[:],
                         is_transpose=True,
                         start=(s == 0),
                         stop=(s == S5 - 1),
                     )
 
-        rcb = {}
+        def invert_c(g):
+            ci = grp.tile([P, HALF], F32, name="ci", tag="ci")
+            cinv[g] = ci
+            nc.vector.reciprocal(out=ci[:], in_=csum[g][:])
 
-        def crecip(g):
-            rb = grp.tile([P, GW], F32, name="rb", tag="rb")
-            rcb[g] = rb
-            nc.vector.reciprocal(out=rb[:], in_=cps[g][:])
+        def c_transpose(g):
+            ct = prc.tile([P, HALF], F32, name="ct", tag="rc")
+            cinv_t[g] = ct
+            for t in range(BLKS):
+                nc.tensor.transpose(ct[:, t * P : (t + 1) * P], cinv[g][:, t * P : (t + 1) * P], ident[:])
 
-        def cback(g):
-            ca = prc.tile([P, GW], F32, name="ca", tag="rc")
-            cinv[g] = ca
-            for t in range(4):
-                nc.tensor.transpose(ca[:, t * P : (t + 1) * P], rcb[g][:, t * P : (t + 1) * P], ident[:])
+        mult = {}
+        mg = {}
+        mc = {}
+        msc = {}
 
-        acc = {}
+        def times_p(v):
+            nc.gpsimd.tensor_tensor(out=u[v][:], in0=u[v][:], in1=p[v][:], op=ALU.mult)
 
-        def qmul(v):
-            if not 0 <= v < UNITS:
-                return
-            e = nc.vector if QE.get(v) == "v" else nc.gpsimd
-            e.tensor_tensor(out=ut[v][:], in0=ut[v][:], in1=et[v][:], op=ALU.mult)
-
-        def amul(v):
-            if not 0 <= v < UNITS:
-                return
+        def soft(v):
             g, s = divmod(v, S5)
-            for t in range(4):
+            for t in range(BLKS):
+                c = s * BLKS + t
                 nc.vector.scalar_tensor_tensor(
-                    out=ut[v][:, t * P : (t + 1) * P],
-                    in0=ut[v][:, t * P : (t + 1) * P],
-                    scalar=rinv[g][:, s * 4 + t : s * 4 + t + 1],
-                    in1=cinv[g][:, t * P : (t + 1) * P],
+                    out=u[v][:, t * P : (t + 1) * P],
+                    in0=u[v][:, t * P : (t + 1) * P],
+                    scalar=rinv[g][:, c : c + 1],
+                    in1=cinv_t[g][:, t * P : (t + 1) * P],
                     op0=ALU.mult,
                     op1=ALU.mult,
                 )
 
-        def prod(v):
-            if not 0 <= v < UNITS:
-                return
+        def factor(v):
             g, s = divmod(v, S5)
             if s == 0:
-                accg = mul.tile([P, GW], F32, name="accg", tag="acc")
-                acc[g] = accg
-                if P0S:
-                    nc.scalar.activation(out=accg[:], in_=ut[v][:], func=ACTF.Identity, bias=1.0, scale=1.0)
-                else:
-                    nc.vector.tensor_scalar(out=accg[:], in0=ut[v][:], scalar1=1.0, scalar2=None, op0=ALU.add)
+                m_g = mul.tile([P, HALF], F32, name="m_g", tag="m")
+                mult[g] = m_g
+                nc.scalar.activation(out=m_g[:], in_=u[v][:], func=ACTF.Identity, bias=1.0, scale=1.0)
             else:
                 nc.vector.scalar_tensor_tensor(
-                    out=acc[g][:], in0=ut[v][:], scalar=1.0, in1=acc[g][:], op0=ALU.add, op1=ALU.mult
+                    out=mult[g][:], in0=u[v][:], scalar=1.0, in1=mult[g][:], op0=ALU.add, op1=ALU.mult
                 )
 
-        mgs = {}
-        mcod = {}
-        mscl = {}
-
-        def cast(g):
-            if not 0 <= g < GROUPS:
-                return
-            mg = mul.tile([P, GW], BF16, name="mg", tag="mg", align_bytes=64)
-            mgs[g] = mg
-            dst = mg[:].rearrange("p (k t) -> p k t", t=4)
-            src = acc[g][:].rearrange("p (t k) -> p k t", t=4)
+        def m_cast(g):
+            mg_g = mul.tile([P, HALF], BF16, name="mg_g", tag="mg", align_bytes=64)
+            mg[g] = mg_g
+            dst = mg_g[:].rearrange("p (k t) -> p k t", t=BLKS)
+            src = mult[g][:].rearrange("p (t k) -> p k t", t=BLKS)
             if g == GROUPS - 1:
                 nc.vector.tensor_copy(out=dst, in_=src)
-            elif CAST == "g":
-                nc.gpsimd.tensor_scalar(out=dst, in0=src, scalar1=1.0, scalar2=0.0, op0=ALU.mult, op1=ALU.add)
-            elif CAST == "s":
-                nc.scalar.copy(out=dst, in_=src)
             else:
-                nc.vector.tensor_copy(out=dst, in_=src)
+                nc.scalar.copy(out=dst, in_=src)
 
-        def mquant(g):
-            if not 0 <= g < GROUPS:
-                return
-            mc = mul.tile([P, P], U32, name="mc", tag="mc", align_bytes=64)
-            msc = mul.tile([P, P], U8, name="msc", tag="msc", align_bytes=64)
-            nc.vector.quantize_mx(out=mc[:].bitcast(FP8X4), scales=msc[:], in_=mgs[g][:])
-            mcod[g] = mc
-            mscl[g] = msc
+        def m_quant(g):
+            mc_g = mul.tile([P, K], U32, name="mc_g", tag="mc", align_bytes=64)
+            msc_g = mul.tile([P, K], U8, name="msc_g", tag="msc", align_bytes=64)
+            mc[g] = mc_g
+            msc[g] = msc_g
+            nc.vector.quantize_mx(out=mc_g[:].bitcast(FP8X4), scales=msc_g[:], in_=mg[g][:])
 
-        xg2s = {}
+        xg2 = {}
         xc2 = {}
         xsc2 = {}
 
-        def xt(n, b, eng):
+        def x_transpose(n, b):
             h, jp = divmod(b, 2)
             if b == 0:
-                xg2 = xgp.tile([P, 4 * PIX], BF16, name="xg2", tag="xg2", bufs=1, align_bytes=64)
-                xg2s[n] = xg2
-            xw = xs[n][:].bitcast(F32).rearrange("p (j a w) -> p j a w", j=4, a=4, w=P)
-            xg2w = xg2s[n][:].bitcast(F32).rearrange("p (h jp c) -> p h jp c", h=2, jp=2)
-            xtb = pzt.tile([P, GW], F32, name="xtb", tag="zt")
+                xg2_n = xgp.tile([P, 4 * PIX], BF16, name="xg2_n", tag="xg2", bufs=1, align_bytes=64)
+                xg2[n] = xg2_n
+            words = xs[n][:].bitcast(F32).rearrange("p (j a w) -> p j a w", j=4, a=4, w=P)
+            xb = pmm.tile([P, CH], F32, name="xb", tag="mm")
             for jl in range(2):
-                for u in range(2):
-                    q = jl * 2 + u
-                    nc.tensor.transpose(xtb[:, q * P : (q + 1) * P], xw[:, jp * 2 + jl, h * 2 + u], ident[:])
-            dst = xg2w[:, h, jp].rearrange("p (jl q u) -> p jl q u", jl=2, u=2)
-            src = xtb[:].rearrange("p (jl u q) -> p jl q u", jl=2, u=2)
-            if eng == 0:
-                nc.scalar.copy(out=dst, in_=src)
-            else:
-                nc.vector.tensor_copy(out=dst, in_=src)
+                for a in range(2):
+                    q = 2 * jl + a
+                    nc.tensor.transpose(xb[:, q * P : (q + 1) * P], words[:, 2 * jp + jl, 2 * h + a], ident[:])
+            dst = xg2[n][:].bitcast(F32).rearrange("p (h jp c) -> p h jp c", h=2, jp=2)[:, h, jp]
+            nc.scalar.copy(
+                out=dst.rearrange("p (jl q a) -> p jl q a", jl=2, a=2),
+                in_=xb[:].rearrange("p (jl a q) -> p jl q a", jl=2, a=2),
+            )
 
-        def x2quant(n, h):
+        def x2_quant(n, h):
             if h == 0:
                 c2 = xq2.tile([P, PIX], U32, name="c2", tag="c2", align_bytes=64)
                 s2 = xq2.tile([P, PIX], U8, name="s2", tag="s2", align_bytes=64)
                 xc2[n] = c2
                 xsc2[n] = s2
+            cols = slice(h * CH, (h + 1) * CH)
             nc.vector.quantize_mx(
-                out=xc2[n][:, h * 512 : (h + 1) * 512].bitcast(FP8X4),
-                scales=xsc2[n][:, h * 512 : (h + 1) * 512],
-                in_=xg2s[n][:, h * 2048 : (h + 1) * 2048],
+                out=xc2[n][:, cols].bitcast(FP8X4), scales=xsc2[n][:, cols], in_=xg2[n][:, 4 * h * CH : 4 * (h + 1) * CH]
             )
 
-        smt = {}
-        vts = {}
-        fst = {}
+        by_vector = {}
+        by_gpsimd = {}
+        vbank = {}
+        vp = {}
 
-        def msum(i):
-            ms = pzt.tile([P, 2], F32, name="ms", tag="zt")
-            for hh in range(2):
-                g = 2 * i + hh
-                for t in range(4):
-                    nc.tensor.matmul(
-                        out=ms[:],
-                        lhsT=acc[g][:, t * P : (t + 1) * P],
-                        rhs=ones[:, 0:2],
-                        start=(hh == 0 and t == 0),
-                        stop=(hh == 1 and t == 3),
-                    )
-            sm = fin.tile([P, 16], F32, name="sm", tag="sm")
-            smt[i] = sm
-            nc.vector.tensor_scalar(out=sm[:, 0:1], in0=ms[:, 0:1], scalar1=-1.0, scalar2=None, op0=ALU.mult)
-
-        def final_mm(i):
-            v = pzt.tile([P, CH], F32, name="v", tag="zt")
-            vts[i] = v
-            for hh in range(2):
-                g = 2 * i + hh
-                nc.tensor.matmul_mx(
-                    out=v[:],
-                    lhsT=mcod[g][:].bitcast(FP8X4),
-                    lhsT_scale=mscl[g][:],
-                    rhs=xc2[i][:, hh * 512 : (hh + 1) * 512].bitcast(FP8X4),
-                    rhs_scale=xsc2[i][:, hh * 512 : (hh + 1) * 512],
-                    start=(hh == 0),
-                    stop=(hh == 1),
+        def sum_mult(g):
+            n, h = divmod(g, 2)
+            ms = pmm.tile([P, 2], F32, name="ms", tag="mm")
+            for t in range(BLKS):
+                nc.tensor.matmul(
+                    out=ms[:],
+                    lhsT=mult[g][:, t * P : (t + 1) * P],
+                    rhs=ones[:, 0:2],
+                    start=(t == 0),
+                    stop=(t == BLKS - 1),
+                )
+            if h == 0:
+                vec = fin.tile([P, 16], F32, name="vec", tag="vec")
+                by_vector[n] = vec
+                nc.vector.tensor_scalar(out=vec[:, 0:1], in0=ms[:, 0:1], scalar1=-1.0, scalar2=None, op0=ALU.mult)
+            else:
+                vec = by_vector[n]
+                nc.vector.scalar_tensor_tensor(
+                    out=vec[:, 1:2], in0=ms[:, 0:1], scalar=-1.0, in1=vec[:, 0:1], op0=ALU.mult, op1=ALU.add
                 )
 
-        def final_a(i):
-            v = vts[i]
-            sm = smt[i]
-            ssq = fin.tile([P, 1], F32, name="ssq", tag="ssq")
-            vp = fin.tile([P, CH], F32, name="vp", tag="vp")
+        def second_mm(n):
+            vb = pmm.tile([P, CH], F32, name="vb", tag="mm")
+            vbank[n] = vb
+            for h in range(2):
+                g = 2 * n + h
+                cols = slice(h * CH, (h + 1) * CH)
+                nc.tensor.matmul_mx(
+                    out=vb[:],
+                    lhsT=mc[g][:].bitcast(FP8X4),
+                    lhsT_scale=msc[g][:],
+                    rhs=xc2[n][:, cols].bitcast(FP8X4),
+                    rhs_scale=xsc2[n][:, cols],
+                    start=(h == 0),
+                    stop=(h == 1),
+                )
+
+        def row_norm(n):
+            ssq = fin.tile([P, 16], F32, name="ssq", tag="ssq")
+            gps = fin.tile([P, 16], F32, name="gps", tag="gps")
+            by_gpsimd[n] = gps
+            vp_n = fin.tile([P, CH], F32, name="vp_n", tag="vp")
+            vp[n] = vp_n
             nc.vector.scalar_tensor_tensor(
-                out=vp[:].rearrange("p (j q) -> p j q", j=4),
+                out=vp_n[:].rearrange("p (j q) -> p j q", j=4),
                 in0=cen[:, 0:CH].rearrange("p (q j) -> p j q", j=4),
-                scalar=sm[:, 0:1],
-                in1=v[:].rearrange("p (j q) -> p j q", j=4),
+                scalar=by_vector[n][:, 1:2],
+                in1=vbank[n][:].rearrange("p (j q) -> p j q", j=4),
                 op0=ALU.mult,
                 op1=ALU.add,
             )
-            nc.scalar.activation(out=junk_w[:], in_=vp[:], func=ACTF.Square, accum_out=ssq[:, 0:1])
-            pg = fin.tile([P, 16], F32, name="pg", tag="pg")
+            nc.scalar.activation(out=junk[:], in_=vp_n[:], func=ACTF.Square, accum_out=ssq[:, 0:1])
             nc.gpsimd.tensor_scalar(
-                out=qcol[:, 0:1], in0=ssq[:, 0:1], scalar1=1.0 / EPS2, scalar2=1.0, op0=ALU.mult, op1=ALU.min
+                out=share[:, 0:1], in0=ssq[:, 0:1], scalar1=1.0 / EPS2, scalar2=1.0, op0=ALU.mult, op1=ALU.min
             )
-            nc.gpsimd.tensor_scalar(out=pg[:, 0:1], in0=ssq[:, 0:1], scalar1=EPS2, scalar2=None, op0=ALU.max)
-            nc.gpsimd.tensor_tensor(out=pg[:, 1:2], in0=pg[:, 0:1], in1=expo[:, 8:9], op=ALU.pow)
-            fst[i] = (sm, pg, vp)
+            nc.gpsimd.tensor_scalar(out=gps[:, 0:1], in0=ssq[:, 0:1], scalar1=EPS2, scalar2=None, op0=ALU.max)
+            nc.gpsimd.tensor_tensor(out=gps[:, 1:2], in0=gps[:, 0:1], in1=minus_half[:], op=ALU.pow)
 
-        def final_b(i):
-            sm, pg, vp = fst[i]
-            tot = pzt.tile([P, 2], F32, name="tot", tag="zt")
-            nc.tensor.matmul(out=tot[:], lhsT=ones[:], rhs=qcol[:], start=True, stop=True)
-            nc.vector.tensor_scalar(out=sm[:, 1:2], in0=tot[:, 0:1], scalar1=EPS2, scalar2=None, op0=ALU.max)
-            nc.gpsimd.tensor_tensor(out=pg[:, 3:4], in0=sm[:, 1:2], in1=expo[:, 8:9], op=ALU.pow)
+        def whole_norm(n):
+            vec = by_vector[n]
+            tot = pmm.tile([P, 2], F32, name="tot", tag="mm")
+            nc.tensor.matmul(out=tot[:], lhsT=ones[:], rhs=share[:], start=True, stop=True)
+            nc.vector.tensor_scalar(out=vec[:, 2:3], in0=tot[:, 0:1], scalar1=EPS2, scalar2=None, op0=ALU.max)
+            nc.gpsimd.tensor_tensor(out=by_gpsimd[n][:, 2:3], in0=vec[:, 2:3], in1=minus_half[:], op=ALU.pow)
 
-        def final_c(i):
-            sm, pg, vp = fst[i]
+        def store(n):
+            gps = by_gpsimd[n]
             o = fin.tile([P, CH], F32, name="o", tag="o")
             nc.vector.tensor_scalar(
                 out=o[:].rearrange("p (q j) -> p q j", j=4),
-                in0=vp[:].rearrange("p (j q) -> p q j", j=4),
-                scalar1=pg[:, 1:2],
-                scalar2=pg[:, 3:4],
+                in0=vp[n][:].rearrange("p (j q) -> p q j", j=4),
+                scalar1=gps[:, 1:2],
+                scalar2=gps[:, 2:3],
                 op0=ALU.mult,
                 op1=ALU.mult,
             )
-            nc.sync.dma_start(out=out[i].rearrange("(k c) -> k c", c=CH), in_=o[:])
+            nc.sync.dma_start(out=out[n].rearrange("(k c) -> k c", c=CH), in_=o[:])
 
-        XT = {}
-        for n, steps in enumerate(XTS):
-            for b in range(4):
-                XT[steps[b]] = (n, b)
+        for s in range(S5):
+            w_transpose(s)
+        w_scale(0)
+        w_scale(1)
+        w_quant(0)
+        make_bias(0, 2)
+        for q in range(4):
+            regroup(0, q)
+        w_quant(1)
+        w_scale(2)
+        x1_quant(0)
+        make_bias(2, S5)
+        first_mm(0)
+        first_mm(1)
+        w_scale(3)
+        w_quant(2)
+        add_bias(0)
+        w_scale(4)
+        w_quant(3)
+        add_bias(1)
+        w_quant(4)
+        z_transpose(0)
+        first_mm(2)
+        add_bias(2)
+        for q in range(3):
+            regroup(1, q)
+        cluster_max(0)
+        z_transpose(1)
+        first_mm(3)
+        add_bias(3)
+        regroup(1, 3)
+        exp1(0)
+        cluster_max(1)
+        x1_quant(1)
+        first_mm(4)
+        add_bias(4)
+        centroid_max(0, 0)
 
-        for u in range(-11, UNITS + LA + 18):
-            if u == -6:
-                head()
-            if u >= -5:
-                w = u + KE
-                if u + KL >= 5:
-                    za(u + KL)
-                if 2 * (KE > 0) <= w + 1 < 5:
-                    za(w + 1)
-                if u + 1 >= 5:
-                    kmax(u + 1)
-                if 2 * (KE > 0) <= w + 1 < 5:
-                    kmax(w + 1)
-                amul(u - LA)
-                if u >= 5:
-                    e1(u)
-                if 2 * (KE > 0) <= w < 5 and w >= 0:
-                    e1(w)
-                qmul(u - LQ)
-                if ZC == 1 and u + 5 >= 5:
-                    zcp(u + 5)
-                if u + 6 >= 5:
-                    zmx(u + 6)
-                    if ZC == 0:
-                        zcp(u + 6)
-                    zmaxp(u + 6 - ZM, 5)
-                prod(u - LA - PD)
-                if u % 5 == 3:
-                    smax((u + 2) // 5, 0)
-                if u % 5 == 4:
-                    smax((u + 1) // 5, 1)
-                if u % 5 == 0:
-                    smax(u // 5, 2)
-            if 2 <= (u + 11) // 5 < GROUPS:
-                if (u + 11) % 5 < 4:
-                    regroup((u + 11) // 5, (u + 11) % 5)
-                else:
-                    xquant((u + 11) // 5)
-            if SP == 0 and u % 5 == 0:
-                smax(u // 5, 3)
-            if SP == 1 and u % 5 == 4:
-                smax((u + 1) // 5, 3)
-            yadd(u - LE + 2)
-            e2(u - LE)
-            dpe(u - LE + 1)
-            if (u - LE) % 5 == 0:
-                cpart((u - LE - 5) // 5, (0, 1))
-            if (u - LE) % 5 == 1:
-                cpart((u - LE - 6) // 5, (2, 3))
+        def stage(fn, v):
+            if 0 <= v < TILES:
+                fn(v)
+
+        for step in range(TILES + PROD_LAG + 21):
+            if step > 0:
+                stage(z_transpose, step + 1)
+            stage(soft, step - SOFT_LAG)
+            if step > 0:
+                stage(cluster_max, step + 1)
+                stage(exp1, step)
+            stage(times_p, step - UP_LAG)
+            stage(first_mm, step + MM_LEAD)
+            stage(add_bias, step + MM_LEAD)
+            stage(factor, step - PROD_LAG)
             for g in range(GROUPS):
-                if u == 5 * g + CC:
-                    crecip(g)
-                if u == 5 * g + LA - CL:
-                    cback(g)
-                p0 = 5 * g + LA + PD + 5
-                if u == p0:
-                    cast(g)
-                if u == p0 + 1:
-                    mquant(g)
-            if u % 5 == 1:
-                rrecip((u - 6) // 5)
-            if u in XT:
-                n, b = XT[u]
-                xt(n, b, XTE.get(n, 0))
-            if u - XQ in XT:
-                n, b = XT[u - XQ]
-                if b == 1:
-                    x2quant(n, 0)
-                if b == 3:
-                    x2quant(n, 1)
-            for i in range(IMAGES):
-                p0 = 10 * i + 5 + LA + PD + 5
-                if u == p0:
-                    msum(i)
-                if u == p0 + 2:
-                    final_mm(i)
-                if u == p0 + 3:
-                    final_a(i)
-                if u == p0 + FB:
-                    final_b(i)
-                if u == p0 + FC:
-                    final_c(i)
+                at = step - g * S5
+                if at in (-1, 0, 1):
+                    centroid_max(g, at + 1)
+            for g in range(2, GROUPS):
+                at = step - g * S5
+                if -10 <= at < -6:
+                    regroup(g, at + 10)
+                if at == -6:
+                    x1_quant(g)
+            for g in range(GROUPS):
+                at = step - g * S5
+                if at == 1:
+                    centroid_max(g, 3)
+            stage(diff, step - EXP2_LAG)
+            stage(exp2, step - EXP2_LAG)
+            for g in range(GROUPS):
+                at = step - g * S5
+                if at == EXP2_LAG + S5:
+                    sum_c(g, (0, 1))
+                if at == EXP2_LAG + S5 + 1:
+                    sum_c(g, (2, 3))
+            for g in range(GROUPS):
+                at = step - g * S5
+                if at == EXP2_LAG + S5 + 3:
+                    invert_c(g)
+                if at == SOFT_LAG - 1:
+                    c_transpose(g)
+                if at == S5 + 3:
+                    invert_r(g)
+                if at == PROD_LAG + S5 + 1:
+                    m_cast(g)
+                    sum_mult(g)
+                if at == PROD_LAG + S5 + 2:
+                    m_quant(g)
+            for n in range(IMAGES):
+                at = step - 2 * n * S5
+                for b in range(4):
+                    if at == (2, 3, 7, 8)[b]:
+                        x_transpose(n, b)
+                if at == 4:
+                    x2_quant(n, 0)
+                if at == 9:
+                    x2_quant(n, 1)
+                done = PROD_LAG + 2 * S5
+                if at == done + 2:
+                    second_mm(n)
+                if at == done + 3:
+                    row_norm(n)
+                if at == done + 9:
+                    whole_norm(n)
+                if at == done + 12:
+                    store(n)

from contextlib import ExitStack

import concourse.mybir as mybir
from concourse.masks import make_identity

F32 = mybir.dt.float32
BF16 = mybir.dt.bfloat16
U32 = mybir.dt.uint32
U8 = mybir.dt.uint8
FP8X4 = mybir.dt.float8_e4m3fn_x4
ALU = mybir.AluOpType
ACTF = mybir.ActivationFunctionType
AX = mybir.AxisListType

P = 128
IMAGES = 4
CH = 512
PIX = 1024
K = 128
S5 = 5
M = K * S5
HALF = PIX // 2
BLKS = HALF // P
GROUPS = 2 * IMAGES
TILES = GROUPS * S5

ALPHA = 100.0
EPS2 = 1e-24

FLOPS = 2 * IMAGES * PIX * M * CH + 2 * IMAGES * K * CH * PIX

MM_LEAD = 5
EXP2_LAG = 4
UP_LAG = 5
SOFT_LAG = 15
PROD_LAG = 17

CLOCK_FROM = 4


def tile_sralnet_pa_kernel(tc, x, centroids, out):
    nc = tc.nc
    with ExitStack() as ctx:
        const = ctx.enter_context(tc.tile_pool(name="const", bufs=1))
        xin = ctx.enter_context(tc.tile_pool(name="xin", bufs=IMAGES))
        xgp = ctx.enter_context(tc.tile_pool(name="xgp", bufs=2))
        xq1 = ctx.enter_context(tc.tile_pool(name="xq1", bufs=2))
        xq2 = ctx.enter_context(tc.tile_pool(name="xq2", bufs=3))
        zp = ctx.enter_context(tc.tile_pool(name="zp", bufs=3))
        pp = ctx.enter_context(tc.tile_pool(name="pp", bufs=EXP2_LAG + 7))
        up = ctx.enter_context(tc.tile_pool(name="up", bufs=PROD_LAG + 1))
        tmp = ctx.enter_context(tc.tile_pool(name="tmp", bufs=1))
        grp = ctx.enter_context(tc.tile_pool(name="grp", bufs=3))
        mul = ctx.enter_context(tc.tile_pool(name="mul", bufs=3))
        fin = ctx.enter_context(tc.tile_pool(name="fin", bufs=2))
        pza = ctx.enter_context(tc.psum_pool(name="pza", bufs=2))
        pdf = ctx.enter_context(tc.psum_pool(name="pdf", bufs=2))
        pmm = ctx.enter_context(tc.psum_pool(name="pmm", bufs=2))
        psc = ctx.enter_context(tc.psum_pool(name="psc", bufs=1))
        prc = ctx.enter_context(tc.psum_pool(name="prc", bufs=1))
        ctx.enter_context(tc.manual_schedule())

        cen = const.tile([P, S5 * CH], BF16, name="cen")
        nc.sync.dma_start(out=cen[:], in_=centroids.rearrange("k s c -> k (s c)"))
        xs = []
        for n in range(IMAGES):
            x_n = xin.tile([P, 4 * PIX], BF16, name="x_n", tag="x")
            xs.append(x_n)
            if n == 0:
                sb = x_n[:].rearrange("p (j c) -> p j c", j=4)
                hbm = x[n].rearrange("(q j) h w -> q j (h w)", j=4)
                nc.sync.dma_start(out=sb[:, :, 0:HALF], in_=hbm[:, :, 0:HALF])
                nc.sync.dma_start(out=sb[:, :, HALF:PIX], in_=hbm[:, :, HALF:PIX])
            else:
                nc.sync.dma_start(out=x_n[:], in_=x[n].rearrange("(q j) h w -> q (j h w)", j=4))

        ident = const.tile([P, P], F32, name="ident")
        make_identity(nc, ident[:])
        ones = const.tile([P, P], F32, name="ones")
        nc.vector.memset(ones[:], 1.0)
        plus_half = const.tile([P, S5], F32, name="plus_half")
        nc.vector.memset(plus_half[:], 0.5)
        minus_half = const.tile([P, 1], F32, name="minus_half")
        nc.vector.memset(minus_half[:], -0.5)
        share = const.tile([P, 2], F32, name="share")
        nc.vector.memset(share[:], 0.0)
        junk = const.tile([P, CH], F32, name="junk")
        nc.scalar.activation(out=junk[:, 0:1], in_=plus_half[:, 0:1], func=ACTF.Exp)

        wg = const.tile([P, 4 * M], BF16, name="wg", align_bytes=64)
        wc = const.tile([P, M], U32, name="wc", align_bytes=64)
        wsc = const.tile([P, M], U8, name="wsc", align_bytes=64)
        n2 = const.tile([P, S5], F32, name="n2")
        norm = const.tile([P, S5], F32, name="norm")
        bias = const.tile([P, S5], F32, name="bias")
        wts = {}

        def w_transpose(s):
            pool, tag = ((psc, "c"), (prc, "rc"), (pdf, "df"), (pdf, "df"), (pza, "za"))[s]
            wt = pool.tile([P, 2 * P], F32, name="wt", tag=tag)
            wts[s] = wt
            words = cen[:].bitcast(F32).rearrange("p (s q u) -> p s u q", s=S5, u=2)
            for u in range(2):
                nc.tensor.transpose(wt[:, u * P : (u + 1) * P], words[:, s, u], ident[:])

        def w_scale(s):
            nc.vector.tensor_scalar(
                out=wg[:, s * 4 * K : (s + 1) * 4 * K].rearrange("p (k u e) -> p k u e", u=2, e=2),
                in0=wts[s][:].bitcast(BF16).rearrange("p (u k e) -> p k u e", u=2, e=2),
                scalar1=2 * ALPHA,
                scalar2=None,
                op0=ALU.mult,
            )

        def w_quant(s):
            nc.vector.quantize_mx(
                out=wc[:, s * K : (s + 1) * K].bitcast(FP8X4),
                scales=wsc[:, s * K : (s + 1) * K],
                in_=wg[:, s * 4 * K : (s + 1) * 4 * K],
            )

        def make_bias(lo, hi):
            for s in range(lo, hi):
                nc.scalar.activation(
                    out=junk[:], in_=cen[:, s * CH : (s + 1) * CH], func=ACTF.Square, accum_out=n2[:, s : s + 1]
                )
            nc.gpsimd.tensor_tensor(out=norm[:, lo:hi], in0=n2[:, lo:hi], in1=plus_half[:, lo:hi], op=ALU.pow)
            nc.gpsimd.tensor_scalar(out=bias[:, lo:hi], in0=norm[:, lo:hi], scalar1=-ALPHA, scalar2=None, op0=ALU.mult)

        xg1 = {}
        xc1 = {}
        xsc1 = {}

        def regroup(g, q):
            n, h = divmod(g, 2)
            a, e = divmod(q, 2)
            if q == 0:
                xg1_g = xgp.tile([P, 4 * HALF], BF16, name="xg1_g", tag="xg1", align_bytes=64)
                xg1[g] = xg1_g
            src = xs[n][:].rearrange("p (j a r e) -> p a e r j", j=4, a=4, r=P, e=2)[:, 2 * h + a, e]
            dst = xg1[g][:].rearrange("p (a e r j) -> p a e r j", a=2, e=2, r=P, j=4)[:, a, e]
            if g > 1 and q == 0:
                nc.gpsimd.tensor_scalar(out=dst, in0=src, scalar1=1.0, scalar2=0.0, op0=ALU.mult, op1=ALU.add)
            elif (g > 1 and q == 3) or (g == 0 and q == 0):
                nc.scalar.copy(out=dst, in_=src)
            else:
                nc.vector.tensor_copy(out=dst, in_=src)

        def x1_quant(g):
            n, h = divmod(g, 2)
            if h == 0:
                c1 = xq1.tile([P, PIX], U32, name="c1", tag="c1", align_bytes=64)
                s1 = xq1.tile([P, PIX], U8, name="s1", tag="s1", align_bytes=64)
                xc1[n] = c1
                xsc1[n] = s1
            cols = slice(h * HALF, (h + 1) * HALF)
            nc.vector.quantize_mx(out=xc1[n][:, cols].bitcast(FP8X4), scales=xsc1[n][:, cols], in_=xg1[g][:])

        zbank = {}
        z = {}

        def first_mm(v):
            g, s = divmod(v, S5)
            n, h = divmod(g, 2)
            if s == 0:
                z_g = zp.tile([P, S5 * HALF], F32, name="z_g", tag="z")
                z[g] = z_g
            pool, tag = (pdf, "df") if v in (1, 3) else (pmm, "mm")
            zb = pool.tile([P, HALF], F32, name="zb", tag=tag)
            zbank[v] = zb
            cols = slice(h * HALF, (h + 1) * HALF)
            nc.tensor.matmul_mx(
                out=zb[:],
                lhsT=wc[:, s * K : (s + 1) * K].bitcast(FP8X4),
                lhsT_scale=wsc[:, s * K : (s + 1) * K],
                rhs=xc1[n][:, cols].bitcast(FP8X4),
                rhs_scale=xsc1[n][:, cols],
                start=True,
                stop=True,
            )

        def add_bias(v):
            g, s = divmod(v, S5)
            nc.scalar.activation(
                out=z[g][:, s * HALF : (s + 1) * HALF],
                in_=zbank.pop(v)[:],
                func=ACTF.Identity,
                bias=bias[:, s : s + 1],
                scale=1.0,
            )

        zmax = {}
        neg_max = {}

        def centroid_max(g, part):
            zg = z[g]
            if part == 0:
                zm = tmp.tile([P, 2 * HALF], F32, name="zm", tag="zm")
                zmax[g] = zm
                nc.vector.tensor_tensor(out=zm[:], in0=zg[:, 0 : 2 * HALF], in1=zg[:, 2 * HALF : 4 * HALF], op=ALU.max)
                return
            lo = zmax[g][:, 0:HALF]
            hi = zmax[g][:, HALF : 2 * HALF]
            if part == 1:
                nc.vector.tensor_tensor(out=lo, in0=lo, in1=hi, op=ALU.max)
            elif part == 2:
                nc.vector.tensor_tensor(out=hi, in0=lo, in1=zg[:, 4 * HALF : 5 * HALF], op=ALU.max)
            else:
                nm = grp.tile([P, HALF], F32, name="nm", tag="nm")
                neg_max[g] = nm
                nc.vector.tensor_scalar(out=nm[:], in0=hi, scalar1=-1.0, scalar2=None, op0=ALU.mult)

        zab = {}
        neg_kmax = {}
        rsum = {}
        rinv = {}
        u = {}

        def z_transpose(v):
            g, s = divmod(v, S5)
            if s == 0:
                nk = grp.tile([P, S5 * BLKS], F32, name="nk", tag="nk")
                rs = grp.tile([P, S5 * BLKS], F32, name="rs", tag="rs")
                neg_kmax[g] = nk
                rsum[g] = rs
            za = pza.tile([P, HALF], F32, name="za", tag="za")
            zab[v] = za
            for t in range(BLKS):
                nc.tensor.matmul(
                    out=za[:, t * P : (t + 1) * P],
                    lhsT=z[g][:, s * HALF + t * P : s * HALF + (t + 1) * P],
                    rhs=ident[:],
                    is_transpose=t < BLKS - 1 or v < CLOCK_FROM,
                    start=True,
                    stop=True,
                )

        def cluster_max(v):
            g, s = divmod(v, S5)
            nc.vector.tensor_reduce(
                out=neg_kmax[g][:, s * BLKS : (s + 1) * BLKS],
                in_=zab[v][:].rearrange("p (t k) -> p t k", t=BLKS),
                axis=AX.X,
                op=ALU.max,
                negate=True,
            )

        def exp1(v):
            g, s = divmod(v, S5)
            ub = up.tile([P, HALF], F32, name="ub", tag="u")
            u[v] = ub
            za = zab.pop(v)
            for t in range(BLKS):
                c = s * BLKS + t
                nc.scalar.activation(
                    out=ub[:, t * P : (t + 1) * P],
                    in_=za[:, t * P : (t + 1) * P],
                    func=ACTF.Exp,
                    bias=neg_kmax[g][:, c : c + 1],
                    scale=1.0,
                    accum_out=rsum[g][:, c : c + 1],
                )

        def invert_r(g):
            ri = grp.tile([P, S5 * BLKS], F32, name="ri", tag="ri")
            rinv[g] = ri
            nc.vector.reciprocal(out=ri[:], in_=rsum[g][:])

        dbank = {}
        p = {}
        csum = {}
        cinv = {}
        cinv_t = {}

        def diff(v):
            g, s = divmod(v, S5)
            db = pdf.tile([P, HALF], F32, name="db", tag="df")
            dbank[v] = db
            for t in range(BLKS):
                nc.tensor.matmul(
                    out=db[:, t * P : (t + 1) * P],
                    lhsT=z[g][:, s * HALF + t * P : s * HALF + (t + 1) * P],
                    rhs=ident[:],
                    is_transpose=t > 0 or v < CLOCK_FROM,
                    start=True,
                    stop=False,
                )
                nc.tensor.matmul(
                    out=db[:, t * P : (t + 1) * P],
                    lhsT=neg_max[g][:, t * P : (t + 1) * P],
                    rhs=ident[:],
                    is_transpose=True,
                    start=False,
                    stop=True,
                )

        def exp2(v):
            pb = pp.tile([P, HALF], F32, name="pb", tag="p")
            p[v] = pb
            nc.scalar.activation(out=pb[:], in_=dbank.pop(v)[:], func=ACTF.Exp)

        def sum_c(g, blocks):
            if blocks[0] == 0:
                cs = psc.tile([P, HALF], F32, name="cs", tag="c")
                csum[g] = cs
            for t in blocks:
                for s in range(S5):
                    nc.tensor.matmul(
                        out=csum[g][:, t * P : (t + 1) * P],
                        lhsT=p[g * S5 + s][:, t * P : (t + 1) * P],
                        rhs=ident[:],
                        is_transpose=True,
                        start=(s == 0),
                        stop=(s == S5 - 1),
                    )

        def invert_c(g):
            ci = grp.tile([P, HALF], F32, name="ci", tag="ci")
            cinv[g] = ci
            nc.vector.reciprocal(out=ci[:], in_=csum[g][:])

        def c_transpose(g):
            ct = prc.tile([P, HALF], F32, name="ct", tag="rc")
            cinv_t[g] = ct
            for t in range(BLKS):
                nc.tensor.transpose(ct[:, t * P : (t + 1) * P], cinv[g][:, t * P : (t + 1) * P], ident[:])

        mult = {}
        mg = {}
        mc = {}
        msc = {}

        def times_p(v):
            nc.gpsimd.tensor_tensor(out=u[v][:], in0=u[v][:], in1=p[v][:], op=ALU.mult)

        def soft(v):
            g, s = divmod(v, S5)
            for t in range(BLKS):
                c = s * BLKS + t
                nc.vector.scalar_tensor_tensor(
                    out=u[v][:, t * P : (t + 1) * P],
                    in0=u[v][:, t * P : (t + 1) * P],
                    scalar=rinv[g][:, c : c + 1],
                    in1=cinv_t[g][:, t * P : (t + 1) * P],
                    op0=ALU.mult,
                    op1=ALU.mult,
                )

        def factor(v):
            g, s = divmod(v, S5)
            if s == 0:
                m_g = mul.tile([P, HALF], F32, name="m_g", tag="m")
                mult[g] = m_g
                nc.scalar.activation(out=m_g[:], in_=u[v][:], func=ACTF.Identity, bias=1.0, scale=1.0)
            else:
                nc.vector.scalar_tensor_tensor(
                    out=mult[g][:], in0=u[v][:], scalar=1.0, in1=mult[g][:], op0=ALU.add, op1=ALU.mult
                )

        def m_cast(g):
            mg_g = mul.tile([P, HALF], BF16, name="mg_g", tag="mg", align_bytes=64)
            mg[g] = mg_g
            dst = mg_g[:].rearrange("p (k t) -> p k t", t=BLKS)
            src = mult[g][:].rearrange("p (t k) -> p k t", t=BLKS)
            if g == GROUPS - 1:
                nc.vector.tensor_copy(out=dst, in_=src)
            else:
                nc.scalar.copy(out=dst, in_=src)

        def m_quant(g):
            mc_g = mul.tile([P, K], U32, name="mc_g", tag="mc", align_bytes=64)
            msc_g = mul.tile([P, K], U8, name="msc_g", tag="msc", align_bytes=64)
            mc[g] = mc_g
            msc[g] = msc_g
            nc.vector.quantize_mx(out=mc_g[:].bitcast(FP8X4), scales=msc_g[:], in_=mg[g][:])

        xg2 = {}
        xc2 = {}
        xsc2 = {}

        def x_transpose(n, b):
            h, jp = divmod(b, 2)
            if b == 0:
                xg2_n = xgp.tile([P, 4 * PIX], BF16, name="xg2_n", tag="xg2", bufs=1, align_bytes=64)
                xg2[n] = xg2_n
            words = xs[n][:].bitcast(F32).rearrange("p (j a w) -> p j a w", j=4, a=4, w=P)
            xb = pmm.tile([P, CH], F32, name="xb", tag="mm")
            for jl in range(2):
                for a in range(2):
                    q = 2 * jl + a
                    nc.tensor.transpose(xb[:, q * P : (q + 1) * P], words[:, 2 * jp + jl, 2 * h + a], ident[:])
            dst = xg2[n][:].bitcast(F32).rearrange("p (h jp c) -> p h jp c", h=2, jp=2)[:, h, jp]
            nc.scalar.copy(
                out=dst.rearrange("p (jl q a) -> p jl q a", jl=2, a=2),
                in_=xb[:].rearrange("p (jl a q) -> p jl q a", jl=2, a=2),
            )

        def x2_quant(n, h):
            if h == 0:
                c2 = xq2.tile([P, PIX], U32, name="c2", tag="c2", align_bytes=64)
                s2 = xq2.tile([P, PIX], U8, name="s2", tag="s2", align_bytes=64)
                xc2[n] = c2
                xsc2[n] = s2
            cols = slice(h * CH, (h + 1) * CH)
            nc.vector.quantize_mx(
                out=xc2[n][:, cols].bitcast(FP8X4), scales=xsc2[n][:, cols], in_=xg2[n][:, 4 * h * CH : 4 * (h + 1) * CH]
            )

        by_vector = {}
        by_gpsimd = {}
        vbank = {}
        vp = {}

        def sum_mult(g):
            n, h = divmod(g, 2)
            ms = pmm.tile([P, 2], F32, name="ms", tag="mm")
            for t in range(BLKS):
                nc.tensor.matmul(
                    out=ms[:],
                    lhsT=mult[g][:, t * P : (t + 1) * P],
                    rhs=ones[:, 0:2],
                    start=(t == 0),
                    stop=(t == BLKS - 1),
                )
            if h == 0:
                vec = fin.tile([P, 16], F32, name="vec", tag="vec")
                by_vector[n] = vec
                nc.vector.tensor_scalar(out=vec[:, 0:1], in0=ms[:, 0:1], scalar1=-1.0, scalar2=None, op0=ALU.mult)
            else:
                vec = by_vector[n]
                nc.vector.scalar_tensor_tensor(
                    out=vec[:, 1:2], in0=ms[:, 0:1], scalar=-1.0, in1=vec[:, 0:1], op0=ALU.mult, op1=ALU.add
                )

        def second_mm(n):
            vb = pmm.tile([P, CH], F32, name="vb", tag="mm")
            vbank[n] = vb
            for h in range(2):
                g = 2 * n + h
                cols = slice(h * CH, (h + 1) * CH)
                nc.tensor.matmul_mx(
                    out=vb[:],
                    lhsT=mc[g][:].bitcast(FP8X4),
                    lhsT_scale=msc[g][:],
                    rhs=xc2[n][:, cols].bitcast(FP8X4),
                    rhs_scale=xsc2[n][:, cols],
                    start=(h == 0),
                    stop=(h == 1),
                )

        def row_norm(n):
            ssq = fin.tile([P, 16], F32, name="ssq", tag="ssq")
            gps = fin.tile([P, 16], F32, name="gps", tag="gps")
            by_gpsimd[n] = gps
            vp_n = fin.tile([P, CH], F32, name="vp_n", tag="vp")
            vp[n] = vp_n
            nc.vector.scalar_tensor_tensor(
                out=vp_n[:].rearrange("p (j q) -> p j q", j=4),
                in0=cen[:, 0:CH].rearrange("p (q j) -> p j q", j=4),
                scalar=by_vector[n][:, 1:2],
                in1=vbank[n][:].rearrange("p (j q) -> p j q", j=4),
                op0=ALU.mult,
                op1=ALU.add,
            )
            nc.scalar.activation(out=junk[:], in_=vp_n[:], func=ACTF.Square, accum_out=ssq[:, 0:1])
            nc.gpsimd.tensor_scalar(
                out=share[:, 0:1], in0=ssq[:, 0:1], scalar1=1.0 / EPS2, scalar2=1.0, op0=ALU.mult, op1=ALU.min
            )
            nc.gpsimd.tensor_scalar(out=gps[:, 0:1], in0=ssq[:, 0:1], scalar1=EPS2, scalar2=None, op0=ALU.max)
            nc.gpsimd.tensor_tensor(out=gps[:, 1:2], in0=gps[:, 0:1], in1=minus_half[:], op=ALU.pow)

        def whole_norm(n):
            vec = by_vector[n]
            tot = pmm.tile([P, 2], F32, name="tot", tag="mm")
            nc.tensor.matmul(out=tot[:], lhsT=ones[:], rhs=share[:], start=True, stop=True)
            nc.vector.tensor_scalar(out=vec[:, 2:3], in0=tot[:, 0:1], scalar1=EPS2, scalar2=None, op0=ALU.max)
            nc.gpsimd.tensor_tensor(out=by_gpsimd[n][:, 2:3], in0=vec[:, 2:3], in1=minus_half[:], op=ALU.pow)

        def store(n):
            gps = by_gpsimd[n]
            o = fin.tile([P, CH], F32, name="o", tag="o")
            nc.vector.tensor_scalar(
                out=o[:].rearrange("p (q j) -> p q j", j=4),
                in0=vp[n][:].rearrange("p (j q) -> p q j", j=4),
                scalar1=gps[:, 1:2],
                scalar2=gps[:, 2:3],
                op0=ALU.mult,
                op1=ALU.mult,
            )
            nc.sync.dma_start(out=out[n].rearrange("(k c) -> k c", c=CH), in_=o[:])

        for s in range(S5):
            w_transpose(s)
        w_scale(0)
        w_scale(1)
        w_quant(0)
        make_bias(0, 2)
        for q in range(4):
            regroup(0, q)
        w_quant(1)
        w_scale(2)
        x1_quant(0)
        make_bias(2, S5)
        first_mm(0)
        first_mm(1)
        w_scale(3)
        w_quant(2)
        add_bias(0)
        w_scale(4)
        w_quant(3)
        add_bias(1)
        w_quant(4)
        z_transpose(0)
        first_mm(2)
        add_bias(2)
        for q in range(3):
            regroup(1, q)
        cluster_max(0)
        z_transpose(1)
        first_mm(3)
        add_bias(3)
        regroup(1, 3)
        exp1(0)
        cluster_max(1)
        x1_quant(1)
        first_mm(4)
        add_bias(4)
        centroid_max(0, 0)

        def stage(fn, v):
            if 0 <= v < TILES:
                fn(v)

        for step in range(TILES + PROD_LAG + 21):
            if step > 0:
                stage(z_transpose, step + 1)
            stage(soft, step - SOFT_LAG)
            if step > 0:
                stage(cluster_max, step + 1)
                stage(exp1, step)
            stage(times_p, step - UP_LAG)
            stage(first_mm, step + MM_LEAD)
            stage(add_bias, step + MM_LEAD)
            stage(factor, step - PROD_LAG)
            for g in range(GROUPS):
                at = step - g * S5
                if at in (-1, 0, 1):
                    centroid_max(g, at + 1)
            for g in range(2, GROUPS):
                at = step - g * S5
                if -10 <= at < -6:
                    regroup(g, at + 10)
                if at == -6:
                    x1_quant(g)
            for g in range(GROUPS):
                at = step - g * S5
                if at == 1:
                    centroid_max(g, 3)
            stage(diff, step - EXP2_LAG)
            stage(exp2, step - EXP2_LAG)
            for g in range(GROUPS):
                at = step - g * S5
                if at == EXP2_LAG + S5:
                    sum_c(g, (0, 1))
                if at == EXP2_LAG + S5 + 1:
                    sum_c(g, (2, 3))
            for g in range(GROUPS):
                at = step - g * S5
                if at == EXP2_LAG + S5 + 3:
                    invert_c(g)
                if at == SOFT_LAG - 1:
                    c_transpose(g)
                if at == S5 + 3:
                    invert_r(g)
                if at == PROD_LAG + S5 + 1:
                    m_cast(g)
                    sum_mult(g)
                if at == PROD_LAG + S5 + 2:
                    m_quant(g)
            for n in range(IMAGES):
                at = step - 2 * n * S5
                for b in range(4):
                    if at == (2, 3, 7, 8)[b]:
                        x_transpose(n, b)
                if at == 4:
                    x2_quant(n, 0)
                if at == 9:
                    x2_quant(n, 1)
                done = PROD_LAG + 2 * S5
                if at == done + 2:
                    second_mm(n)
                if at == done + 3:
                    row_norm(n)
                if at == done + 9:
                    whole_norm(n)
                if at == done + 12:
                    store(n)
